import numpy as np
import ml_dtypes


def mxq(x, axis, fmt="e4m3"):
    dtype, down = {"e4m3": (ml_dtypes.float8_e4m3fn, 7), "e5m2": (ml_dtypes.float8_e5m2, 14)}[fmt]
    v = np.moveaxis(np.asarray(x, np.float32).astype(ml_dtypes.bfloat16).astype(np.float64), axis, -1)
    blocks = v.reshape(v.shape[:-1] + (-1, 32))
    amax = np.abs(blocks).max(-1, keepdims=True)
    byte = np.maximum(np.where(amax > 0, np.frexp(amax)[1] - 1 + 127, 0) - down, 1)
    scale = np.exp2(byte - 127.0)
    codes = (blocks / scale).astype(np.float32).astype(dtype).astype(np.float64)
    return np.moveaxis((codes * scale).reshape(v.shape), -1, axis)


WIDE = False


def mx_kscale(k):
    if not WIDE:
        return np.ones(k)
    levels = np.array([10, -10, 5, -5, 0])
    a = np.random.permutation(np.resize(levels, k // 512 * 4)).reshape(k // 512, 4)
    idx = np.arange(k)
    return np.exp2(a[idx // 512, idx % 128 // 32])


BF16 = ml_dtypes.bfloat16


def bf(x):
    return np.asarray(x, np.float32).astype(BF16)


def f64(x):
    return np.asarray(x).astype(np.float64)


B, C, O, M, K, NR, NT = 2, 1024, 512, 4, 8, 8, 8
BN_EPS = 1e-5


def setup_inputs():
    s = mx_kscale(C)

    def p(gain):
        return bf(np.random.standard_normal((O, C)) * gain / np.sqrt(C) / s[None, :])

    return {"A": bf(np.random.standard_normal((B, C, M, K, NR, NT)) * s[None, :, None, None, None, None]),
            "P1": p(1.0), "P2": p(2.0 * np.sqrt(M)), "P3": p(2.0 * np.sqrt(NT)), "P4": p(np.sqrt(NR)),
            "a5": bf(np.random.standard_normal((B, O, M, K, NT)) * 1.2 / np.sqrt(K)),
            "gamma": bf(1.0 + 0.2 * np.random.standard_normal(O)),
            "beta": bf(0.3 * np.random.standard_normal(O))}


def mix(P, X):
    y = mxq(f64(P), 1, "e4m3") @ mxq(X.reshape(B, C, -1), 1, "e4m3")
    return y.reshape((B, O) + X.shape[2:])


def reference(A, P1, P2, P3, P4, a5, gamma, beta):
    Af = f64(A)
    A1 = mix(P1, Af)
    A2 = mix(P2, Af.mean(2))[:, :, None]
    A3 = mix(P3, Af.mean(5))[..., None]
    A4 = mix(P4, Af.mean(4))[:, :, :, :, None, :]
    A5 = f64(a5)[:, :, :, :, None, :]
    y = A1 + 0.1 * A2 + 0.1 * A3 + 0.5 * A4 + 2.0 * A5
    y = np.maximum(y, 0.0)
    ax = (0, 2, 3, 4, 5)
    mean = y.mean(axis=ax, keepdims=True)
    var = y.var(axis=ax, keepdims=True)
    g = f64(gamma)[None, :, None, None, None, None]
    bta = f64(beta)[None, :, None, None, None, None]
    return (y - mean) * (1.0 / np.sqrt(var + BN_EPS)) * g + bta

@@ -1,0 +1,372 @@
+from contextlib import ExitStack
+
+import concourse.mybir as mybir
+from concourse.masks import make_identity
+
+F32 = mybir.dt.float32
+BF16 = mybir.dt.bfloat16
+U32 = mybir.dt.uint32
+U8 = mybir.dt.uint8
+FP8X4 = mybir.dt.float8_e4m3fn_x4
+ALU = mybir.AluOpType
+ACT = mybir.ActivationFunctionType
+AXIS_X = mybir.AxisListType.X
+
+B, C, O, M, K, NR, NT = 2, 1024, 512, 4, 8, 8, 8
+BN_EPS = 1e-5
+
+P = 128
+PACK = 4
+K_PASS = P * PACK
+PASSES = C // K_PASS
+POS = M * K * NR * NT
+HALF = POS // 2
+SLAB = K * NR * NT
+SMALL = M * K * NT
+O_TILES = O // P
+BLOCKS = SLAB // P
+PER_BLOCK = P // NT
+
+FLOPS = 2 * O * C * B * (POS + SLAB + 2 * SMALL)
+
+
+def mx_product(nc, acc, w_codes, w_scales, x_codes, x_scales):
+    for g in range(PASSES):
+        nc.tensor.matmul_mx(
+            out=acc,
+            lhsT=w_codes[:, g, :].bitcast(FP8X4),
+            lhsT_scale=w_scales[:, g, :],
+            rhs=x_codes[:, g, :].bitcast(FP8X4),
+            rhs_scale=x_scales[:, g, :],
+            start=(g == 0),
+            stop=(g == PASSES - 1),
+        )
+
+
+def tile_layer_3d_dep_pa_kernel(tc, A, P1, P2, P3, P4, a5, gamma, beta, out):
+    nc = tc.nc
+    a_rows = A.rearrange("b c m k r t -> b c (m k r t)")
+    a5_rows = a5.rearrange("b o m k t -> b o (m k t)")
+    out_rows = out.rearrange("b o m k r t -> b o (m k r t)")
+    weights = (P1, P2, P3, P4)
+
+    with ExitStack() as whole:
+        keep = whole.enter_context(tc.tile_pool(name="keep", bufs=1))
+
+        a_codes = keep.tile([P, PASSES, B, POS], U32, align_bytes=64)
+        a_scales = keep.tile([P, PASSES, B, POS], U8, align_bytes=64)
+        am_codes = keep.tile([P, PASSES, B * SLAB], U32, align_bytes=64)
+        am_scales = keep.tile([P, PASSES, B * SLAB], U8, align_bytes=64)
+        at_codes = keep.tile([P, PASSES, B * SMALL], U32, align_bytes=64)
+        at_scales = keep.tile([P, PASSES, B * SMALL], U8, align_bytes=64)
+        ar_codes = keep.tile([P, PASSES, B * SMALL], U32, align_bytes=64)
+        ar_scales = keep.tile([P, PASSES, B * SMALL], U8, align_bytes=64)
+        w_codes = keep.tile([P, len(weights), PASSES, O], U32, align_bytes=64)
+        w_scales = keep.tile([P, len(weights), PASSES, O], U8, align_bytes=64)
+
+        ident_f32 = keep.tile([P, P], F32)
+        make_identity(nc, ident_f32[:])
+        ident_bf = keep.tile([P, P], BF16)
+        nc.vector.tensor_copy(out=ident_bf[:], in_=ident_f32[:])
+
+        member = keep.tile([P, 2 * PER_BLOCK], F32)
+        nc.vector.tensor_reduce(
+            out=member[:, 0:PER_BLOCK],
+            in_=ident_f32[:].rearrange("q (n t) -> q n t", t=NT),
+            axis=AXIS_X,
+            op=ALU.add,
+        )
+        nc.vector.tensor_reduce(
+            out=member[:, PER_BLOCK : 2 * PER_BLOCK].rearrange("q (k t) -> q k t", t=NT),
+            in_=ident_f32[:].rearrange("q (k r t) -> q k t r", r=NR, t=NT),
+            axis=AXIS_X,
+            op=ALU.add,
+        )
+        mean_w = keep.tile([P, 2 * PER_BLOCK], BF16)
+        nc.vector.tensor_scalar_mul(out=mean_w[:], in0=member[:], scalar1=1.0 / NT)
+
+        minus_half = keep.tile([P, 1], F32)
+        nc.gpsimd.memset(minus_half[:], -0.5)
+
+        gb_rows = keep.tile([P, P], BF16)
+        nc.vector.memset(gb_rows[:], 0.0)
+        nc.scalar.dma_start(out=gb_rows[0:O_TILES, :], in_=gamma.rearrange("(t o) -> t o", o=P))
+        nc.scalar.dma_start(
+            out=gb_rows[O_TILES : 2 * O_TILES, :], in_=beta.rearrange("(t o) -> t o", o=P)
+        )
+        gamma_beta = keep.tile([P, 2 * O_TILES], F32)
+
+        a5_sb = keep.tile([P, O_TILES, B, SMALL], BF16)
+        for b in range(B):
+            nc.scalar.dma_start(
+                out=a5_sb[:, :, b, :], in_=a5_rows[b].rearrange("(t o) x -> o t x", o=P)
+            )
+        a5_twice = keep.tile([P, O_TILES, B * SMALL], F32)
+        nc.gpsimd.tensor_scalar(
+            out=a5_twice[:].rearrange("o t x -> o (t x)"),
+            in0=a5_sb[:].rearrange("o t b x -> o (t b x)"),
+            scalar1=2.0,
+            scalar2=0.0,
+            op0=ALU.mult,
+            op1=ALU.add,
+        )
+
+        with ExitStack() as first:
+            stage = first.enter_context(tc.tile_pool(name="stage", bufs=2))
+            psum = first.enter_context(tc.psum_pool(name="psum_first", bufs=2))
+
+            gb_ps = psum.tile([P, P], BF16, bufs=1)
+            nc.tensor.transpose(out=gb_ps[:], in_=gb_rows[:], identity=ident_bf[:])
+            nc.vector.tensor_copy(out=gamma_beta[:], in_=gb_ps[:, 0 : 2 * O_TILES])
+
+            for b in range(B):
+                for g in range(PASSES):
+                    at_grp = stage.tile([P, SMALL, PACK], BF16, align_bytes=64)
+                    ar_grp = stage.tile([P, SMALL, PACK], BF16, align_bytes=64)
+                    pair_sums = []
+                    for h in range(2):
+                        cols = slice(h * HALF, (h + 1) * HALF)
+                        raw = stage.tile([P, PACK, HALF], BF16, bufs=4)
+                        nc.sync.dma_start(
+                            out=raw[:],
+                            in_=a_rows[b, g * K_PASS : (g + 1) * K_PASS, cols].rearrange(
+                                "(p j) w -> p j w", j=PACK
+                            ),
+                        )
+                        grouped = stage.tile([P, HALF, PACK], BF16, bufs=3, align_bytes=64)
+                        regroup = nc.vector.tensor_copy if h == 0 else nc.scalar.copy
+                        for mm in range(2):
+                            slab = slice(mm * SLAB, (mm + 1) * SLAB)
+                            regroup(
+                                out=grouped[:, slab, :].rearrange("p (c i) j -> p c j i", i=4),
+                                in_=raw[:, :, slab].rearrange("p j (c i) -> p c j i", i=4),
+                            )
+                        flat = grouped[:].rearrange("p w j -> p (w j)")
+                        nc.vector.quantize_mx(
+                            out=a_codes[:, g, b, cols].bitcast(FP8X4),
+                            scales=a_scales[:, g, b, cols],
+                            in_=flat,
+                        )
+                        pair_sum = stage.tile([P, SLAB * PACK], F32, bufs=3)
+                        nc.vector.tensor_tensor(
+                            out=pair_sum[:],
+                            in0=flat[:, 0 : SLAB * PACK],
+                            in1=flat[:, SLAB * PACK : 2 * SLAB * PACK],
+                            op=ALU.add,
+                        )
+                        pair_sums.append(pair_sum)
+
+                        for mm in range(2):
+                            m = 2 * h + mm
+                            mean_ps = psum.tile([P, PACK, BLOCKS, 2 * PER_BLOCK], F32)
+                            for jj in range(PACK // 2):
+                                flipped_ps = psum.tile([P, 2, BLOCKS, P], BF16, bufs=3)
+                                for j2 in range(2):
+                                    for blk in range(BLOCKS):
+                                        first_pos = mm * SLAB + blk * P
+                                        nc.tensor.transpose(
+                                            out=flipped_ps[:, j2, blk, :],
+                                            in_=raw[:, 2 * jj + j2, first_pos : first_pos + P],
+                                            identity=ident_bf[:],
+                                        )
+                                flipped = stage.tile([P, 2, BLOCKS, P], BF16, bufs=4)
+                                nc.scalar.copy(out=flipped[:], in_=flipped_ps[:])
+                                for j2 in range(2):
+                                    for blk in range(BLOCKS):
+                                        nc.tensor.matmul(
+                                            out=mean_ps[:, 2 * jj + j2, blk, :],
+                                            lhsT=flipped[:, j2, blk, :],
+                                            rhs=mean_w[:],
+                                            start=True,
+                                            stop=True,
+                                        )
+                            leave = nc.vector.tensor_copy if mm == 0 else nc.scalar.copy
+                            by_pos = mean_ps[:].rearrange("p j k n -> p k n j")
+                            mine = slice(m * K * NR, (m + 1) * K * NR)
+                            leave(
+                                out=at_grp[:, mine, :].rearrange(
+                                    "p (k n) j -> p k n j", n=PER_BLOCK
+                                ),
+                                in_=by_pos[:, :, 0:PER_BLOCK, :],
+                            )
+                            leave(
+                                out=ar_grp[:, mine, :].rearrange(
+                                    "p (k n) j -> p k n j", n=PER_BLOCK
+                                ),
+                                in_=by_pos[:, :, PER_BLOCK : 2 * PER_BLOCK, :],
+                            )
+
+                    am_grp = stage.tile([P, SLAB * PACK], BF16, align_bytes=64)
+                    nc.vector.tensor_tensor(
+                        out=am_grp[:], in0=pair_sums[0][:], in1=pair_sums[1][:], op=ALU.add
+                    )
+                    nc.vector.quantize_mx(
+                        out=am_codes[:, g, b * SLAB : (b + 1) * SLAB].bitcast(FP8X4),
+                        scales=am_scales[:, g, b * SLAB : (b + 1) * SLAB],
+                        in_=am_grp[:],
+                    )
+                    nc.vector.quantize_mx(
+                        out=at_codes[:, g, b * SMALL : (b + 1) * SMALL].bitcast(FP8X4),
+                        scales=at_scales[:, g, b * SMALL : (b + 1) * SMALL],
+                        in_=at_grp[:].rearrange("p w j -> p (w j)"),
+                    )
+                    nc.vector.quantize_mx(
+                        out=ar_codes[:, g, b * SMALL : (b + 1) * SMALL].bitcast(FP8X4),
+                        scales=ar_scales[:, g, b * SMALL : (b + 1) * SMALL],
+                        in_=ar_grp[:].rearrange("p w j -> p (w j)"),
+                    )
+
+                    which = b * PASSES + g
+                    w_raw = stage.tile([P, O_TILES * C], BF16)
+                    nc.sync.dma_start(
+                        out=w_raw[:].rearrange("o (t c) -> o t c", t=O_TILES),
+                        in_=weights[which].rearrange("(t o) c -> o t c", o=P),
+                    )
+                    w_words = w_raw[:].bitcast(F32).rearrange(
+                        "o (t g p u) -> o t g p u", t=O_TILES, g=PASSES, u=2
+                    )
+                    for wg in range(PASSES):
+                        w_grp = stage.tile([P, O * PACK], BF16, align_bytes=64)
+                        w_grp_words = w_grp[:].bitcast(F32).rearrange("p (o u) -> p o u", u=2)
+                        for tp in range(O_TILES // 2):
+                            wt_ps = psum.tile([P, 2, 2, P], F32)
+                            for t2 in range(2):
+                                for u in range(2):
+                                    nc.tensor.transpose(
+                                        out=wt_ps[:, t2, u, :],
+                                        in_=w_words[:, 2 * tp + t2, wg, :, u],
+                                        identity=ident_f32[:],
+                                    )
+                            nc.scalar.copy(
+                                out=w_grp_words[:, tp * 2 * P : (tp + 1) * 2 * P, :].rearrange(
+                                    "p (t o) u -> p t o u", t=2
+                                ),
+                                in_=wt_ps[:].rearrange("p t u o -> p t o u"),
+                            )
+                        nc.vector.quantize_mx(
+                            out=w_codes[:, which, wg, :].bitcast(FP8X4),
+                            scales=w_scales[:, which, wg, :],
+                            in_=w_grp[:],
+                        )
+
+        with ExitStack() as second:
+            work = second.enter_context(tc.tile_pool(name="work", bufs=2))
+            psum = second.enter_context(tc.psum_pool(name="psum_second", bufs=1))
+
+            for ot in range(O_TILES):
+                o_cols = slice(ot * P, (ot + 1) * P)
+
+                def mix(acc, which, x_codes, x_scales):
+                    mx_product(
+                        nc, acc, w_codes[:, which, :, o_cols], w_scales[:, which, :, o_cols],
+                        x_codes, x_scales,
+                    )
+
+                a4_ps = psum.tile([P, B * SMALL], F32)
+                mix(a4_ps[:], 3, ar_codes[:], ar_scales[:])
+                along_r = work.tile([P, B, SMALL], F32)
+                nc.vector.scalar_tensor_tensor(
+                    out=along_r[:].rearrange("o b x -> o (b x)"),
+                    in0=a4_ps[:],
+                    scalar=0.5,
+                    in1=a5_twice[:, ot, :],
+                    op0=ALU.mult,
+                    op1=ALU.add,
+                )
+                a3_ps = psum.tile([P, B * SMALL], F32)
+                mix(a3_ps[:], 2, at_codes[:], at_scales[:])
+
+                y = work.tile([P, B, POS], F32, bufs=3)
+                sums = work.tile([P, 2, B], F32)
+                for b in range(B):
+                    a2_ps = psum.tile([P, SLAB], F32, bufs=2)
+                    b_slab = slice(b * SLAB, (b + 1) * SLAB)
+                    mix(a2_ps[:], 1, am_codes[:, :, b_slab], am_scales[:, :, b_slab])
+                    for m in range(M):
+                        slab = slice(m * SLAB, (m + 1) * SLAB)
+                        a1_ps = psum.tile([P, SLAB], F32, bufs=4)
+                        mix(a1_ps[:], 0, a_codes[:, :, b, slab], a_scales[:, :, b, slab])
+                        nc.vector.tensor_tensor(
+                            out=y[:, b, slab].rearrange("o (k r t) -> o k r t", r=NR, t=NT),
+                            in0=a1_ps[:].rearrange("o (k r t) -> o k r t", r=NR, t=NT),
+                            in1=along_r[:, b, m * K * NT : (m + 1) * K * NT]
+                            .rearrange("o (k t) -> o k t", t=NT)
+                            .unsqueeze(2)
+                            .to_broadcast([P, K, NR, NT]),
+                            op=ALU.add,
+                        )
+                    nc.vector.scalar_tensor_tensor(
+                        out=y[:, b, :].rearrange("o (m x) -> o m x", m=M),
+                        in0=a2_ps[:].unsqueeze(1).to_broadcast([P, M, SLAB]),
+                        scalar=0.1 / M,
+                        in1=y[:, b, :].rearrange("o (m x) -> o m x", m=M),
+                        op0=ALU.mult,
+                        op1=ALU.add,
+                    )
+                    nc.vector.scalar_tensor_tensor(
+                        out=y[:, b, :].rearrange("o (x t) -> o x t", t=NT),
+                        in0=a3_ps[:, b * SMALL : (b + 1) * SMALL]
+                        .unsqueeze(2)
+                        .to_broadcast([P, SMALL, NT]),
+                        scalar=0.1,
+                        in1=y[:, b, :].rearrange("o (x t) -> o x t", t=NT),
+                        op0=ALU.mult,
+                        op1=ALU.add,
+                    )
+                    nc.scalar.activation(
+                        out=y[:, b, :], in_=y[:, b, :], func=ACT.Relu,
+                        accum_out=sums[:, 0, b : b + 1],
+                    )
+                    squares = work.tile([P, POS], BF16)
+                    nc.scalar.activation(
+                        out=squares[:], in_=y[:, b, :], func=ACT.Square,
+                        accum_out=sums[:, 1, b : b + 1],
+                    )
+
+                total = work.tile([P, 2], F32)
+                nc.gpsimd.tensor_tensor(
+                    out=total[:], in0=sums[:, :, 0], in1=sums[:, :, 1], op=ALU.add
+                )
+                moments = work.tile([P, 2], F32)
+                nc.gpsimd.tensor_scalar(
+                    out=moments[:], in0=total[:], scalar1=1.0 / (B * POS), scalar2=0.0,
+                    op0=ALU.mult, op1=ALU.add,
+                )
+                mean = moments[:, 0:1]
+                mean_sq = work.tile([P, 1], F32)
+                nc.gpsimd.tensor_tensor(out=mean_sq[:], in0=mean, in1=mean, op=ALU.mult)
+                var = work.tile([P, 1], F32)
+                nc.gpsimd.tensor_tensor(
+                    out=var[:], in0=moments[:, 1:2], in1=mean_sq[:], op=ALU.subtract
+                )
+                var_eps = work.tile([P, 1], F32)
+                nc.gpsimd.tensor_scalar(
+                    out=var_eps[:], in0=var[:], scalar1=0.0, scalar2=BN_EPS,
+                    op0=ALU.max, op1=ALU.add,
+                )
+                rstd = work.tile([P, 1], F32)
+                nc.gpsimd.tensor_tensor(
+                    out=rstd[:], in0=var_eps[:], in1=minus_half[:], op=ALU.pow
+                )
+                gain = work.tile([P, 1], F32)
+                nc.gpsimd.tensor_tensor(
+                    out=gain[:], in0=gamma_beta[:, ot : ot + 1], in1=rstd[:], op=ALU.mult
+                )
+                mean_gain = work.tile([P, 1], F32)
+                nc.gpsimd.tensor_tensor(out=mean_gain[:], in0=mean, in1=gain[:], op=ALU.mult)
+                shift = work.tile([P, 1], F32)
+                nc.gpsimd.tensor_tensor(
+                    out=shift[:], in0=gamma_beta[:, O_TILES + ot : O_TILES + ot + 1],
+                    in1=mean_gain[:], op=ALU.subtract,
+                )
+
+                nc.gpsimd.tensor_scalar(
+                    out=y[:, 0, :], in0=y[:, 0, :], scalar1=gain[:], scalar2=shift[:],
+                    op0=ALU.mult, op1=ALU.add,
+                )
+                nc.scalar.activation(
+                    out=y[:, 1, :], in_=y[:, 1, :], func=ACT.Identity,
+                    scale=gain[:], bias=shift[:],
+                )
+                for b in range(B):
+                    nc.sync.dma_start(out=out_rows[b, o_cols, :], in_=y[:, b, :])

@@ -26,21 +26,10 @@ SMALL = M * K * NT
 O_TILES = O // P
 BLOCKS = SLAB // P
 PER_BLOCK = P // NT
+N_W = 4
+UNITS = 2 * B
 
 FLOPS = 2 * O * C * B * (POS + SLAB + 2 * SMALL)
-
-
-def mx_product(nc, acc, w_codes, w_scales, x_codes, x_scales):
-    for g in range(PASSES):
-        nc.tensor.matmul_mx(
-            out=acc,
-            lhsT=w_codes[:, g, :].bitcast(FP8X4),
-            lhsT_scale=w_scales[:, g, :],
-            rhs=x_codes[:, g, :].bitcast(FP8X4),
-            rhs_scale=x_scales[:, g, :],
-            start=(g == 0),
-            stop=(g == PASSES - 1),
-        )
 
 
 def tile_layer_3d_dep_pa_kernel(tc, A, P1, P2, P3, P4, a5, gamma, beta, out):
@@ -52,6 +41,8 @@ def tile_layer_3d_dep_pa_kernel(tc, A, P1, P2, P3, P4, a5, gamma, beta, out):
 
     with ExitStack() as whole:
         keep = whole.enter_context(tc.tile_pool(name="keep", bufs=1))
+        work = whole.enter_context(tc.tile_pool(name="work", bufs=2))
+        psum_mix = whole.enter_context(tc.psum_pool(name="psum_mix", bufs=1))
 
         a_codes = keep.tile([P, PASSES, B, POS], U32, align_bytes=64)
         a_scales = keep.tile([P, PASSES, B, POS], U8, align_bytes=64)
@@ -61,8 +52,11 @@ def tile_layer_3d_dep_pa_kernel(tc, A, P1, P2, P3, P4, a5, gamma, beta, out):
         at_scales = keep.tile([P, PASSES, B * SMALL], U8, align_bytes=64)
         ar_codes = keep.tile([P, PASSES, B * SMALL], U32, align_bytes=64)
         ar_scales = keep.tile([P, PASSES, B * SMALL], U8, align_bytes=64)
-        w_codes = keep.tile([P, len(weights), PASSES, O], U32, align_bytes=64)
-        w_scales = keep.tile([P, len(weights), PASSES, O], U8, align_bytes=64)
+        w_codes = keep.tile([P, O_TILES, N_W * PASSES, P], U32, align_bytes=64)
+        w_scales = keep.tile([P, O_TILES, N_W * PASSES, P], U8, align_bytes=64)
+
+        y_first = keep.tile([P, O_TILES, POS], F32)
+        sums = keep.tile([P, O_TILES, 2, UNITS], F32)
 
         ident_f32 = keep.tile([P, P], F32)
         make_identity(nc, ident_f32[:])
@@ -90,115 +84,223 @@ def tile_layer_3d_dep_pa_kernel(tc, A, P1, P2, P3, P4, a5, gamma, beta, out):
 
         gb_rows = keep.tile([P, P], BF16)
         nc.vector.memset(gb_rows[:], 0.0)
-        nc.scalar.dma_start(out=gb_rows[0:O_TILES, :], in_=gamma.rearrange("(t o) -> t o", o=P))
-        nc.scalar.dma_start(
-            out=gb_rows[O_TILES : 2 * O_TILES, :], in_=beta.rearrange("(t o) -> t o", o=P)
-        )
         gamma_beta = keep.tile([P, 2 * O_TILES], F32)
-
         a5_sb = keep.tile([P, O_TILES, B, SMALL], BF16)
-        for b in range(B):
-            nc.scalar.dma_start(
-                out=a5_sb[:, :, b, :], in_=a5_rows[b].rearrange("(t o) x -> o t x", o=P)
+        a5_twice = keep.tile([P, O_TILES, B, SMALL], BF16)
+
+        def mix(acc, ot, which, x_codes, x_scales):
+            for g in range(PASSES):
+                nc.tensor.matmul_mx(
+                    out=acc,
+                    lhsT=w_codes[:, ot, which * PASSES + g, :].bitcast(FP8X4),
+                    lhsT_scale=w_scales[:, ot, which * PASSES + g, :],
+                    rhs=x_codes[:, g, :].bitcast(FP8X4),
+                    rhs_scale=x_scales[:, g, :],
+                    start=(g == 0),
+                    stop=(g == PASSES - 1),
+                )
+
+        def small_terms(ot, b):
+            mine = slice(b * SMALL, (b + 1) * SMALL)
+            a43_ps = psum_mix.tile([P, 2, SMALL], F32)
+            mix(a43_ps[:, 0, :], ot, 3, ar_codes[:, :, mine], ar_scales[:, :, mine])
+            mix(a43_ps[:, 1, :], ot, 2, at_codes[:, :, mine], at_scales[:, :, mine])
+            along_r = work.tile([P, SMALL], F32)
+            nc.vector.scalar_tensor_tensor(
+                out=along_r[:], in0=a43_ps[:, 0, :], scalar=0.5, in1=a5_twice[:, ot, b, :],
+                op0=ALU.mult, op1=ALU.add,
             )
-        a5_twice = keep.tile([P, O_TILES, B * SMALL], F32)
-        nc.gpsimd.tensor_scalar(
-            out=a5_twice[:].rearrange("o t x -> o (t x)"),
-            in0=a5_sb[:].rearrange("o t b x -> o (t b x)"),
-            scalar1=2.0,
-            scalar2=0.0,
-            op0=ALU.mult,
-            op1=ALU.add,
-        )
+            along_t = work.tile([P, SMALL], F32)
+            nc.scalar.activation(out=along_t[:], in_=a43_ps[:, 1, :], func=ACT.Copy, scale=0.1)
+            a2_ps = psum_mix.tile([P, SLAB], F32)
+            b_slab = slice(b * SLAB, (b + 1) * SLAB)
+            mix(a2_ps[:], ot, 1, am_codes[:, :, b_slab], am_scales[:, :, b_slab])
+            return along_r, along_t, a2_ps
+
+        def weighted_sums(ot, b, y, terms, a1_pool, a1_bufs):
+            along_r, along_t, a2_ps = terms
+            for hm in range(2):
+                half = slice(hm * HALF, (hm + 1) * HALF)
+                for mm in range(2):
+                    m = 2 * hm + mm
+                    slab = slice(m * SLAB, (m + 1) * SLAB)
+                    a1_ps = a1_pool.tile([P, SLAB], F32, bufs=a1_bufs)
+                    mix(a1_ps[:], ot, 0, a_codes[:, :, b, slab], a_scales[:, :, b, slab])
+                    nc.vector.tensor_tensor(
+                        out=y[:, slab].rearrange("o (k r t) -> o k r t", r=NR, t=NT),
+                        in0=a1_ps[:].rearrange("o (k r t) -> o k r t", r=NR, t=NT),
+                        in1=along_r[:, m * K * NT : (m + 1) * K * NT]
+                        .rearrange("o (k t) -> o k t", t=NT)
+                        .unsqueeze(2)
+                        .to_broadcast([P, K, NR, NT]),
+                        op=ALU.add,
+                    )
+                nc.vector.scalar_tensor_tensor(
+                    out=y[:, half].rearrange("o (m x) -> o m x", m=2),
+                    in0=a2_ps[:].unsqueeze(1).to_broadcast([P, 2, SLAB]),
+                    scalar=0.1 / M,
+                    in1=y[:, half].rearrange("o (m x) -> o m x", m=2),
+                    op0=ALU.mult,
+                    op1=ALU.add,
+                )
+                nc.vector.tensor_tensor(
+                    out=y[:, half].rearrange("o (x t) -> o x t", t=NT),
+                    in0=y[:, half].rearrange("o (x t) -> o x t", t=NT),
+                    in1=along_t[:, hm * (SMALL // 2) : (hm + 1) * (SMALL // 2)]
+                    .unsqueeze(2)
+                    .to_broadcast([P, SMALL // 2, NT]),
+                    op=ALU.add,
+                )
+                unit = 2 * b + hm
+                nc.scalar.activation(
+                    out=y[:, half], in_=y[:, half], func=ACT.Relu,
+                    accum_out=sums[:, ot, 0, unit : unit + 1],
+                )
+                squares = work.tile([P, HALF], BF16)
+                nc.scalar.activation(
+                    out=squares[:], in_=y[:, half], func=ACT.Square,
+                    accum_out=sums[:, ot, 1, unit : unit + 1],
+                )
 
         with ExitStack() as first:
             stage = first.enter_context(tc.tile_pool(name="stage", bufs=2))
             psum = first.enter_context(tc.psum_pool(name="psum_first", bufs=2))
 
-            gb_ps = psum.tile([P, P], BF16, bufs=1)
-            nc.tensor.transpose(out=gb_ps[:], in_=gb_rows[:], identity=ident_bf[:])
-            nc.vector.tensor_copy(out=gamma_beta[:], in_=gb_ps[:, 0 : 2 * O_TILES])
+            def small_inputs():
+                nc.sync.dma_start(
+                    out=gb_rows[0:O_TILES, :], in_=gamma.rearrange("(t o) -> t o", o=P)
+                )
+                nc.sync.dma_start(
+                    out=gb_rows[O_TILES : 2 * O_TILES, :], in_=beta.rearrange("(t o) -> t o", o=P)
+                )
+                for b in range(B):
+                    nc.sync.dma_start(
+                        out=a5_sb[:, :, b, :], in_=a5_rows[b].rearrange("(t o) x -> o t x", o=P)
+                    )
+                nc.gpsimd.tensor_scalar(
+                    out=a5_twice[:].rearrange("o t b x -> o (t b x)"),
+                    in0=a5_sb[:].rearrange("o t b x -> o (t b x)"),
+                    scalar1=2.0, scalar2=0.0, op0=ALU.mult, op1=ALU.add,
+                )
+                gb_ps = psum.tile([P, P], BF16, tag="turned")
+                nc.tensor.transpose(out=gb_ps[:], in_=gb_rows[:], identity=ident_bf[:])
+                nc.vector.tensor_copy(out=gamma_beta[:], in_=gb_ps[:, 0 : 2 * O_TILES])
 
-            for b in range(B):
-                for g in range(PASSES):
+            def prepare_weights(ot):
+                w_raw = stage.tile([P, N_W * C], BF16, bufs=1)
+                for which in range(N_W):
+                    nc.sync.dma_start(
+                        out=w_raw[:, which * C : (which + 1) * C],
+                        in_=weights[which][ot * P : (ot + 1) * P, :],
+                    )
+                w_words = w_raw[:].bitcast(F32).rearrange(
+                    "o (w g p u) -> o w g p u", w=N_W, g=PASSES, u=2
+                )
+                w_grp = stage.tile([P, N_W * PASSES * P * PACK], BF16, bufs=1, align_bytes=64)
+                w_grp_words = w_grp[:].bitcast(F32).rearrange(
+                    "p (s o u) -> p s o u", s=N_W * PASSES, u=2
+                )
+                for which in range(N_W):
+                    wt_ps = psum.tile([P, PASSES, 2, P], F32, tag="turned")
+                    for g in range(PASSES):
+                        for u in range(2):
+                            nc.tensor.transpose(
+                                out=wt_ps[:, g, u, :],
+                                in_=w_words[:, which, g, :, u],
+                                identity=ident_f32[:],
+                            )
+                    nc.scalar.copy(
+                        out=w_grp_words[:, which * PASSES : (which + 1) * PASSES, :, :],
+                        in_=wt_ps[:].rearrange("p g u o -> p g o u"),
+                    )
+                nc.vector.quantize_mx(
+                    out=w_codes[:, ot, :, :].rearrange("p s o -> p (s o)").bitcast(FP8X4),
+                    scales=w_scales[:, ot, :, :].rearrange("p s o -> p (s o)"),
+                    in_=w_grp[:],
+                )
+
+            open_slab = {}
+
+            def quantise_chunk(b, g, h, vector_slabs):
+                if h == 0:
                     at_grp = stage.tile([P, SMALL, PACK], BF16, align_bytes=64)
                     ar_grp = stage.tile([P, SMALL, PACK], BF16, align_bytes=64)
-                    pair_sums = []
-                    for h in range(2):
-                        cols = slice(h * HALF, (h + 1) * HALF)
-                        raw = stage.tile([P, PACK, HALF], BF16, bufs=4)
-                        nc.sync.dma_start(
-                            out=raw[:],
-                            in_=a_rows[b, g * K_PASS : (g + 1) * K_PASS, cols].rearrange(
-                                "(p j) w -> p j w", j=PACK
-                            ),
-                        )
-                        grouped = stage.tile([P, HALF, PACK], BF16, bufs=3, align_bytes=64)
-                        regroup = nc.vector.tensor_copy if h == 0 else nc.scalar.copy
-                        for mm in range(2):
-                            slab = slice(mm * SLAB, (mm + 1) * SLAB)
-                            regroup(
-                                out=grouped[:, slab, :].rearrange("p (c i) j -> p c j i", i=4),
-                                in_=raw[:, :, slab].rearrange("p j (c i) -> p c j i", i=4),
-                            )
-                        flat = grouped[:].rearrange("p w j -> p (w j)")
-                        nc.vector.quantize_mx(
-                            out=a_codes[:, g, b, cols].bitcast(FP8X4),
-                            scales=a_scales[:, g, b, cols],
-                            in_=flat,
-                        )
-                        pair_sum = stage.tile([P, SLAB * PACK], F32, bufs=3)
-                        nc.vector.tensor_tensor(
-                            out=pair_sum[:],
-                            in0=flat[:, 0 : SLAB * PACK],
-                            in1=flat[:, SLAB * PACK : 2 * SLAB * PACK],
-                            op=ALU.add,
-                        )
-                        pair_sums.append(pair_sum)
+                    open_slab["at"] = at_grp
+                    open_slab["ar"] = ar_grp
+                    open_slab["pairs"] = []
+                at_grp = open_slab["at"]
+                ar_grp = open_slab["ar"]
+                cols = slice(h * HALF, (h + 1) * HALF)
+                raw = stage.tile([P, PACK, HALF], BF16, bufs=3)
+                nc.sync.dma_start(
+                    out=raw[:],
+                    in_=a_rows[b, g * K_PASS : (g + 1) * K_PASS, cols].rearrange(
+                        "(p j) w -> p j w", j=PACK
+                    ),
+                )
+                grouped = stage.tile([P, HALF, PACK], BF16, bufs=2, align_bytes=64)
+                for mm in range(2):
+                    slab = slice(mm * SLAB, (mm + 1) * SLAB)
+                    regroup = nc.vector.tensor_copy if mm < vector_slabs else nc.scalar.copy
+                    regroup(
+                        out=grouped[:, slab, :].rearrange("p (c i) j -> p c j i", i=4),
+                        in_=raw[:, :, slab].rearrange("p j (c i) -> p c j i", i=4),
+                    )
+                flat = grouped[:].rearrange("p w j -> p (w j)")
+                nc.vector.quantize_mx(
+                    out=a_codes[:, g, b, cols].bitcast(FP8X4),
+                    scales=a_scales[:, g, b, cols],
+                    in_=flat,
+                )
+                pair_sum = stage.tile([P, SLAB * PACK], F32, bufs=2)
+                nc.vector.tensor_tensor(
+                    out=pair_sum[:],
+                    in0=flat[:, 0 : SLAB * PACK],
+                    in1=flat[:, SLAB * PACK : 2 * SLAB * PACK],
+                    op=ALU.add,
+                )
+                open_slab["pairs"].append(pair_sum)
 
-                        for mm in range(2):
-                            m = 2 * h + mm
-                            mean_ps = psum.tile([P, PACK, BLOCKS, 2 * PER_BLOCK], F32)
-                            for jj in range(PACK // 2):
-                                flipped_ps = psum.tile([P, 2, BLOCKS, P], BF16, bufs=3)
-                                for j2 in range(2):
-                                    for blk in range(BLOCKS):
-                                        first_pos = mm * SLAB + blk * P
-                                        nc.tensor.transpose(
-                                            out=flipped_ps[:, j2, blk, :],
-                                            in_=raw[:, 2 * jj + j2, first_pos : first_pos + P],
-                                            identity=ident_bf[:],
-                                        )
-                                flipped = stage.tile([P, 2, BLOCKS, P], BF16, bufs=4)
-                                nc.scalar.copy(out=flipped[:], in_=flipped_ps[:])
-                                for j2 in range(2):
-                                    for blk in range(BLOCKS):
-                                        nc.tensor.matmul(
-                                            out=mean_ps[:, 2 * jj + j2, blk, :],
-                                            lhsT=flipped[:, j2, blk, :],
-                                            rhs=mean_w[:],
-                                            start=True,
-                                            stop=True,
-                                        )
-                            leave = nc.vector.tensor_copy if mm == 0 else nc.scalar.copy
-                            by_pos = mean_ps[:].rearrange("p j k n -> p k n j")
-                            mine = slice(m * K * NR, (m + 1) * K * NR)
-                            leave(
-                                out=at_grp[:, mine, :].rearrange(
-                                    "p (k n) j -> p k n j", n=PER_BLOCK
-                                ),
-                                in_=by_pos[:, :, 0:PER_BLOCK, :],
-                            )
-                            leave(
-                                out=ar_grp[:, mine, :].rearrange(
-                                    "p (k n) j -> p k n j", n=PER_BLOCK
-                                ),
-                                in_=by_pos[:, :, PER_BLOCK : 2 * PER_BLOCK, :],
-                            )
+                for mm in range(2):
+                    m = 2 * h + mm
+                    mean_ps = psum.tile([P, PACK, BLOCKS, 2 * PER_BLOCK], F32)
+                    for jj in range(PACK // 2):
+                        flipped_ps = psum.tile([P, 2, BLOCKS, P], BF16, tag="turned")
+                        for j2 in range(2):
+                            for blk in range(BLOCKS):
+                                first_pos = mm * SLAB + blk * P
+                                nc.tensor.transpose(
+                                    out=flipped_ps[:, j2, blk, :],
+                                    in_=raw[:, 2 * jj + j2, first_pos : first_pos + P],
+                                    identity=ident_bf[:],
+                                )
+                        flipped = stage.tile([P, 2, BLOCKS, P], BF16, bufs=4)
+                        nc.scalar.copy(out=flipped[:], in_=flipped_ps[:])
+                        for j2 in range(2):
+                            for blk in range(BLOCKS):
+                                nc.tensor.matmul(
+                                    out=mean_ps[:, 2 * jj + j2, blk, :],
+                                    lhsT=flipped[:, j2, blk, :],
+                                    rhs=mean_w[:],
+                                    start=True,
+                                    stop=True,
+                                )
+                    by_pos = mean_ps[:].rearrange("p j k n -> p k n j")
+                    mine = slice(m * K * NR, (m + 1) * K * NR)
+                    nc.scalar.copy(
+                        out=at_grp[:, mine, :].rearrange("p (k n) j -> p k n j", n=PER_BLOCK),
+                        in_=by_pos[:, :, 0:PER_BLOCK, :],
+                    )
+                    nc.scalar.copy(
+                        out=ar_grp[:, mine, :].rearrange("p (k n) j -> p k n j", n=PER_BLOCK),
+                        in_=by_pos[:, :, PER_BLOCK : 2 * PER_BLOCK, :],
+                    )
 
-                    am_grp = stage.tile([P, SLAB * PACK], BF16, align_bytes=64)
+                if h == 1:
+                    pairs = open_slab["pairs"]
+                    am_grp = stage.tile([P, SLAB * PACK], BF16, bufs=1, align_bytes=64)
                     nc.vector.tensor_tensor(
-                        out=am_grp[:], in0=pair_sums[0][:], in1=pair_sums[1][:], op=ALU.add
+                        out=am_grp[:], in0=pairs[0][:], in1=pairs[1][:], op=ALU.add
                     )
                     nc.vector.quantize_mx(
                         out=am_codes[:, g, b * SLAB : (b + 1) * SLAB].bitcast(FP8X4),
@@ -216,116 +318,37 @@ def tile_layer_3d_dep_pa_kernel(tc, A, P1, P2, P3, P4, a5, gamma, beta, out):
                         in_=ar_grp[:].rearrange("p w j -> p (w j)"),
                     )
 
-                    which = b * PASSES + g
-                    w_raw = stage.tile([P, O_TILES * C], BF16)
-                    nc.sync.dma_start(
-                        out=w_raw[:].rearrange("o (t c) -> o t c", t=O_TILES),
-                        in_=weights[which].rearrange("(t o) c -> o t c", o=P),
-                    )
-                    w_words = w_raw[:].bitcast(F32).rearrange(
-                        "o (t g p u) -> o t g p u", t=O_TILES, g=PASSES, u=2
-                    )
-                    for wg in range(PASSES):
-                        w_grp = stage.tile([P, O * PACK], BF16, align_bytes=64)
-                        w_grp_words = w_grp[:].bitcast(F32).rearrange("p (o u) -> p o u", u=2)
-                        for tp in range(O_TILES // 2):
-                            wt_ps = psum.tile([P, 2, 2, P], F32)
-                            for t2 in range(2):
-                                for u in range(2):
-                                    nc.tensor.transpose(
-                                        out=wt_ps[:, t2, u, :],
-                                        in_=w_words[:, 2 * tp + t2, wg, :, u],
-                                        identity=ident_f32[:],
-                                    )
-                            nc.scalar.copy(
-                                out=w_grp_words[:, tp * 2 * P : (tp + 1) * 2 * P, :].rearrange(
-                                    "p (t o) u -> p t o u", t=2
-                                ),
-                                in_=wt_ps[:].rearrange("p t u o -> p t o u"),
-                            )
-                        nc.vector.quantize_mx(
-                            out=w_codes[:, which, wg, :].bitcast(FP8X4),
-                            scales=w_scales[:, which, wg, :],
-                            in_=w_grp[:],
-                        )
+            quantise_chunk(0, 0, 0, 2)
+            quantise_chunk(0, 0, 1, 0)
+            small_inputs()
+            prepare_weights(0)
+            quantise_chunk(0, 1, 0, 2)
+            quantise_chunk(0, 1, 1, 0)
+            prepare_weights(1)
+
+            for step in range(O_TILES):
+                g, h = divmod(step, 2)
+                quantise_chunk(1, g, h, 1 if h == 0 else 0)
+                terms = small_terms(step, 0)
+                weighted_sums(step, 0, y_first[:, step, :], terms, psum, 2)
+                if step + 2 < O_TILES:
+                    prepare_weights(step + 2)
 
         with ExitStack() as second:
-            work = second.enter_context(tc.tile_pool(name="work", bufs=2))
-            psum = second.enter_context(tc.psum_pool(name="psum_second", bufs=1))
+            late = second.enter_context(tc.tile_pool(name="late", bufs=3))
+            psum = second.enter_context(tc.psum_pool(name="psum_late", bufs=6))
 
+            terms = small_terms(0, 1)
             for ot in range(O_TILES):
                 o_cols = slice(ot * P, (ot + 1) * P)
-
-                def mix(acc, which, x_codes, x_scales):
-                    mx_product(
-                        nc, acc, w_codes[:, which, :, o_cols], w_scales[:, which, :, o_cols],
-                        x_codes, x_scales,
-                    )
-
-                a4_ps = psum.tile([P, B * SMALL], F32)
-                mix(a4_ps[:], 3, ar_codes[:], ar_scales[:])
-                along_r = work.tile([P, B, SMALL], F32)
-                nc.vector.scalar_tensor_tensor(
-                    out=along_r[:].rearrange("o b x -> o (b x)"),
-                    in0=a4_ps[:],
-                    scalar=0.5,
-                    in1=a5_twice[:, ot, :],
-                    op0=ALU.mult,
-                    op1=ALU.add,
-                )
-                a3_ps = psum.tile([P, B * SMALL], F32)
-                mix(a3_ps[:], 2, at_codes[:], at_scales[:])
-
-                y = work.tile([P, B, POS], F32, bufs=3)
-                sums = work.tile([P, 2, B], F32)
-                for b in range(B):
-                    a2_ps = psum.tile([P, SLAB], F32, bufs=2)
-                    b_slab = slice(b * SLAB, (b + 1) * SLAB)
-                    mix(a2_ps[:], 1, am_codes[:, :, b_slab], am_scales[:, :, b_slab])
-                    for m in range(M):
-                        slab = slice(m * SLAB, (m + 1) * SLAB)
-                        a1_ps = psum.tile([P, SLAB], F32, bufs=4)
-                        mix(a1_ps[:], 0, a_codes[:, :, b, slab], a_scales[:, :, b, slab])
-                        nc.vector.tensor_tensor(
-                            out=y[:, b, slab].rearrange("o (k r t) -> o k r t", r=NR, t=NT),
-                            in0=a1_ps[:].rearrange("o (k r t) -> o k r t", r=NR, t=NT),
-                            in1=along_r[:, b, m * K * NT : (m + 1) * K * NT]
-                            .rearrange("o (k t) -> o k t", t=NT)
-                            .unsqueeze(2)
-                            .to_broadcast([P, K, NR, NT]),
-                            op=ALU.add,
-                        )
-                    nc.vector.scalar_tensor_tensor(
-                        out=y[:, b, :].rearrange("o (m x) -> o m x", m=M),
-                        in0=a2_ps[:].unsqueeze(1).to_broadcast([P, M, SLAB]),
-                        scalar=0.1 / M,
-                        in1=y[:, b, :].rearrange("o (m x) -> o m x", m=M),
-                        op0=ALU.mult,
-                        op1=ALU.add,
-                    )
-                    nc.vector.scalar_tensor_tensor(
-                        out=y[:, b, :].rearrange("o (x t) -> o x t", t=NT),
-                        in0=a3_ps[:, b * SMALL : (b + 1) * SMALL]
-                        .unsqueeze(2)
-                        .to_broadcast([P, SMALL, NT]),
-                        scalar=0.1,
-                        in1=y[:, b, :].rearrange("o (x t) -> o x t", t=NT),
-                        op0=ALU.mult,
-                        op1=ALU.add,
-                    )
-                    nc.scalar.activation(
-                        out=y[:, b, :], in_=y[:, b, :], func=ACT.Relu,
-                        accum_out=sums[:, 0, b : b + 1],
-                    )
-                    squares = work.tile([P, POS], BF16)
-                    nc.scalar.activation(
-                        out=squares[:], in_=y[:, b, :], func=ACT.Square,
-                        accum_out=sums[:, 1, b : b + 1],
-                    )
+                y_second = late.tile([P, POS], F32)
+                weighted_sums(ot, 1, y_second[:], terms, psum, 6)
+                if ot + 1 < O_TILES:
+                    terms = small_terms(ot + 1, 1)
 
                 total = work.tile([P, 2], F32)
-                nc.gpsimd.tensor_tensor(
-                    out=total[:], in0=sums[:, :, 0], in1=sums[:, :, 1], op=ALU.add
+                nc.vector.tensor_reduce(
+                    out=total[:], in_=sums[:, ot, :, :], axis=AXIS_X, op=ALU.add
                 )
                 moments = work.tile([P, 2], F32)
                 nc.gpsimd.tensor_scalar(
@@ -360,13 +383,15 @@ def tile_layer_3d_dep_pa_kernel(tc, A, P1, P2, P3, P4, a5, gamma, beta, out):
                     in1=mean_gain[:], op=ALU.subtract,
                 )
 
-                nc.gpsimd.tensor_scalar(
-                    out=y[:, 0, :], in0=y[:, 0, :], scalar1=gain[:], scalar2=shift[:],
-                    op0=ALU.mult, op1=ALU.add,
-                )
-                nc.scalar.activation(
-                    out=y[:, 1, :], in_=y[:, 1, :], func=ACT.Identity,
-                    scale=gain[:], bias=shift[:],
-                )
-                for b in range(B):
-                    nc.sync.dma_start(out=out_rows[b, o_cols, :], in_=y[:, b, :])
+                for hm in range(2):
+                    half = slice(hm * HALF, (hm + 1) * HALF)
+                    nc.gpsimd.tensor_scalar(
+                        out=y_first[:, ot, half], in0=y_first[:, ot, half],
+                        scalar1=gain[:], scalar2=shift[:], op0=ALU.mult, op1=ALU.add,
+                    )
+                    nc.sync.dma_start(out=out_rows[0, o_cols, half], in_=y_first[:, ot, half])
+                    nc.scalar.activation(
+                        out=y_second[:, half], in_=y_second[:, half], func=ACT.Identity,
+                        scale=gain[:], bias=shift[:],
+                    )
+                    nc.sync.dma_start(out=out_rows[1, o_cols, half], in_=y_second[:, half])

@@ -24,9 +24,12 @@ HALF = POS // 2
 SLAB = K * NR * NT
 SMALL = M * K * NT
 O_TILES = O // P
-BLOCKS = SLAB // P
-PER_BLOCK = P // NT
+TILE_POS = 2 * P
+TILES = SLAB // TILE_POS
+PER_TILE = TILE_POS // NT
+TP = NT // 2
 N_W = 4
+STEPS = B * PASSES * M
 UNITS = 2 * B
 
 FLOPS = 2 * O * C * B * (POS + SLAB + 2 * SMALL)
@@ -63,20 +66,24 @@ def tile_layer_3d_dep_pa_kernel(tc, A, P1, P2, P3, P4, a5, gamma, beta, out):
         ident_bf = keep.tile([P, P], BF16)
         nc.vector.tensor_copy(out=ident_bf[:], in_=ident_f32[:])
 
-        member = keep.tile([P, 2 * PER_BLOCK], F32)
-        nc.vector.tensor_reduce(
-            out=member[:, 0:PER_BLOCK],
-            in_=ident_f32[:].rearrange("q (n t) -> q n t", t=NT),
-            axis=AXIS_X,
-            op=ALU.add,
-        )
-        nc.vector.tensor_reduce(
-            out=member[:, PER_BLOCK : 2 * PER_BLOCK].rearrange("q (k t) -> q k t", t=NT),
-            in_=ident_f32[:].rearrange("q (k r t) -> q k t r", r=NR, t=NT),
-            axis=AXIS_X,
-            op=ALU.add,
-        )
-        mean_w = keep.tile([P, 2 * PER_BLOCK], BF16)
+        member = keep.tile([P, 2, 2 * PER_TILE], F32)
+        nc.vector.memset(member[:], 0.0)
+        for e in range(2):
+            nc.vector.tensor_reduce(
+                out=member[:, e, 0:PER_TILE],
+                in_=ident_f32[:].rearrange("q (n tp) -> q n tp", tp=TP),
+                axis=AXIS_X,
+                op=ALU.add,
+            )
+            nc.vector.tensor_reduce(
+                out=member[:, e, PER_TILE : 2 * PER_TILE].rearrange(
+                    "q (k tp e2) -> q k tp e2", tp=TP, e2=2
+                )[:, :, :, e],
+                in_=ident_f32[:].rearrange("q (k r tp) -> q k tp r", r=NR, tp=TP),
+                axis=AXIS_X,
+                op=ALU.add,
+            )
+        mean_w = keep.tile([P, 2, 2 * PER_TILE], BF16)
         nc.vector.tensor_scalar_mul(out=mean_w[:], in0=member[:], scalar1=1.0 / NT)
 
         minus_half = keep.tile([P, 1], F32)
@@ -100,9 +107,11 @@ def tile_layer_3d_dep_pa_kernel(tc, A, P1, P2, P3, P4, a5, gamma, beta, out):
                     stop=(g == PASSES - 1),
                 )
 
-        def small_terms(ot, b):
+        terms_of = {}
+
+        def small_terms(ot, b, small_pool):
             mine = slice(b * SMALL, (b + 1) * SMALL)
-            a43_ps = psum_mix.tile([P, 2, SMALL], F32)
+            a43_ps = small_pool.tile([P, 2, SMALL], F32, bufs=1)
             mix(a43_ps[:, 0, :], ot, 3, ar_codes[:, :, mine], ar_scales[:, :, mine])
             mix(a43_ps[:, 1, :], ot, 2, at_codes[:, :, mine], at_scales[:, :, mine])
             along_r = work.tile([P, SMALL], F32)
@@ -112,59 +121,192 @@ def tile_layer_3d_dep_pa_kernel(tc, A, P1, P2, P3, P4, a5, gamma, beta, out):
             )
             along_t = work.tile([P, SMALL], F32)
             nc.scalar.activation(out=along_t[:], in_=a43_ps[:, 1, :], func=ACT.Copy, scale=0.1)
-            a2_ps = psum_mix.tile([P, SLAB], F32)
+            a2_ps = small_pool.tile([P, SLAB], F32, bufs=1)
             b_slab = slice(b * SLAB, (b + 1) * SLAB)
             mix(a2_ps[:], ot, 1, am_codes[:, :, b_slab], am_scales[:, :, b_slab])
-            return along_r, along_t, a2_ps
+            terms_of[(ot, b)] = (along_r, along_t, a2_ps)
 
-        def weighted_sums(ot, b, y, terms, a1_pool, a1_bufs):
-            along_r, along_t, a2_ps = terms
-            for hm in range(2):
-                half = slice(hm * HALF, (hm + 1) * HALF)
-                for mm in range(2):
-                    m = 2 * hm + mm
-                    slab = slice(m * SLAB, (m + 1) * SLAB)
-                    a1_ps = a1_pool.tile([P, SLAB], F32, bufs=a1_bufs)
-                    mix(a1_ps[:], ot, 0, a_codes[:, :, b, slab], a_scales[:, :, b, slab])
-                    nc.vector.tensor_tensor(
-                        out=y[:, slab].rearrange("o (k r t) -> o k r t", r=NR, t=NT),
-                        in0=a1_ps[:].rearrange("o (k r t) -> o k r t", r=NR, t=NT),
-                        in1=along_r[:, m * K * NT : (m + 1) * K * NT]
-                        .rearrange("o (k t) -> o k t", t=NT)
-                        .unsqueeze(2)
-                        .to_broadcast([P, K, NR, NT]),
-                        op=ALU.add,
-                    )
-                nc.vector.scalar_tensor_tensor(
-                    out=y[:, half].rearrange("o (m x) -> o m x", m=2),
-                    in0=a2_ps[:].unsqueeze(1).to_broadcast([P, 2, SLAB]),
-                    scalar=0.1 / M,
-                    in1=y[:, half].rearrange("o (m x) -> o m x", m=2),
-                    op0=ALU.mult,
-                    op1=ALU.add,
-                )
+        def weighted_sum(ot, b, hm, y, a1_pool, a1_bufs):
+            along_r, along_t, a2_ps = terms_of[(ot, b)]
+            half = slice(hm * HALF, (hm + 1) * HALF)
+            for mm in range(2):
+                m = 2 * hm + mm
+                slab = slice(m * SLAB, (m + 1) * SLAB)
+                a1_ps = a1_pool.tile([P, SLAB], F32, bufs=a1_bufs)
+                mix(a1_ps[:], ot, 0, a_codes[:, :, b, slab], a_scales[:, :, b, slab])
                 nc.vector.tensor_tensor(
-                    out=y[:, half].rearrange("o (x t) -> o x t", t=NT),
-                    in0=y[:, half].rearrange("o (x t) -> o x t", t=NT),
-                    in1=along_t[:, hm * (SMALL // 2) : (hm + 1) * (SMALL // 2)]
+                    out=y[:, slab].rearrange("o (k r t) -> o k r t", r=NR, t=NT),
+                    in0=a1_ps[:].rearrange("o (k r t) -> o k r t", r=NR, t=NT),
+                    in1=along_r[:, m * K * NT : (m + 1) * K * NT]
+                    .rearrange("o (k t) -> o k t", t=NT)
                     .unsqueeze(2)
-                    .to_broadcast([P, SMALL // 2, NT]),
+                    .to_broadcast([P, K, NR, NT]),
                     op=ALU.add,
                 )
-                unit = 2 * b + hm
-                nc.scalar.activation(
-                    out=y[:, half], in_=y[:, half], func=ACT.Relu,
-                    accum_out=sums[:, ot, 0, unit : unit + 1],
-                )
-                squares = work.tile([P, HALF], BF16)
-                nc.scalar.activation(
-                    out=squares[:], in_=y[:, half], func=ACT.Square,
-                    accum_out=sums[:, ot, 1, unit : unit + 1],
-                )
+            nc.vector.scalar_tensor_tensor(
+                out=y[:, half].rearrange("o (m x) -> o m x", m=2),
+                in0=a2_ps[:].unsqueeze(1).to_broadcast([P, 2, SLAB]),
+                scalar=0.1 / M,
+                in1=y[:, half].rearrange("o (m x) -> o m x", m=2),
+                op0=ALU.mult,
+                op1=ALU.add,
+            )
+            nc.vector.tensor_tensor(
+                out=y[:, half].rearrange("o (x t) -> o x t", t=NT),
+                in0=y[:, half].rearrange("o (x t) -> o x t", t=NT),
+                in1=along_t[:, hm * (SMALL // 2) : (hm + 1) * (SMALL // 2)]
+                .unsqueeze(2)
+                .to_broadcast([P, SMALL // 2, NT]),
+                op=ALU.add,
+            )
+
+        def relu_and_sums(ot, b, hm, y):
+            half = slice(hm * HALF, (hm + 1) * HALF)
+            unit = 2 * b + hm
+            nc.scalar.activation(
+                out=y[:, half], in_=y[:, half], func=ACT.Relu,
+                accum_out=sums[:, ot, 0, unit : unit + 1],
+            )
+            squares = work.tile([P, HALF], BF16)
+            nc.scalar.activation(
+                out=squares[:], in_=y[:, half], func=ACT.Square,
+                accum_out=sums[:, ot, 1, unit : unit + 1],
+            )
 
         with ExitStack() as first:
             stage = first.enter_context(tc.tile_pool(name="stage", bufs=2))
             psum = first.enter_context(tc.psum_pool(name="psum_first", bufs=2))
+
+            raw_of = {}
+            grouped_of = {}
+            flipped_of = {}
+            means_of = {}
+            pairs_of = {}
+            w_raw_of = {}
+            w_grp_of = {}
+
+            def place(sg):
+                c, mm = divmod(sg, 2)
+                return c // 4, (c // 2) % 2, 2 * (c % 2) + mm
+
+            def load(sg):
+                b, g, m = place(sg)
+                raw = stage.tile([P, PACK, SLAB], BF16, bufs=6)
+                nc.sync.dma_start(
+                    out=raw[:],
+                    in_=a_rows[
+                        b, g * K_PASS : (g + 1) * K_PASS, m * SLAB : (m + 1) * SLAB
+                    ].rearrange("(p j) w -> p j w", j=PACK),
+                )
+                raw_of[sg] = raw
+
+            def regroup(sg):
+                c, mm = divmod(sg, 2)
+                b, g, m = place(sg)
+                if mm == 0:
+                    grouped = stage.tile([P, HALF, PACK], BF16, bufs=2, align_bytes=64)
+                    grouped_of[c] = grouped
+                on_vector = (m < 2) if b == 0 else (m == 0)
+                copy = nc.vector.tensor_copy if on_vector else nc.scalar.copy
+                copy(
+                    out=grouped_of[c][:, mm * SLAB : (mm + 1) * SLAB, :].rearrange(
+                        "p (c i) j -> p c j i", i=4
+                    ),
+                    in_=raw_of[sg][:].rearrange("p j (c i) -> p c j i", i=4),
+                )
+
+            def quantise_pairs(c):
+                b, g, m = place(2 * c)
+                cols = slice(m * SLAB, (m + 2) * SLAB)
+                flat = grouped_of[c][:].rearrange("p w j -> p (w j)")
+                nc.vector.quantize_mx(
+                    out=a_codes[:, g, b, cols].bitcast(FP8X4),
+                    scales=a_scales[:, g, b, cols],
+                    in_=flat,
+                )
+                pair_sum = stage.tile([P, SLAB * PACK], F32, bufs=2)
+                nc.vector.tensor_tensor(
+                    out=pair_sum[:],
+                    in0=flat[:, 0 : SLAB * PACK],
+                    in1=flat[:, SLAB * PACK : 2 * SLAB * PACK],
+                    op=ALU.add,
+                )
+                pairs_of.setdefault((b, g), []).append(pair_sum)
+
+            def sum_over_m(b, g):
+                pairs = pairs_of[(b, g)]
+                am_grp = stage.tile([P, SLAB * PACK], BF16, bufs=1, align_bytes=64)
+                nc.vector.tensor_tensor(
+                    out=am_grp[:], in0=pairs[0][:], in1=pairs[1][:], op=ALU.add
+                )
+                nc.vector.quantize_mx(
+                    out=am_codes[:, g, b * SLAB : (b + 1) * SLAB].bitcast(FP8X4),
+                    scales=am_scales[:, g, b * SLAB : (b + 1) * SLAB],
+                    in_=am_grp[:],
+                )
+
+            def turn(sg):
+                raw_words = raw_of[sg][:].bitcast(F32)
+                flipped_of[sg] = []
+                for tl in range(TILES):
+                    flipped_ps = psum.tile([P, PACK, P], F32, tag="turned")
+                    for j in range(PACK):
+                        nc.tensor.transpose(
+                            out=flipped_ps[:, j, :],
+                            in_=raw_words[:, j, tl * P : (tl + 1) * P],
+                            identity=ident_f32[:],
+                        )
+                    flipped = stage.tile([P, PACK, P], F32, bufs=4)
+                    nc.scalar.copy(out=flipped[:], in_=flipped_ps[:])
+                    flipped_of[sg].append(flipped)
+
+            def means(sg):
+                b, g, m = place(sg)
+                if m == 0:
+                    at_grp = stage.tile([P, SMALL, PACK], BF16, align_bytes=64)
+                    ar_grp = stage.tile([P, SMALL, PACK], BF16, align_bytes=64)
+                    means_of[(b, g)] = (at_grp, ar_grp)
+                at_grp, ar_grp = means_of[(b, g)]
+                mean_ps = psum.tile([P, PACK, TILES, 2 * PER_TILE], F32)
+                for tl in range(TILES):
+                    halves = (
+                        flipped_of[sg][tl][:]
+                        .rearrange("q j p -> q (j p)")
+                        .bitcast(BF16)
+                        .rearrange("q (j p e) -> q j p e", j=PACK, e=2)
+                    )
+                    for j in range(PACK):
+                        for e in range(2):
+                            nc.tensor.matmul(
+                                out=mean_ps[:, j, tl, :],
+                                lhsT=halves[:, j, :, e],
+                                rhs=mean_w[:, e, :],
+                                start=(e == 0),
+                                stop=(e == 1),
+                            )
+                by_pos = mean_ps[:].rearrange("p j k n -> p k n j")
+                mine = slice(m * K * NR, (m + 1) * K * NR)
+                nc.scalar.copy(
+                    out=at_grp[:, mine, :].rearrange("p (k n) j -> p k n j", n=PER_TILE),
+                    in_=by_pos[:, :, 0:PER_TILE, :],
+                )
+                nc.scalar.copy(
+                    out=ar_grp[:, mine, :].rearrange("p (k n) j -> p k n j", n=PER_TILE),
+                    in_=by_pos[:, :, PER_TILE : 2 * PER_TILE, :],
+                )
+
+            def finish(b, g):
+                at_grp, ar_grp = means_of[(b, g)]
+                nc.vector.quantize_mx(
+                    out=at_codes[:, g, b * SMALL : (b + 1) * SMALL].bitcast(FP8X4),
+                    scales=at_scales[:, g, b * SMALL : (b + 1) * SMALL],
+                    in_=at_grp[:].rearrange("p w j -> p (w j)"),
+                )
+                nc.vector.quantize_mx(
+                    out=ar_codes[:, g, b * SMALL : (b + 1) * SMALL].bitcast(FP8X4),
+                    scales=ar_scales[:, g, b * SMALL : (b + 1) * SMALL],
+                    in_=ar_grp[:].rearrange("p w j -> p (w j)"),
+                )
 
             def small_inputs():
                 nc.sync.dma_start(
@@ -182,25 +324,32 @@ def tile_layer_3d_dep_pa_kernel(tc, A, P1, P2, P3, P4, a5, gamma, beta, out):
                     in0=a5_sb[:].rearrange("o t b x -> o (t b x)"),
                     scalar1=2.0, scalar2=0.0, op0=ALU.mult, op1=ALU.add,
                 )
+
+            def turn_gamma_beta():
                 gb_ps = psum.tile([P, P], BF16, tag="turned")
                 nc.tensor.transpose(out=gb_ps[:], in_=gb_rows[:], identity=ident_bf[:])
                 nc.vector.tensor_copy(out=gamma_beta[:], in_=gb_ps[:, 0 : 2 * O_TILES])
 
-            def prepare_weights(ot):
-                w_raw = stage.tile([P, N_W * C], BF16, bufs=1)
+            def load_weights(ot):
+                w_raw = stage.tile([P, N_W * C], BF16, bufs=2)
                 for which in range(N_W):
                     nc.sync.dma_start(
                         out=w_raw[:, which * C : (which + 1) * C],
                         in_=weights[which][ot * P : (ot + 1) * P, :],
                     )
-                w_words = w_raw[:].bitcast(F32).rearrange(
+                w_raw_of[ot] = w_raw
+
+            def turn_weights(ot, pair):
+                if pair == 0:
+                    w_grp = stage.tile([P, N_W * PASSES * P * PACK], BF16, bufs=1, align_bytes=64)
+                    w_grp_of[ot] = w_grp
+                w_words = w_raw_of[ot][:].bitcast(F32).rearrange(
                     "o (w g p u) -> o w g p u", w=N_W, g=PASSES, u=2
                 )
-                w_grp = stage.tile([P, N_W * PASSES * P * PACK], BF16, bufs=1, align_bytes=64)
-                w_grp_words = w_grp[:].bitcast(F32).rearrange(
+                w_grp_words = w_grp_of[ot][:].bitcast(F32).rearrange(
                     "p (s o u) -> p s o u", s=N_W * PASSES, u=2
                 )
-                for which in range(N_W):
+                for which in (2 * pair, 2 * pair + 1):
                     wt_ps = psum.tile([P, PASSES, 2, P], F32, tag="turned")
                     for g in range(PASSES):
                         for u in range(2):
@@ -213,139 +362,65 @@ def tile_layer_3d_dep_pa_kernel(tc, A, P1, P2, P3, P4, a5, gamma, beta, out):
                         out=w_grp_words[:, which * PASSES : (which + 1) * PASSES, :, :],
                         in_=wt_ps[:].rearrange("p g u o -> p g o u"),
                     )
+
+            def quantise_weights(ot):
                 nc.vector.quantize_mx(
                     out=w_codes[:, ot, :, :].rearrange("p s o -> p (s o)").bitcast(FP8X4),
                     scales=w_scales[:, ot, :, :].rearrange("p s o -> p (s o)"),
-                    in_=w_grp[:],
+                    in_=w_grp_of[ot][:],
                 )
 
-            open_slab = {}
-
-            def quantise_chunk(b, g, h, vector_slabs):
-                if h == 0:
-                    at_grp = stage.tile([P, SMALL, PACK], BF16, align_bytes=64)
-                    ar_grp = stage.tile([P, SMALL, PACK], BF16, align_bytes=64)
-                    open_slab["at"] = at_grp
-                    open_slab["ar"] = ar_grp
-                    open_slab["pairs"] = []
-                at_grp = open_slab["at"]
-                ar_grp = open_slab["ar"]
-                cols = slice(h * HALF, (h + 1) * HALF)
-                raw = stage.tile([P, PACK, HALF], BF16, bufs=3)
-                nc.sync.dma_start(
-                    out=raw[:],
-                    in_=a_rows[b, g * K_PASS : (g + 1) * K_PASS, cols].rearrange(
-                        "(p j) w -> p j w", j=PACK
-                    ),
-                )
-                grouped = stage.tile([P, HALF, PACK], BF16, bufs=2, align_bytes=64)
-                for mm in range(2):
-                    slab = slice(mm * SLAB, (mm + 1) * SLAB)
-                    regroup = nc.vector.tensor_copy if mm < vector_slabs else nc.scalar.copy
-                    regroup(
-                        out=grouped[:, slab, :].rearrange("p (c i) j -> p c j i", i=4),
-                        in_=raw[:, :, slab].rearrange("p j (c i) -> p c j i", i=4),
-                    )
-                flat = grouped[:].rearrange("p w j -> p (w j)")
-                nc.vector.quantize_mx(
-                    out=a_codes[:, g, b, cols].bitcast(FP8X4),
-                    scales=a_scales[:, g, b, cols],
-                    in_=flat,
-                )
-                pair_sum = stage.tile([P, SLAB * PACK], F32, bufs=2)
-                nc.vector.tensor_tensor(
-                    out=pair_sum[:],
-                    in0=flat[:, 0 : SLAB * PACK],
-                    in1=flat[:, SLAB * PACK : 2 * SLAB * PACK],
-                    op=ALU.add,
-                )
-                open_slab["pairs"].append(pair_sum)
-
-                for mm in range(2):
-                    m = 2 * h + mm
-                    mean_ps = psum.tile([P, PACK, BLOCKS, 2 * PER_BLOCK], F32)
-                    for jj in range(PACK // 2):
-                        flipped_ps = psum.tile([P, 2, BLOCKS, P], BF16, tag="turned")
-                        for j2 in range(2):
-                            for blk in range(BLOCKS):
-                                first_pos = mm * SLAB + blk * P
-                                nc.tensor.transpose(
-                                    out=flipped_ps[:, j2, blk, :],
-                                    in_=raw[:, 2 * jj + j2, first_pos : first_pos + P],
-                                    identity=ident_bf[:],
-                                )
-                        flipped = stage.tile([P, 2, BLOCKS, P], BF16, bufs=4)
-                        nc.scalar.copy(out=flipped[:], in_=flipped_ps[:])
-                        for j2 in range(2):
-                            for blk in range(BLOCKS):
-                                nc.tensor.matmul(
-                                    out=mean_ps[:, 2 * jj + j2, blk, :],
-                                    lhsT=flipped[:, j2, blk, :],
-                                    rhs=mean_w[:],
-                                    start=True,
-                                    stop=True,
-                                )
-                    by_pos = mean_ps[:].rearrange("p j k n -> p k n j")
-                    mine = slice(m * K * NR, (m + 1) * K * NR)
-                    nc.scalar.copy(
-                        out=at_grp[:, mine, :].rearrange("p (k n) j -> p k n j", n=PER_BLOCK),
-                        in_=by_pos[:, :, 0:PER_BLOCK, :],
-                    )
-                    nc.scalar.copy(
-                        out=ar_grp[:, mine, :].rearrange("p (k n) j -> p k n j", n=PER_BLOCK),
-                        in_=by_pos[:, :, PER_BLOCK : 2 * PER_BLOCK, :],
-                    )
-
-                if h == 1:
-                    pairs = open_slab["pairs"]
-                    am_grp = stage.tile([P, SLAB * PACK], BF16, bufs=1, align_bytes=64)
-                    nc.vector.tensor_tensor(
-                        out=am_grp[:], in0=pairs[0][:], in1=pairs[1][:], op=ALU.add
-                    )
-                    nc.vector.quantize_mx(
-                        out=am_codes[:, g, b * SLAB : (b + 1) * SLAB].bitcast(FP8X4),
-                        scales=am_scales[:, g, b * SLAB : (b + 1) * SLAB],
-                        in_=am_grp[:],
-                    )
-                    nc.vector.quantize_mx(
-                        out=at_codes[:, g, b * SMALL : (b + 1) * SMALL].bitcast(FP8X4),
-                        scales=at_scales[:, g, b * SMALL : (b + 1) * SMALL],
-                        in_=at_grp[:].rearrange("p w j -> p (w j)"),
-                    )
-                    nc.vector.quantize_mx(
-                        out=ar_codes[:, g, b * SMALL : (b + 1) * SMALL].bitcast(FP8X4),
-                        scales=ar_scales[:, g, b * SMALL : (b + 1) * SMALL],
-                        in_=ar_grp[:].rearrange("p w j -> p (w j)"),
-                    )
-
-            quantise_chunk(0, 0, 0, 2)
-            quantise_chunk(0, 0, 1, 0)
-            small_inputs()
-            prepare_weights(0)
-            quantise_chunk(0, 1, 0, 2)
-            quantise_chunk(0, 1, 1, 0)
-            prepare_weights(1)
-
-            for step in range(O_TILES):
-                g, h = divmod(step, 2)
-                quantise_chunk(1, g, h, 1 if h == 0 else 0)
-                terms = small_terms(step, 0)
-                weighted_sums(step, 0, y_first[:, step, :], terms, psum, 2)
-                if step + 2 < O_TILES:
-                    prepare_weights(step + 2)
+            for sg in range(4):
+                load(sg)
+            regroup(0)
+            regroup(1)
+            load_weights(0)
+            for sg in range(STEPS):
+                c, mm = divmod(sg, 2)
+                if sg + 4 < STEPS:
+                    load(sg + 4)
+                turn(sg)
+                if sg + 2 < STEPS:
+                    regroup(sg + 2)
+                if mm == 0:
+                    quantise_pairs(c)
+                    if c % 2 == 1:
+                        sum_over_m(c // 4, (c // 2) % 2)
+                if sg >= 1:
+                    means(sg - 1)
+                if sg >= 4 and sg % 4 == 0:
+                    finish((sg - 4) // 8, ((sg - 4) // 4) % 2)
+                if sg == 1:
+                    small_inputs()
+                if sg == 4:
+                    turn_gamma_beta()
+                unit = sg - STEPS // 2
+                if unit >= 0:
+                    ot, hm = divmod(unit, 2)
+                    if hm == 0:
+                        small_terms(ot, 0, psum_mix)
+                    weighted_sum(ot, 0, hm, y_first[:, ot, :], psum, 2)
+                if unit >= 1:
+                    ot, hm = divmod(unit - 1, 2)
+                    relu_and_sums(ot, 0, hm, y_first[:, ot, :])
+                if sg >= 2:
+                    ot, part = divmod(sg - 2, 3)
+                    if ot < O_TILES and part < 2:
+                        turn_weights(ot, part)
+                    if ot < O_TILES and part == 1:
+                        quantise_weights(ot)
+                        if ot + 1 < O_TILES:
+                            load_weights(ot + 1)
+            means(STEPS - 1)
+            finish(1, 1)
 
         with ExitStack() as second:
             late = second.enter_context(tc.tile_pool(name="late", bufs=3))
-            psum = second.enter_context(tc.psum_pool(name="psum_late", bufs=6))
+            psum = second.enter_context(tc.psum_pool(name="psum_late", bufs=1))
+            y_second_of = {}
+            affine_of = {}
 
-            terms = small_terms(0, 1)
-            for ot in range(O_TILES):
-                o_cols = slice(ot * P, (ot + 1) * P)
-                y_second = late.tile([P, POS], F32)
-                weighted_sums(ot, 1, y_second[:], terms, psum, 6)
-                if ot + 1 < O_TILES:
-                    terms = small_terms(ot + 1, 1)
-
+            def statistics(ot):
                 total = work.tile([P, 2], F32)
                 nc.vector.tensor_reduce(
                     out=total[:], in_=sums[:, ot, :, :], axis=AXIS_X, op=ALU.add
@@ -382,7 +457,12 @@ def tile_layer_3d_dep_pa_kernel(tc, A, P1, P2, P3, P4, a5, gamma, beta, out):
                     out=shift[:], in0=gamma_beta[:, O_TILES + ot : O_TILES + ot + 1],
                     in1=mean_gain[:], op=ALU.subtract,
                 )
+                affine_of[ot] = (gain, shift)
 
+            def normalise_and_store(ot):
+                gain, shift = affine_of[ot]
+                o_cols = slice(ot * P, (ot + 1) * P)
+                y_second = y_second_of[ot]
                 for hm in range(2):
                     half = slice(hm * HALF, (hm + 1) * HALF)
                     nc.gpsimd.tensor_scalar(
@@ -395,3 +475,23 @@ def tile_layer_3d_dep_pa_kernel(tc, A, P1, P2, P3, P4, a5, gamma, beta, out):
                         scale=gain[:], bias=shift[:],
                     )
                     nc.sync.dma_start(out=out_rows[1, o_cols, half], in_=y_second[:, half])
+
+            small_terms(0, 1, psum_mix)
+            for unit in range(2 * O_TILES + 2):
+                ot, hm = divmod(unit, 2)
+                if ot < O_TILES:
+                    if hm == 0:
+                        y_second = late.tile([P, POS], F32)
+                        y_second_of[ot] = y_second
+                    if hm == 1 and ot + 1 < O_TILES:
+                        small_terms(ot + 1, 1, psum if ot % 2 == 0 else psum_mix)
+                    weighted_sum(ot, 1, hm, y_second_of[ot][:], psum, 4)
+                if unit == 0:
+                    relu_and_sums(O_TILES - 1, 0, 1, y_first[:, O_TILES - 1, :])
+                elif unit <= 2 * O_TILES:
+                    ot, hm = divmod(unit - 1, 2)
+                    relu_and_sums(ot, 1, hm, y_second_of[ot][:])
+                    if hm == 1:
+                        statistics(ot)
+                if unit >= 3 and unit % 2 == 1:
+                    normalise_and_store((unit - 3) // 2)

@@ -30,6 +30,10 @@ PER_TILE = TILE_POS // NT
 TP = NT // 2
 N_W = 4
 STEPS = B * PASSES * M
+N_UNITS = 2 * B * O_TILES
+COUNT = B * POS
+ROOT_COUNT = 64.0
+assert ROOT_COUNT * ROOT_COUNT == COUNT
 UNITS = 2 * B
 
 FLOPS = 2 * O * C * B * (POS + SLAB + 2 * SMALL)
@@ -59,7 +63,8 @@ def tile_layer_3d_dep_pa_kernel(tc, A, P1, P2, P3, P4, a5, gamma, beta, out):
         w_scales = keep.tile([P, O_TILES, N_W * PASSES, P], U8, align_bytes=64)
 
         y_first = keep.tile([P, O_TILES, POS], F32)
-        sums = keep.tile([P, O_TILES, 2, UNITS], F32)
+        sums = keep.tile([P, O_TILES, 2, UNITS + 1], F32)
+        gamma_pair = keep.tile([P, O_TILES, 2], F32)
 
         ident_f32 = keep.tile([P, P], F32)
         make_identity(nc, ident_f32[:])
@@ -88,6 +93,10 @@ def tile_layer_3d_dep_pa_kernel(tc, A, P1, P2, P3, P4, a5, gamma, beta, out):
 
         minus_half = keep.tile([P, 1], F32)
         nc.gpsimd.memset(minus_half[:], -0.5)
+        nc.vector.memset(sums[:, :, :, UNITS], 0.0)
+        nc.vector.tensor_scalar_add(
+            out=sums[:, :, 1, UNITS], in0=sums[:, :, 1, UNITS], scalar1=BN_EPS * COUNT * COUNT
+        )
 
         gb_rows = keep.tile([P, P], BF16)
         nc.vector.memset(gb_rows[:], 0.0)
@@ -107,11 +116,20 @@ def tile_layer_3d_dep_pa_kernel(tc, A, P1, P2, P3, P4, a5, gamma, beta, out):
                     stop=(g == PASSES - 1),
                 )
 
-        terms_of = {}
+        a43_of = {}
+        a2_of = {}
+        along_r_of = {}
+        y_of = {}
 
-        def small_terms(ot, b, small_pool):
+        def where(n):
+            stage, hm = divmod(n, 2)
+            b, ot = divmod(stage, O_TILES)
+            return stage, b, ot, hm
+
+        def mix_pooled(stage):
+            b, ot = divmod(stage, O_TILES)
             mine = slice(b * SMALL, (b + 1) * SMALL)
-            a43_ps = small_pool.tile([P, 2, SMALL], F32, bufs=1)
+            a43_ps = psum_mix.tile([P, 2, SMALL], F32, bufs=2)
             mix(a43_ps[:, 0, :], ot, 3, ar_codes[:, :, mine], ar_scales[:, :, mine])
             mix(a43_ps[:, 1, :], ot, 2, at_codes[:, :, mine], at_scales[:, :, mine])
             along_r = work.tile([P, SMALL], F32)
@@ -119,16 +137,19 @@ def tile_layer_3d_dep_pa_kernel(tc, A, P1, P2, P3, P4, a5, gamma, beta, out):
                 out=along_r[:], in0=a43_ps[:, 0, :], scalar=0.5, in1=a5_twice[:, ot, b, :],
                 op0=ALU.mult, op1=ALU.add,
             )
-            along_t = work.tile([P, SMALL], F32)
-            nc.scalar.activation(out=along_t[:], in_=a43_ps[:, 1, :], func=ACT.Copy, scale=0.1)
-            a2_ps = small_pool.tile([P, SLAB], F32, bufs=1)
+            a43_of[stage] = a43_ps
+            along_r_of[stage] = along_r
+
+        def mix_over_m(stage):
+            b, ot = divmod(stage, O_TILES)
+            a2_ps = psum_mix.tile([P, SLAB], F32, bufs=1)
             b_slab = slice(b * SLAB, (b + 1) * SLAB)
             mix(a2_ps[:], ot, 1, am_codes[:, :, b_slab], am_scales[:, :, b_slab])
-            terms_of[(ot, b)] = (along_r, along_t, a2_ps)
+            a2_of[stage] = a2_ps
 
-        def weighted_sum(ot, b, hm, y, a1_pool, a1_bufs):
-            along_r, along_t, a2_ps = terms_of[(ot, b)]
-            half = slice(hm * HALF, (hm + 1) * HALF)
+        def add_along_r(n, a1_pool, a1_bufs):
+            stage, b, ot, hm = where(n)
+            y = y_of[stage]
             for mm in range(2):
                 m = 2 * hm + mm
                 slab = slice(m * SLAB, (m + 1) * SLAB)
@@ -137,41 +158,81 @@ def tile_layer_3d_dep_pa_kernel(tc, A, P1, P2, P3, P4, a5, gamma, beta, out):
                 nc.vector.tensor_tensor(
                     out=y[:, slab].rearrange("o (k r t) -> o k r t", r=NR, t=NT),
                     in0=a1_ps[:].rearrange("o (k r t) -> o k r t", r=NR, t=NT),
-                    in1=along_r[:, m * K * NT : (m + 1) * K * NT]
+                    in1=along_r_of[stage][:, m * K * NT : (m + 1) * K * NT]
                     .rearrange("o (k t) -> o k t", t=NT)
                     .unsqueeze(2)
                     .to_broadcast([P, K, NR, NT]),
                     op=ALU.add,
                 )
+
+        def add_along_m(n):
+            stage, b, ot, hm = where(n)
+            half = y_of[stage][:, hm * HALF : (hm + 1) * HALF].rearrange("o (m x) -> o m x", m=2)
             nc.vector.scalar_tensor_tensor(
-                out=y[:, half].rearrange("o (m x) -> o m x", m=2),
-                in0=a2_ps[:].unsqueeze(1).to_broadcast([P, 2, SLAB]),
-                scalar=0.1 / M,
-                in1=y[:, half].rearrange("o (m x) -> o m x", m=2),
-                op0=ALU.mult,
-                op1=ALU.add,
-            )
-            nc.vector.tensor_tensor(
-                out=y[:, half].rearrange("o (x t) -> o x t", t=NT),
-                in0=y[:, half].rearrange("o (x t) -> o x t", t=NT),
-                in1=along_t[:, hm * (SMALL // 2) : (hm + 1) * (SMALL // 2)]
-                .unsqueeze(2)
-                .to_broadcast([P, SMALL // 2, NT]),
-                op=ALU.add,
+                out=half, in0=a2_of[stage][:].unsqueeze(1).to_broadcast([P, 2, SLAB]),
+                scalar=0.1 / M, in1=half, op0=ALU.mult, op1=ALU.add,
             )
 
-        def relu_and_sums(ot, b, hm, y):
-            half = slice(hm * HALF, (hm + 1) * HALF)
-            unit = 2 * b + hm
-            nc.scalar.activation(
-                out=y[:, half], in_=y[:, half], func=ACT.Relu,
-                accum_out=sums[:, ot, 0, unit : unit + 1],
+        def add_along_t(n):
+            stage, b, ot, hm = where(n)
+            half = y_of[stage][:, hm * HALF : (hm + 1) * HALF].rearrange("o (x t) -> o x t", t=NT)
+            nc.vector.scalar_tensor_tensor(
+                out=half,
+                in0=a43_of[stage][:, 1, hm * (SMALL // 2) : (hm + 1) * (SMALL // 2)]
+                .unsqueeze(2)
+                .to_broadcast([P, SMALL // 2, NT]),
+                scalar=0.1, in1=half, op0=ALU.mult, op1=ALU.add,
             )
+
+        def relu(n):
+            stage, b, ot, hm = where(n)
+            half = y_of[stage][:, hm * HALF : (hm + 1) * HALF]
+            nc.scalar.activation(
+                out=half, in_=half, func=ACT.Relu,
+                accum_out=sums[:, ot, 0, 2 * b + hm : 2 * b + hm + 1],
+            )
+
+        def square(n):
+            stage, b, ot, hm = where(n)
             squares = work.tile([P, HALF], BF16)
             nc.scalar.activation(
-                out=squares[:], in_=y[:, half], func=ACT.Square,
-                accum_out=sums[:, ot, 1, unit : unit + 1],
+                out=squares[:], in_=y_of[stage][:, hm * HALF : (hm + 1) * HALF], func=ACT.Square,
+                scale=ROOT_COUNT,
+                accum_out=sums[:, ot, 1, 2 * b + hm : 2 * b + hm + 1],
             )
+
+        relus = []
+
+        def relus_up_to(n, after_square):
+            if n is None:
+                return
+            for unit in range(len(relus), min(n, N_UNITS) + 1):
+                if unit >= 1:
+                    square(unit - 1)
+                    after_square(unit - 1)
+                if unit < N_UNITS:
+                    relu(unit)
+                relus.append(unit)
+
+        def nothing(unit):
+            return
+
+        def begun(step):
+            n = step if step < N_UNITS // 2 else step - 1
+            return n if step != N_UNITS // 2 and 0 <= n < N_UNITS else None
+
+        def unit_step(step, a1_pool, a1_bufs):
+            n = begun(step)
+            if n is not None and n % 2 == 0:
+                mix_pooled(n // 2)
+            if begun(step - 1) is not None:
+                add_along_m(begun(step - 1))
+            if n is not None and n % 2 == 0:
+                mix_over_m(n // 2)
+            if n is not None:
+                add_along_r(n, a1_pool, a1_bufs)
+            if begun(step - 2) is not None:
+                add_along_t(begun(step - 2))
 
         with ExitStack() as first:
             stage = first.enter_context(tc.tile_pool(name="stage", bufs=2))
@@ -182,6 +243,7 @@ def tile_layer_3d_dep_pa_kernel(tc, A, P1, P2, P3, P4, a5, gamma, beta, out):
             flipped_of = {}
             means_of = {}
             pairs_of = {}
+            am_of = {}
             w_raw_of = {}
             w_grp_of = {}
 
@@ -239,11 +301,7 @@ def tile_layer_3d_dep_pa_kernel(tc, A, P1, P2, P3, P4, a5, gamma, beta, out):
                 nc.vector.tensor_tensor(
                     out=am_grp[:], in0=pairs[0][:], in1=pairs[1][:], op=ALU.add
                 )
-                nc.vector.quantize_mx(
-                    out=am_codes[:, g, b * SLAB : (b + 1) * SLAB].bitcast(FP8X4),
-                    scales=am_scales[:, g, b * SLAB : (b + 1) * SLAB],
-                    in_=am_grp[:],
-                )
+                am_of[(b, g)] = am_grp
 
             def turn(sg):
                 raw_words = raw_of[sg][:].bitcast(F32)
@@ -267,7 +325,7 @@ def tile_layer_3d_dep_pa_kernel(tc, A, P1, P2, P3, P4, a5, gamma, beta, out):
                     ar_grp = stage.tile([P, SMALL, PACK], BF16, align_bytes=64)
                     means_of[(b, g)] = (at_grp, ar_grp)
                 at_grp, ar_grp = means_of[(b, g)]
-                mean_ps = psum.tile([P, PACK, TILES, 2 * PER_TILE], F32)
+                mean_ps = psum.tile([P, PACK, TILES, 2 * PER_TILE], F32, bufs=1)
                 for tl in range(TILES):
                     halves = (
                         flipped_of[sg][tl][:]
@@ -297,6 +355,12 @@ def tile_layer_3d_dep_pa_kernel(tc, A, P1, P2, P3, P4, a5, gamma, beta, out):
 
             def finish(b, g):
                 at_grp, ar_grp = means_of[(b, g)]
+                am_grp = am_of[(b, g)]
+                nc.vector.quantize_mx(
+                    out=am_codes[:, g, b * SLAB : (b + 1) * SLAB].bitcast(FP8X4),
+                    scales=am_scales[:, g, b * SLAB : (b + 1) * SLAB],
+                    in_=am_grp[:],
+                )
                 nc.vector.quantize_mx(
                     out=at_codes[:, g, b * SMALL : (b + 1) * SMALL].bitcast(FP8X4),
                     scales=at_scales[:, g, b * SMALL : (b + 1) * SMALL],
@@ -329,6 +393,12 @@ def tile_layer_3d_dep_pa_kernel(tc, A, P1, P2, P3, P4, a5, gamma, beta, out):
                 gb_ps = psum.tile([P, P], BF16, tag="turned")
                 nc.tensor.transpose(out=gb_ps[:], in_=gb_rows[:], identity=ident_bf[:])
                 nc.vector.tensor_copy(out=gamma_beta[:], in_=gb_ps[:, 0 : 2 * O_TILES])
+                nc.vector.tensor_scalar_mul(
+                    out=gamma_pair[:, :, 0], in0=gamma_beta[:, 0:O_TILES], scalar1=1.0 * COUNT
+                )
+                nc.vector.tensor_scalar_mul(
+                    out=gamma_pair[:, :, 1], in0=gamma_beta[:, 0:O_TILES], scalar1=-1.0
+                )
 
             def load_weights(ot):
                 w_raw = stage.tile([P, N_W * C], BF16, bufs=2)
@@ -370,6 +440,8 @@ def tile_layer_3d_dep_pa_kernel(tc, A, P1, P2, P3, P4, a5, gamma, beta, out):
                     in_=w_grp_of[ot][:],
                 )
 
+            for ot in range(O_TILES):
+                y_of[ot] = y_first[:, ot, :]
             for sg in range(4):
                 load(sg)
             regroup(0)
@@ -384,8 +456,8 @@ def tile_layer_3d_dep_pa_kernel(tc, A, P1, P2, P3, P4, a5, gamma, beta, out):
                     regroup(sg + 2)
                 if mm == 0:
                     quantise_pairs(c)
-                    if c % 2 == 1:
-                        sum_over_m(c // 4, (c // 2) % 2)
+                if sg % 4 == 3:
+                    sum_over_m(sg // 8, (sg // 4) % 2)
                 if sg >= 1:
                     means(sg - 1)
                 if sg >= 4 and sg % 4 == 0:
@@ -394,15 +466,9 @@ def tile_layer_3d_dep_pa_kernel(tc, A, P1, P2, P3, P4, a5, gamma, beta, out):
                     small_inputs()
                 if sg == 4:
                     turn_gamma_beta()
-                unit = sg - STEPS // 2
-                if unit >= 0:
-                    ot, hm = divmod(unit, 2)
-                    if hm == 0:
-                        small_terms(ot, 0, psum_mix)
-                    weighted_sum(ot, 0, hm, y_first[:, ot, :], psum, 2)
-                if unit >= 1:
-                    ot, hm = divmod(unit - 1, 2)
-                    relu_and_sums(ot, 0, hm, y_first[:, ot, :])
+                if sg >= STEPS // 2:
+                    unit_step(sg - STEPS // 2, psum, 2)
+                    relus_up_to(begun(sg - STEPS // 2 - 3), nothing)
                 if sg >= 2:
                     ot, part = divmod(sg - 2, 3)
                     if ot < O_TILES and part < 2:
@@ -412,12 +478,13 @@ def tile_layer_3d_dep_pa_kernel(tc, A, P1, P2, P3, P4, a5, gamma, beta, out):
                         if ot + 1 < O_TILES:
                             load_weights(ot + 1)
             means(STEPS - 1)
+            unit_step(N_UNITS // 2, psum, 2)
+            relus_up_to(begun(N_UNITS // 2 - 3), nothing)
             finish(1, 1)
 
         with ExitStack() as second:
-            late = second.enter_context(tc.tile_pool(name="late", bufs=3))
-            psum = second.enter_context(tc.psum_pool(name="psum_late", bufs=1))
-            y_second_of = {}
+            late = second.enter_context(tc.tile_pool(name="late", bufs=4))
+            psum = second.enter_context(tc.psum_pool(name="psum_late", bufs=5))
             affine_of = {}
 
             def statistics(ot):
@@ -425,73 +492,63 @@ def tile_layer_3d_dep_pa_kernel(tc, A, P1, P2, P3, P4, a5, gamma, beta, out):
                 nc.vector.tensor_reduce(
                     out=total[:], in_=sums[:, ot, :, :], axis=AXIS_X, op=ALU.add
                 )
-                moments = work.tile([P, 2], F32)
+                minus_spread = work.tile([P, 1], F32)
+                nc.vector.scalar_tensor_tensor(
+                    out=minus_spread[:], in0=total[:, 0:1], scalar=total[:, 0:1],
+                    in1=total[:, 1:2], op0=ALU.mult, op1=ALU.subtract,
+                )
+                spread = work.tile([P, 1], F32)
+                nc.vector.tensor_scalar(
+                    out=spread[:], in0=minus_spread[:], scalar1=-1.0,
+                    scalar2=BN_EPS * COUNT * COUNT, op0=ALU.mult, op1=ALU.max,
+                )
+                w = work.tile([P, 1], F32)
+                nc.gpsimd.tensor_tensor(out=w[:], in0=spread[:], in1=minus_half[:], op=ALU.pow)
+                gains = work.tile([P, 2], F32)
+                nc.gpsimd.tensor_tensor(
+                    out=gains[:], in0=gamma_pair[:, ot, :], in1=w[:].to_broadcast([P, 2]),
+                    op=ALU.mult,
+                )
+                shift = work.tile([P, 1], F32)
                 nc.gpsimd.tensor_scalar(
-                    out=moments[:], in0=total[:], scalar1=1.0 / (B * POS), scalar2=0.0,
+                    out=shift[:], in0=total[:, 0:1], scalar1=gains[:, 1:2],
+                    scalar2=gamma_beta[:, O_TILES + ot : O_TILES + ot + 1],
                     op0=ALU.mult, op1=ALU.add,
                 )
-                mean = moments[:, 0:1]
-                mean_sq = work.tile([P, 1], F32)
-                nc.gpsimd.tensor_tensor(out=mean_sq[:], in0=mean, in1=mean, op=ALU.mult)
-                var = work.tile([P, 1], F32)
-                nc.gpsimd.tensor_tensor(
-                    out=var[:], in0=moments[:, 1:2], in1=mean_sq[:], op=ALU.subtract
-                )
-                var_eps = work.tile([P, 1], F32)
-                nc.gpsimd.tensor_scalar(
-                    out=var_eps[:], in0=var[:], scalar1=0.0, scalar2=BN_EPS,
-                    op0=ALU.max, op1=ALU.add,
-                )
-                rstd = work.tile([P, 1], F32)
-                nc.gpsimd.tensor_tensor(
-                    out=rstd[:], in0=var_eps[:], in1=minus_half[:], op=ALU.pow
-                )
-                gain = work.tile([P, 1], F32)
-                nc.gpsimd.tensor_tensor(
-                    out=gain[:], in0=gamma_beta[:, ot : ot + 1], in1=rstd[:], op=ALU.mult
-                )
-                mean_gain = work.tile([P, 1], F32)
-                nc.gpsimd.tensor_tensor(out=mean_gain[:], in0=mean, in1=gain[:], op=ALU.mult)
-                shift = work.tile([P, 1], F32)
-                nc.gpsimd.tensor_tensor(
-                    out=shift[:], in0=gamma_beta[:, O_TILES + ot : O_TILES + ot + 1],
-                    in1=mean_gain[:], op=ALU.subtract,
-                )
-                affine_of[ot] = (gain, shift)
+                affine_of[ot] = (gains[:, 0:1], shift[:])
 
-            def normalise_and_store(ot):
+            def normalise_and_store(ot, b):
                 gain, shift = affine_of[ot]
-                o_cols = slice(ot * P, (ot + 1) * P)
-                y_second = y_second_of[ot]
+                y = y_of[b * O_TILES + ot]
+                on_vector = ot + b == O_TILES - 1 and ot >= O_TILES - 2
                 for hm in range(2):
                     half = slice(hm * HALF, (hm + 1) * HALF)
-                    nc.gpsimd.tensor_scalar(
-                        out=y_first[:, ot, half], in0=y_first[:, ot, half],
-                        scalar1=gain[:], scalar2=shift[:], op0=ALU.mult, op1=ALU.add,
-                    )
-                    nc.sync.dma_start(out=out_rows[0, o_cols, half], in_=y_first[:, ot, half])
-                    nc.scalar.activation(
-                        out=y_second[:, half], in_=y_second[:, half], func=ACT.Identity,
-                        scale=gain[:], bias=shift[:],
-                    )
-                    nc.sync.dma_start(out=out_rows[1, o_cols, half], in_=y_second[:, half])
+                    if b == 1 and not on_vector:
+                        nc.scalar.activation(
+                            out=y[:, half], in_=y[:, half], func=ACT.Identity,
+                            scale=gain, bias=shift,
+                        )
+                    else:
+                        engine = nc.vector if on_vector else nc.gpsimd
+                        engine.tensor_scalar(
+                            out=y[:, half], in0=y[:, half],
+                            scalar1=gain, scalar2=shift, op0=ALU.mult, op1=ALU.add,
+                        )
+                    nc.sync.dma_start(out=out_rows[b, ot * P : (ot + 1) * P, half], in_=y[:, half])
 
-            small_terms(0, 1, psum_mix)
-            for unit in range(2 * O_TILES + 2):
-                ot, hm = divmod(unit, 2)
-                if ot < O_TILES:
-                    if hm == 0:
-                        y_second = late.tile([P, POS], F32)
-                        y_second_of[ot] = y_second
-                    if hm == 1 and ot + 1 < O_TILES:
-                        small_terms(ot + 1, 1, psum if ot % 2 == 0 else psum_mix)
-                    weighted_sum(ot, 1, hm, y_second_of[ot][:], psum, 4)
-                if unit == 0:
-                    relu_and_sums(O_TILES - 1, 0, 1, y_first[:, O_TILES - 1, :])
-                elif unit <= 2 * O_TILES:
-                    ot, hm = divmod(unit - 1, 2)
-                    relu_and_sums(ot, 1, hm, y_second_of[ot][:])
-                    if hm == 1:
-                        statistics(ot)
-                if unit >= 3 and unit % 2 == 1:
-                    normalise_and_store((unit - 3) // 2)
+            def after_square(unit):
+                stage, b, ot, hm = where(unit)
+                if b == 1 and hm == 0 and ot >= 1:
+                    normalise_and_store(ot - 1, 1)
+                if b == 1 and hm == 1:
+                    statistics(ot)
+                    normalise_and_store(ot, 0)
+
+            for step in range(N_UNITS // 2 + 1, N_UNITS + 4):
+                n = begun(step)
+                if n is not None and n % 2 == 0:
+                    y_second = late.tile([P, POS], F32)
+                    y_of[n // 2] = y_second[:]
+                unit_step(step, psum, 5)
+                relus_up_to(step - 3, after_square)
+            normalise_and_store(O_TILES - 1, 1)

@@ -29,6 +29,10 @@ TILES = SLAB // TILE_POS
 PER_TILE = TILE_POS // NT
 TP = NT // 2
 N_W = 4
+TEN = 10.0
+SLOT_8P1, SLOT_2P1, SLOT_P2, SLOT_P3, SLOT_P4 = 0, 2, 4, 6, 8
+N_SLOTS = 10
+SLOT_COLS = PASSES * P * PACK
 STEPS = B * PASSES * M
 N_UNITS = 2 * B * O_TILES
 COUNT = B * POS
@@ -59,8 +63,8 @@ def tile_layer_3d_dep_pa_kernel(tc, A, P1, P2, P3, P4, a5, gamma, beta, out):
         at_scales = keep.tile([P, PASSES, B * SMALL], U8, align_bytes=64)
         ar_codes = keep.tile([P, PASSES, B * SMALL], U32, align_bytes=64)
         ar_scales = keep.tile([P, PASSES, B * SMALL], U8, align_bytes=64)
-        w_codes = keep.tile([P, O_TILES, N_W * PASSES, P], U32, align_bytes=64)
-        w_scales = keep.tile([P, O_TILES, N_W * PASSES, P], U8, align_bytes=64)
+        w_codes = keep.tile([P, O_TILES, N_SLOTS, P], U32, align_bytes=64)
+        w_scales = keep.tile([P, O_TILES, N_SLOTS, P], U8, align_bytes=64)
 
         y_first = keep.tile([P, O_TILES, POS], F32)
         sums = keep.tile([P, O_TILES, 2, UNITS + 1], F32)
@@ -95,29 +99,29 @@ def tile_layer_3d_dep_pa_kernel(tc, A, P1, P2, P3, P4, a5, gamma, beta, out):
         nc.gpsimd.memset(minus_half[:], -0.5)
         nc.vector.memset(sums[:, :, :, UNITS], 0.0)
         nc.vector.tensor_scalar_add(
-            out=sums[:, :, 1, UNITS], in0=sums[:, :, 1, UNITS], scalar1=BN_EPS * COUNT * COUNT
+            out=sums[:, :, 1, UNITS], in0=sums[:, :, 1, UNITS],
+            scalar1=BN_EPS * TEN * TEN * COUNT * COUNT,
         )
 
         gb_rows = keep.tile([P, P], BF16)
         nc.vector.memset(gb_rows[:], 0.0)
         gamma_beta = keep.tile([P, 2 * O_TILES], F32)
         a5_sb = keep.tile([P, O_TILES, B, SMALL], BF16)
-        a5_twice = keep.tile([P, O_TILES, B, SMALL], BF16)
+        a5_scaled = keep.tile([P, O_TILES, B, SMALL], F32)
 
-        def mix(acc, ot, which, x_codes, x_scales):
-            for g in range(PASSES):
+        def passes(acc, ot, operands):
+            for i, (slot, x_codes, x_scales) in enumerate(operands):
                 nc.tensor.matmul_mx(
                     out=acc,
-                    lhsT=w_codes[:, ot, which * PASSES + g, :].bitcast(FP8X4),
-                    lhsT_scale=w_scales[:, ot, which * PASSES + g, :],
-                    rhs=x_codes[:, g, :].bitcast(FP8X4),
-                    rhs_scale=x_scales[:, g, :],
-                    start=(g == 0),
-                    stop=(g == PASSES - 1),
+                    lhsT=w_codes[:, ot, slot, :].bitcast(FP8X4),
+                    lhsT_scale=w_scales[:, ot, slot, :],
+                    rhs=x_codes.bitcast(FP8X4),
+                    rhs_scale=x_scales,
+                    start=(i == 0),
+                    stop=(i == len(operands) - 1),
                 )
 
         a43_of = {}
-        a2_of = {}
         along_r_of = {}
         y_of = {}
 
@@ -130,31 +134,36 @@ def tile_layer_3d_dep_pa_kernel(tc, A, P1, P2, P3, P4, a5, gamma, beta, out):
             b, ot = divmod(stage, O_TILES)
             mine = slice(b * SMALL, (b + 1) * SMALL)
             a43_ps = psum_mix.tile([P, 2, SMALL], F32, bufs=2)
-            mix(a43_ps[:, 0, :], ot, 3, ar_codes[:, :, mine], ar_scales[:, :, mine])
-            mix(a43_ps[:, 1, :], ot, 2, at_codes[:, :, mine], at_scales[:, :, mine])
+            passes(
+                a43_ps[:, 0, :], ot,
+                [(SLOT_P4 + g, ar_codes[:, g, mine], ar_scales[:, g, mine]) for g in range(PASSES)],
+            )
+            passes(
+                a43_ps[:, 1, :], ot,
+                [(SLOT_P3 + g, at_codes[:, g, mine], at_scales[:, g, mine]) for g in range(PASSES)],
+            )
             along_r = work.tile([P, SMALL], F32)
             nc.vector.scalar_tensor_tensor(
-                out=along_r[:], in0=a43_ps[:, 0, :], scalar=0.5, in1=a5_twice[:, ot, b, :],
+                out=along_r[:], in0=a43_ps[:, 0, :], scalar=0.5 * TEN, in1=a5_scaled[:, ot, b, :],
                 op0=ALU.mult, op1=ALU.add,
             )
             a43_of[stage] = a43_ps
             along_r_of[stage] = along_r
 
-        def mix_over_m(stage):
-            b, ot = divmod(stage, O_TILES)
-            a2_ps = psum_mix.tile([P, SLAB], F32, bufs=1)
-            b_slab = slice(b * SLAB, (b + 1) * SLAB)
-            mix(a2_ps[:], ot, 1, am_codes[:, :, b_slab], am_scales[:, :, b_slab])
-            a2_of[stage] = a2_ps
-
         def add_along_r(n, a1_pool, a1_bufs):
             stage, b, ot, hm = where(n)
             y = y_of[stage]
+            b_slab = slice(b * SLAB, (b + 1) * SLAB)
             for mm in range(2):
                 m = 2 * hm + mm
                 slab = slice(m * SLAB, (m + 1) * SLAB)
                 a1_ps = a1_pool.tile([P, SLAB], F32, bufs=a1_bufs)
-                mix(a1_ps[:], ot, 0, a_codes[:, :, b, slab], a_scales[:, :, b, slab])
+                passes(
+                    a1_ps[:], ot,
+                    [(SLOT_8P1 + g, a_codes[:, g, b, slab], a_scales[:, g, b, slab]) for g in range(PASSES)]
+                    + [(SLOT_2P1 + g, a_codes[:, g, b, slab], a_scales[:, g, b, slab]) for g in range(PASSES)]
+                    + [(SLOT_P2 + g, am_codes[:, g, b_slab], am_scales[:, g, b_slab]) for g in range(PASSES)],
+                )
                 nc.vector.tensor_tensor(
                     out=y[:, slab].rearrange("o (k r t) -> o k r t", r=NR, t=NT),
                     in0=a1_ps[:].rearrange("o (k r t) -> o k r t", r=NR, t=NT),
@@ -165,23 +174,15 @@ def tile_layer_3d_dep_pa_kernel(tc, A, P1, P2, P3, P4, a5, gamma, beta, out):
                     op=ALU.add,
                 )
 
-        def add_along_m(n):
-            stage, b, ot, hm = where(n)
-            half = y_of[stage][:, hm * HALF : (hm + 1) * HALF].rearrange("o (m x) -> o m x", m=2)
-            nc.vector.scalar_tensor_tensor(
-                out=half, in0=a2_of[stage][:].unsqueeze(1).to_broadcast([P, 2, SLAB]),
-                scalar=0.1 / M, in1=half, op0=ALU.mult, op1=ALU.add,
-            )
-
         def add_along_t(n):
             stage, b, ot, hm = where(n)
             half = y_of[stage][:, hm * HALF : (hm + 1) * HALF].rearrange("o (x t) -> o x t", t=NT)
-            nc.vector.scalar_tensor_tensor(
+            nc.vector.tensor_tensor(
                 out=half,
                 in0=a43_of[stage][:, 1, hm * (SMALL // 2) : (hm + 1) * (SMALL // 2)]
                 .unsqueeze(2)
                 .to_broadcast([P, SMALL // 2, NT]),
-                scalar=0.1, in1=half, op0=ALU.mult, op1=ALU.add,
+                in1=half, op=ALU.add,
             )
 
         def relu(n):
@@ -225,14 +226,10 @@ def tile_layer_3d_dep_pa_kernel(tc, A, P1, P2, P3, P4, a5, gamma, beta, out):
             n = begun(step)
             if n is not None and n % 2 == 0:
                 mix_pooled(n // 2)
-            if begun(step - 1) is not None:
-                add_along_m(begun(step - 1))
-            if n is not None and n % 2 == 0:
-                mix_over_m(n // 2)
             if n is not None:
                 add_along_r(n, a1_pool, a1_bufs)
-            if begun(step - 2) is not None:
-                add_along_t(begun(step - 2))
+            if begun(step - 1) is not None:
+                add_along_t(begun(step - 1))
 
         with ExitStack() as first:
             stage = first.enter_context(tc.tile_pool(name="stage", bufs=2))
@@ -246,6 +243,7 @@ def tile_layer_3d_dep_pa_kernel(tc, A, P1, P2, P3, P4, a5, gamma, beta, out):
             am_of = {}
             w_raw_of = {}
             w_grp_of = {}
+            w_plain_of = {}
 
             def place(sg):
                 c, mm = divmod(sg, 2)
@@ -384,9 +382,9 @@ def tile_layer_3d_dep_pa_kernel(tc, A, P1, P2, P3, P4, a5, gamma, beta, out):
                         out=a5_sb[:, :, b, :], in_=a5_rows[b].rearrange("(t o) x -> o t x", o=P)
                     )
                 nc.gpsimd.tensor_scalar(
-                    out=a5_twice[:].rearrange("o t b x -> o (t b x)"),
+                    out=a5_scaled[:].rearrange("o t b x -> o (t b x)"),
                     in0=a5_sb[:].rearrange("o t b x -> o (t b x)"),
-                    scalar1=2.0, scalar2=0.0, op0=ALU.mult, op1=ALU.add,
+                    scalar1=2.0 * TEN, scalar2=0.0, op0=ALU.mult, op1=ALU.add,
                 )
 
             def turn_gamma_beta():
@@ -401,7 +399,7 @@ def tile_layer_3d_dep_pa_kernel(tc, A, P1, P2, P3, P4, a5, gamma, beta, out):
                 )
 
             def load_weights(ot):
-                w_raw = stage.tile([P, N_W * C], BF16, bufs=2)
+                w_raw = stage.tile([P, N_W * C], BF16, bufs=1)
                 for which in range(N_W):
                     nc.sync.dma_start(
                         out=w_raw[:, which * C : (which + 1) * C],
@@ -411,15 +409,18 @@ def tile_layer_3d_dep_pa_kernel(tc, A, P1, P2, P3, P4, a5, gamma, beta, out):
 
             def turn_weights(ot, pair):
                 if pair == 0:
-                    w_grp = stage.tile([P, N_W * PASSES * P * PACK], BF16, bufs=1, align_bytes=64)
+                    w_plain = stage.tile([P, 2 * SLOT_COLS], BF16, bufs=1)
+                    w_grp = stage.tile([P, N_SLOTS * P * PACK], BF16, bufs=1, align_bytes=64)
+                    w_plain_of[ot] = w_plain
                     w_grp_of[ot] = w_grp
                 w_words = w_raw_of[ot][:].bitcast(F32).rearrange(
                     "o (w g p u) -> o w g p u", w=N_W, g=PASSES, u=2
                 )
-                w_grp_words = w_grp_of[ot][:].bitcast(F32).rearrange(
-                    "p (s o u) -> p s o u", s=N_W * PASSES, u=2
-                )
-                for which in (2 * pair, 2 * pair + 1):
+                target = w_plain_of[ot] if pair == 0 else w_grp_of[ot]
+                target_words = target[:].bitcast(F32).rearrange("p (s o u) -> p s o u", o=P, u=2)
+                for half in range(2):
+                    which = 2 * pair + half
+                    first_slot = half * PASSES if pair == 0 else SLOT_P3 + half * PASSES
                     wt_ps = psum.tile([P, PASSES, 2, P], F32, tag="turned")
                     for g in range(PASSES):
                         for u in range(2):
@@ -429,16 +430,26 @@ def tile_layer_3d_dep_pa_kernel(tc, A, P1, P2, P3, P4, a5, gamma, beta, out):
                                 identity=ident_f32[:],
                             )
                     nc.scalar.copy(
-                        out=w_grp_words[:, which * PASSES : (which + 1) * PASSES, :, :],
+                        out=target_words[:, first_slot : first_slot + PASSES, :, :],
                         in_=wt_ps[:].rearrange("p g u o -> p g o u"),
                     )
+                if pair == 0:
+                    for slot, source, factor in (
+                        (SLOT_8P1, 0, 8.0), (SLOT_2P1, 0, 2.0), (SLOT_P2, 1, 1.0 / M)
+                    ):
+                        nc.vector.tensor_scalar_mul(
+                            out=w_grp_of[ot][:, slot * P * PACK : slot * P * PACK + SLOT_COLS],
+                            in0=w_plain_of[ot][:, source * SLOT_COLS : (source + 1) * SLOT_COLS],
+                            scalar1=factor,
+                        )
 
             def quantise_weights(ot):
-                nc.vector.quantize_mx(
-                    out=w_codes[:, ot, :, :].rearrange("p s o -> p (s o)").bitcast(FP8X4),
-                    scales=w_scales[:, ot, :, :].rearrange("p s o -> p (s o)"),
-                    in_=w_grp_of[ot][:],
-                )
+                for first, last in ((0, SLOT_P4), (SLOT_P4, N_SLOTS)):
+                    nc.vector.quantize_mx(
+                        out=w_codes[:, ot, first:last, :].rearrange("p s o -> p (s o)").bitcast(FP8X4),
+                        scales=w_scales[:, ot, first:last, :].rearrange("p s o -> p (s o)"),
+                        in_=w_grp_of[ot][:, first * P * PACK : last * P * PACK],
+                    )
 
             for ot in range(O_TILES):
                 y_of[ot] = y_first[:, ot, :]
@@ -467,8 +478,8 @@ def tile_layer_3d_dep_pa_kernel(tc, A, P1, P2, P3, P4, a5, gamma, beta, out):
                 if sg == 4:
                     turn_gamma_beta()
                 if sg >= STEPS // 2:
-                    unit_step(sg - STEPS // 2, psum, 2)
-                    relus_up_to(begun(sg - STEPS // 2 - 3), nothing)
+                    unit_step(sg - STEPS // 2, psum, 3)
+                    relus_up_to(begun(sg - STEPS // 2 - 2), nothing)
                 if sg >= 2:
                     ot, part = divmod(sg - 2, 3)
                     if ot < O_TILES and part < 2:
@@ -478,13 +489,13 @@ def tile_layer_3d_dep_pa_kernel(tc, A, P1, P2, P3, P4, a5, gamma, beta, out):
                         if ot + 1 < O_TILES:
                             load_weights(ot + 1)
             means(STEPS - 1)
-            unit_step(N_UNITS // 2, psum, 2)
-            relus_up_to(begun(N_UNITS // 2 - 3), nothing)
+            unit_step(N_UNITS // 2, psum, 3)
+            relus_up_to(begun(N_UNITS // 2 - 2), nothing)
             finish(1, 1)
 
         with ExitStack() as second:
             late = second.enter_context(tc.tile_pool(name="late", bufs=4))
-            psum = second.enter_context(tc.psum_pool(name="psum_late", bufs=5))
+            psum = second.enter_context(tc.psum_pool(name="psum_late", bufs=6))
             affine_of = {}
 
             def statistics(ot):
@@ -500,7 +511,7 @@ def tile_layer_3d_dep_pa_kernel(tc, A, P1, P2, P3, P4, a5, gamma, beta, out):
                 spread = work.tile([P, 1], F32)
                 nc.vector.tensor_scalar(
                     out=spread[:], in0=minus_spread[:], scalar1=-1.0,
-                    scalar2=BN_EPS * COUNT * COUNT, op0=ALU.mult, op1=ALU.max,
+                    scalar2=BN_EPS * TEN * TEN * COUNT * COUNT, op0=ALU.mult, op1=ALU.max,
                 )
                 w = work.tile([P, 1], F32)
                 nc.gpsimd.tensor_tensor(out=w[:], in0=spread[:], in1=minus_half[:], op=ALU.pow)
@@ -544,11 +555,11 @@ def tile_layer_3d_dep_pa_kernel(tc, A, P1, P2, P3, P4, a5, gamma, beta, out):
                     statistics(ot)
                     normalise_and_store(ot, 0)
 
-            for step in range(N_UNITS // 2 + 1, N_UNITS + 4):
+            for step in range(N_UNITS // 2 + 1, N_UNITS + 3):
                 n = begun(step)
                 if n is not None and n % 2 == 0:
                     y_second = late.tile([P, POS], F32)
                     y_of[n // 2] = y_second[:]
-                unit_step(step, psum, 5)
-                relus_up_to(step - 3, after_square)
+                unit_step(step, psum, 6)
+                relus_up_to(step - 2, after_square)
             normalise_and_store(O_TILES - 1, 1)

@@ -26,11 +26,14 @@ SMALL = M * K * NT
 O_TILES = O // P
 TILE_POS = 2 * P
 TILES = SLAB // TILE_POS
+POS_K = NR * NT
+STEP_K = TILES
+CHUNK_K = 2 * STEP_K
 PER_TILE = TILE_POS // NT
 TP = NT // 2
 N_W = 4
-TEN = 10.0
-SLOT_8P1, SLOT_2P1, SLOT_P2, SLOT_P3, SLOT_P4 = 0, 2, 4, 6, 8
+FORTY = 40.0
+SLOT_32P1, SLOT_8P1, SLOT_P2, SLOT_P3, SLOT_P4 = 0, 2, 4, 6, 8
 N_SLOTS = 10
 SLOT_COLS = PASSES * P * PACK
 STEPS = B * PASSES * M
@@ -46,6 +49,7 @@ FLOPS = 2 * O * C * B * (POS + SLAB + 2 * SMALL)
 def tile_layer_3d_dep_pa_kernel(tc, A, P1, P2, P3, P4, a5, gamma, beta, out):
     nc = tc.nc
     a_rows = A.rearrange("b c m k r t -> b c (m k r t)")
+    a_by_k = A.rearrange("b c m k r t -> b k (c m) (r t)")
     a5_rows = a5.rearrange("b o m k t -> b o (m k t)")
     out_rows = out.rearrange("b o m k r t -> b o (m k r t)")
     weights = (P1, P2, P3, P4)
@@ -59,10 +63,8 @@ def tile_layer_3d_dep_pa_kernel(tc, A, P1, P2, P3, P4, a5, gamma, beta, out):
         a_scales = keep.tile([P, PASSES, B, POS], U8, align_bytes=64)
         am_codes = keep.tile([P, PASSES, B * SLAB], U32, align_bytes=64)
         am_scales = keep.tile([P, PASSES, B * SLAB], U8, align_bytes=64)
-        at_codes = keep.tile([P, PASSES, B * SMALL], U32, align_bytes=64)
-        at_scales = keep.tile([P, PASSES, B * SMALL], U8, align_bytes=64)
-        ar_codes = keep.tile([P, PASSES, B * SMALL], U32, align_bytes=64)
-        ar_scales = keep.tile([P, PASSES, B * SMALL], U8, align_bytes=64)
+        atr_codes = keep.tile([P, PASSES, B, 2, SMALL], U32, align_bytes=64)
+        atr_scales = keep.tile([P, PASSES, B, 2, SMALL], U8, align_bytes=64)
         w_codes = keep.tile([P, O_TILES, N_SLOTS, P], U32, align_bytes=64)
         w_scales = keep.tile([P, O_TILES, N_SLOTS, P], U8, align_bytes=64)
 
@@ -93,14 +95,38 @@ def tile_layer_3d_dep_pa_kernel(tc, A, P1, P2, P3, P4, a5, gamma, beta, out):
                 op=ALU.add,
             )
         mean_w = keep.tile([P, 2, 2 * PER_TILE], BF16)
-        nc.vector.tensor_scalar_mul(out=mean_w[:], in0=member[:], scalar1=1.0 / NT)
+        for first, factor in ((0, M / NT), (PER_TILE, 1.0 / NR)):
+            nc.vector.tensor_scalar_mul(
+                out=mean_w[:, :, first : first + PER_TILE],
+                in0=member[:, :, first : first + PER_TILE],
+                scalar1=factor,
+            )
+
+        rm_member = keep.tile([P, 3 * PER_TILE // 2], F32)
+        nc.vector.tensor_reduce(
+            out=rm_member[:, 0 : PER_TILE // 2].rearrange("q (m tp) -> q m tp", tp=TP),
+            in_=ident_f32[:].rearrange("q (m r tp) -> q m tp r", r=NR, tp=TP),
+            axis=AXIS_X,
+            op=ALU.add,
+        )
+        nc.vector.tensor_reduce(
+            out=rm_member[:, PER_TILE // 2 : 3 * PER_TILE // 2],
+            in_=ident_f32[:].rearrange("q (m x) -> q x m", m=M),
+            axis=AXIS_X,
+            op=ALU.add,
+        )
+        rm_w = keep.tile([P, 3 * PER_TILE // 2], BF16)
+        for first, last, factor in ((0, PER_TILE // 2, 1.0 / NR), (PER_TILE // 2, 3 * PER_TILE // 2, 1.0)):
+            nc.vector.tensor_scalar_mul(
+                out=rm_w[:, first:last], in0=rm_member[:, first:last], scalar1=factor
+            )
 
         minus_half = keep.tile([P, 1], F32)
         nc.gpsimd.memset(minus_half[:], -0.5)
         nc.vector.memset(sums[:, :, :, UNITS], 0.0)
         nc.vector.tensor_scalar_add(
             out=sums[:, :, 1, UNITS], in0=sums[:, :, 1, UNITS],
-            scalar1=BN_EPS * TEN * TEN * COUNT * COUNT,
+            scalar1=BN_EPS * FORTY * FORTY * COUNT * COUNT,
         )
 
         gb_rows = keep.tile([P, P], BF16)
@@ -122,6 +148,7 @@ def tile_layer_3d_dep_pa_kernel(tc, A, P1, P2, P3, P4, a5, gamma, beta, out):
                 )
 
         a43_of = {}
+        a2_of = {}
         along_r_of = {}
         y_of = {}
 
@@ -132,45 +159,72 @@ def tile_layer_3d_dep_pa_kernel(tc, A, P1, P2, P3, P4, a5, gamma, beta, out):
 
         def mix_pooled(stage):
             b, ot = divmod(stage, O_TILES)
-            mine = slice(b * SMALL, (b + 1) * SMALL)
             a43_ps = psum_mix.tile([P, 2, SMALL], F32, bufs=2)
             passes(
                 a43_ps[:, 0, :], ot,
-                [(SLOT_P4 + g, ar_codes[:, g, mine], ar_scales[:, g, mine]) for g in range(PASSES)],
+                [(SLOT_P4 + g, atr_codes[:, g, b, 1, :], atr_scales[:, g, b, 1, :]) for g in range(PASSES)],
             )
             passes(
                 a43_ps[:, 1, :], ot,
-                [(SLOT_P3 + g, at_codes[:, g, mine], at_scales[:, g, mine]) for g in range(PASSES)],
+                [(SLOT_P3 + g, atr_codes[:, g, b, 0, :], atr_scales[:, g, b, 0, :]) for g in range(PASSES)],
             )
             along_r = work.tile([P, SMALL], F32)
             nc.vector.scalar_tensor_tensor(
-                out=along_r[:], in0=a43_ps[:, 0, :], scalar=0.5 * TEN, in1=a5_scaled[:, ot, b, :],
+                out=along_r[:], in0=a43_ps[:, 0, :], scalar=0.5 * FORTY, in1=a5_scaled[:, ot, b, :],
                 op0=ALU.mult, op1=ALU.add,
             )
             a43_of[stage] = a43_ps
             along_r_of[stage] = along_r
 
-        def add_along_r(n, a1_pool, a1_bufs):
+        def a2_apart(stage):
+            return stage < O_TILES
+
+        def mix(n, a1_pool, a1_bufs):
             stage, b, ot, hm = where(n)
             y = y_of[stage]
             b_slab = slice(b * SLAB, (b + 1) * SLAB)
+            a2 = [(SLOT_P2 + g, am_codes[:, g, b_slab], am_scales[:, g, b_slab]) for g in range(PASSES)]
+            if a2_apart(stage) and hm == 0:
+                a2_ps = a1_pool.tile([P, SLAB], F32, bufs=a1_bufs, tag="a1")
+                passes(a2_ps[:], ot, a2)
+                a2_sb = work.tile([P, SLAB], F32)
+                nc.scalar.copy(out=a2_sb[:], in_=a2_ps[:])
+                a2_of[stage] = a2_sb
             for mm in range(2):
                 m = 2 * hm + mm
                 slab = slice(m * SLAB, (m + 1) * SLAB)
-                a1_ps = a1_pool.tile([P, SLAB], F32, bufs=a1_bufs)
-                passes(
-                    a1_ps[:], ot,
-                    [(SLOT_8P1 + g, a_codes[:, g, b, slab], a_scales[:, g, b, slab]) for g in range(PASSES)]
-                    + [(SLOT_2P1 + g, a_codes[:, g, b, slab], a_scales[:, g, b, slab]) for g in range(PASSES)]
-                    + [(SLOT_P2 + g, am_codes[:, g, b_slab], am_scales[:, g, b_slab]) for g in range(PASSES)],
-                )
+                a1_ps = a1_pool.tile([P, SLAB], F32, bufs=a1_bufs, tag="a1")
+                rows = [(a_codes[:, g, b, slab], a_scales[:, g, b, slab]) for g in range(PASSES)]
+                a1_32 = [(SLOT_32P1 + g, *rows[g]) for g in range(PASSES)]
+                a1_8 = [(SLOT_8P1 + g, *rows[g]) for g in range(PASSES)]
+                if a2_apart(stage):
+                    passes(a1_ps[:], ot, a1_32)
+                    nc.vector.scalar_tensor_tensor(
+                        out=y[:, slab], in0=a1_ps[:], scalar=FORTY / 32.0, in1=a2_of[stage][:],
+                        op0=ALU.mult, op1=ALU.add,
+                    )
+                else:
+                    passes(a1_ps[:], ot, a1_32 + a1_8 + a2)
+                    nc.vector.tensor_tensor(
+                        out=y[:, slab].rearrange("o (k r t) -> o k r t", r=NR, t=NT),
+                        in0=a1_ps[:].rearrange("o (k r t) -> o k r t", r=NR, t=NT),
+                        in1=along_r_of[stage][:, m * K * NT : (m + 1) * K * NT]
+                        .rearrange("o (k t) -> o k t", t=NT)
+                        .unsqueeze(2)
+                        .to_broadcast([P, K, NR, NT]),
+                        op=ALU.add,
+                    )
+
+        def add_along_r(n):
+            stage, b, ot, hm = where(n)
+            if a2_apart(stage):
+                half = y_of[stage][:, hm * HALF : (hm + 1) * HALF].rearrange("o (x r t) -> o x r t", r=NR, t=NT)
                 nc.vector.tensor_tensor(
-                    out=y[:, slab].rearrange("o (k r t) -> o k r t", r=NR, t=NT),
-                    in0=a1_ps[:].rearrange("o (k r t) -> o k r t", r=NR, t=NT),
-                    in1=along_r_of[stage][:, m * K * NT : (m + 1) * K * NT]
-                    .rearrange("o (k t) -> o k t", t=NT)
+                    out=half, in0=half,
+                    in1=along_r_of[stage][:, hm * (SMALL // 2) : (hm + 1) * (SMALL // 2)]
+                    .rearrange("o (x t) -> o x t", t=NT)
                     .unsqueeze(2)
-                    .to_broadcast([P, K, NR, NT]),
+                    .to_broadcast([P, 2 * K, NR, NT]),
                     op=ALU.add,
                 )
 
@@ -219,17 +273,19 @@ def tile_layer_3d_dep_pa_kernel(tc, A, P1, P2, P3, P4, a5, gamma, beta, out):
             return
 
         def begun(step):
-            n = step if step < N_UNITS // 2 else step - 1
-            return n if step != N_UNITS // 2 and 0 <= n < N_UNITS else None
+            n = step - 1
+            return n if 0 <= n < N_UNITS else None
 
         def unit_step(step, a1_pool, a1_bufs):
             n = begun(step)
             if n is not None and n % 2 == 0:
                 mix_pooled(n // 2)
             if n is not None:
-                add_along_r(n, a1_pool, a1_bufs)
+                mix(n, a1_pool, a1_bufs)
             if begun(step - 1) is not None:
                 add_along_t(begun(step - 1))
+            if n is not None:
+                add_along_r(n)
 
         with ExitStack() as first:
             stage = first.enter_context(tc.tile_pool(name="stage", bufs=2))
@@ -246,39 +302,72 @@ def tile_layer_3d_dep_pa_kernel(tc, A, P1, P2, P3, P4, a5, gamma, beta, out):
             w_plain_of = {}
 
             def place(sg):
-                c, mm = divmod(sg, 2)
-                return c // 4, (c // 2) % 2, 2 * (c % 2) + mm
+                return sg // 8, (sg // 4) % 2, sg % 4
 
             def load(sg):
-                b, g, m = place(sg)
-                raw = stage.tile([P, PACK, SLAB], BF16, bufs=6)
-                nc.sync.dma_start(
-                    out=raw[:],
-                    in_=a_rows[
-                        b, g * K_PASS : (g + 1) * K_PASS, m * SLAB : (m + 1) * SLAB
-                    ].rearrange("(p j) w -> p j w", j=PACK),
-                )
-                raw_of[sg] = raw
+                b, g, part = place(sg)
+                c, mm = divmod(sg, 2)
+                if mm == 0:
+                    raw = stage.tile([P, 2 * PACK * SLAB], BF16, bufs=3)
+                    raw_of[c] = raw
+                if b == 0:
+                    nc.sync.dma_start(
+                        out=raw_of[c][:].rearrange("p (s j w) -> p s j w", s=2, j=PACK)[:, mm],
+                        in_=a_rows[
+                            b, g * K_PASS : (g + 1) * K_PASS, part * SLAB : (part + 1) * SLAB
+                        ].rearrange("(p j) w -> p j w", j=PACK),
+                    )
+                elif mm == 0:
+                    for kk in range(CHUNK_K):
+                        k = (part // 2) * CHUNK_K + kk
+                        nc.sync.dma_start(
+                            out=raw_of[c][:].rearrange("p (k q x) -> p k q x", k=CHUNK_K, x=POS_K)[:, kk],
+                            in_=a_by_k[
+                                b, k, g * K_PASS * M : (g + 1) * K_PASS * M, :
+                            ].rearrange("(p q) x -> p q x", q=PACK * M),
+                        )
 
             def regroup(sg):
                 c, mm = divmod(sg, 2)
-                b, g, m = place(sg)
+                b, g, part = place(sg)
                 if mm == 0:
                     grouped = stage.tile([P, HALF, PACK], BF16, bufs=2, align_bytes=64)
                     grouped_of[c] = grouped
-                on_vector = (m < 2) if b == 0 else (m == 0)
-                copy = nc.vector.tensor_copy if on_vector else nc.scalar.copy
-                copy(
-                    out=grouped_of[c][:, mm * SLAB : (mm + 1) * SLAB, :].rearrange(
-                        "p (c i) j -> p c j i", i=4
-                    ),
-                    in_=raw_of[sg][:].rearrange("p j (c i) -> p c j i", i=4),
-                )
+                if b == 0:
+                    copy = nc.vector.tensor_copy if part < 2 else nc.scalar.copy
+                    copy(
+                        out=grouped_of[c][:, mm * SLAB : (mm + 1) * SLAB, :].rearrange(
+                            "p (c i) j -> p c j i", i=4
+                        ),
+                        in_=raw_of[c][:]
+                        .rearrange("p (s j w) -> p s j w", s=2, j=PACK)[:, mm]
+                        .rearrange("p j (c i) -> p c j i", i=4),
+                    )
+                else:
+                    for m in (2 * mm, 2 * mm + 1):
+                        nc.vector.tensor_copy(
+                            out=grouped_of[c][
+                                :, m * CHUNK_K * POS_K : (m + 1) * CHUNK_K * POS_K, :
+                            ].rearrange("p (k x) j -> p k x j", k=CHUNK_K),
+                            in_=raw_of[c][:]
+                            .rearrange("p (k j m x) -> p k j m x", k=CHUNK_K, j=PACK, m=M)[:, :, :, m]
+                            .rearrange("p k j x -> p k x j"),
+                        )
 
-            def quantise_pairs(c):
-                b, g, m = place(2 * c)
-                cols = slice(m * SLAB, (m + 2) * SLAB)
+            def quantise(c):
+                b, g, part = place(2 * c)
                 flat = grouped_of[c][:].rearrange("p w j -> p (w j)")
+                if b == 1:
+                    width = CHUNK_K * POS_K
+                    for m in range(M):
+                        first = m * SLAB + (part // 2) * width
+                        nc.vector.quantize_mx(
+                            out=a_codes[:, g, b, first : first + width].bitcast(FP8X4),
+                            scales=a_scales[:, g, b, first : first + width],
+                            in_=flat[:, m * width * PACK : (m + 1) * width * PACK],
+                        )
+                    return
+                cols = slice(part * SLAB, (part + 2) * SLAB)
                 nc.vector.quantize_mx(
                     out=a_codes[:, g, b, cols].bitcast(FP8X4),
                     scales=a_scales[:, g, b, cols],
@@ -291,68 +380,108 @@ def tile_layer_3d_dep_pa_kernel(tc, A, P1, P2, P3, P4, a5, gamma, beta, out):
                     in1=flat[:, SLAB * PACK : 2 * SLAB * PACK],
                     op=ALU.add,
                 )
-                pairs_of.setdefault((b, g), []).append(pair_sum)
+                pairs_of.setdefault(g, []).append(pair_sum)
 
-            def sum_over_m(b, g):
-                pairs = pairs_of[(b, g)]
+            def am_tile(b, g):
                 am_grp = stage.tile([P, SLAB * PACK], BF16, bufs=1, align_bytes=64)
+                am_of[(b, g)] = am_grp
+                return am_grp
+
+            def sum_over_m(g):
+                pairs = pairs_of[g]
+                am_grp = am_tile(0, g)
                 nc.vector.tensor_tensor(
                     out=am_grp[:], in0=pairs[0][:], in1=pairs[1][:], op=ALU.add
                 )
-                am_of[(b, g)] = am_grp
 
             def turn(sg):
-                raw_words = raw_of[sg][:].bitcast(F32)
+                b, g, part = place(sg)
+                c, mm = divmod(sg, 2)
+                raw_words = raw_of[c][:].bitcast(F32)
                 flipped_of[sg] = []
                 for tl in range(TILES):
                     flipped_ps = psum.tile([P, PACK, P], F32, tag="turned")
                     for j in range(PACK):
+                        if b == 0:
+                            first = ((mm * PACK + j) * TILES + tl) * P
+                        else:
+                            first = ((mm * STEP_K + tl) * PACK + j) * P
                         nc.tensor.transpose(
                             out=flipped_ps[:, j, :],
-                            in_=raw_words[:, j, tl * P : (tl + 1) * P],
+                            in_=raw_words[:, first : first + P],
                             identity=ident_f32[:],
                         )
                     flipped = stage.tile([P, PACK, P], F32, bufs=4)
                     nc.scalar.copy(out=flipped[:], in_=flipped_ps[:])
                     flipped_of[sg].append(flipped)
 
+            def halves_of(sg, tl):
+                return (
+                    flipped_of[sg][tl][:]
+                    .rearrange("q j p -> q (j p)")
+                    .bitcast(BF16)
+                    .rearrange("q (j p e) -> q j p e", j=PACK, e=2)
+                )
+
             def means(sg):
-                b, g, m = place(sg)
-                if m == 0:
-                    at_grp = stage.tile([P, SMALL, PACK], BF16, align_bytes=64)
-                    ar_grp = stage.tile([P, SMALL, PACK], BF16, align_bytes=64)
-                    means_of[(b, g)] = (at_grp, ar_grp)
-                at_grp, ar_grp = means_of[(b, g)]
-                mean_ps = psum.tile([P, PACK, TILES, 2 * PER_TILE], F32, bufs=1)
-                for tl in range(TILES):
-                    halves = (
-                        flipped_of[sg][tl][:]
-                        .rearrange("q j p -> q (j p)")
-                        .bitcast(BF16)
-                        .rearrange("q (j p e) -> q j p e", j=PACK, e=2)
+                b, g, part = place(sg)
+                if part == 0:
+                    atr_grp = stage.tile([P, 2 * M, K, NR, PACK], BF16, align_bytes=64)
+                    means_of[(b, g)] = atr_grp
+                    if b == 1:
+                        am_tile(b, g)
+                atr_grp = means_of[(b, g)]
+                if b == 0:
+                    mean_ps = psum.tile([P, PACK, 2, TILES, PER_TILE], F32, bufs=1, tag="means")
+                    for tl in range(TILES):
+                        halves = halves_of(sg, tl)
+                        for j in range(PACK):
+                            for e in range(2):
+                                nc.tensor.matmul(
+                                    out=mean_ps[:, j, :, tl, :],
+                                    lhsT=halves[:, j, :, e],
+                                    rhs=mean_w[:, e, :].rearrange("q (w n) -> q w n", w=2),
+                                    start=(e == 0),
+                                    stop=(e == 1),
+                                )
+                    nc.scalar.copy(
+                        out=atr_grp[:, part : 2 * M : M].rearrange("p w k n j -> p w (k n) j"),
+                        in_=mean_ps[:].rearrange("p j w k n -> p w (k n) j"),
                     )
+                    return
+                for tl in range(STEP_K):
+                    k = part * STEP_K + tl
+                    halves = halves_of(sg, tl)
+                    sums_ps = psum.tile([P, PACK, P], F32, bufs=1, tag="means")
                     for j in range(PACK):
                         for e in range(2):
                             nc.tensor.matmul(
-                                out=mean_ps[:, j, tl, :],
+                                out=sums_ps[:, j, 0:PER_TILE],
                                 lhsT=halves[:, j, :, e],
-                                rhs=mean_w[:, e, :],
+                                rhs=mean_w[:, e, 0:PER_TILE],
                                 start=(e == 0),
                                 stop=(e == 1),
                             )
-                by_pos = mean_ps[:].rearrange("p j k n -> p k n j")
-                mine = slice(m * K * NR, (m + 1) * K * NR)
-                nc.scalar.copy(
-                    out=at_grp[:, mine, :].rearrange("p (k n) j -> p k n j", n=PER_TILE),
-                    in_=by_pos[:, :, 0:PER_TILE, :],
-                )
-                nc.scalar.copy(
-                    out=ar_grp[:, mine, :].rearrange("p (k n) j -> p k n j", n=PER_TILE),
-                    in_=by_pos[:, :, PER_TILE : 2 * PER_TILE, :],
-                )
+                        for e in range(2):
+                            nc.tensor.matmul(
+                                out=sums_ps[:, j, PER_TILE + e : P : 2],
+                                lhsT=halves[:, j, :, e],
+                                rhs=rm_w[:],
+                                start=True,
+                                stop=True,
+                            )
+                    nc.scalar.copy(
+                        out=atr_grp[:, :, k],
+                        in_=sums_ps[:, :, 0:POS_K].rearrange("p j (q x) -> p q x j", x=NR),
+                    )
+                    nc.scalar.copy(
+                        out=am_of[(b, g)][:, k * POS_K * PACK : (k + 1) * POS_K * PACK].rearrange(
+                            "p (x j) -> p x j", j=PACK
+                        ),
+                        in_=sums_ps[:, :, POS_K:P].rearrange("p j x -> p x j"),
+                    )
 
             def finish(b, g):
-                at_grp, ar_grp = means_of[(b, g)]
                 am_grp = am_of[(b, g)]
                 nc.vector.quantize_mx(
                     out=am_codes[:, g, b * SLAB : (b + 1) * SLAB].bitcast(FP8X4),
@@ -360,14 +489,9 @@ def tile_layer_3d_dep_pa_kernel(tc, A, P1, P2, P3, P4, a5, gamma, beta, out):
                     in_=am_grp[:],
                 )
                 nc.vector.quantize_mx(
-                    out=at_codes[:, g, b * SMALL : (b + 1) * SMALL].bitcast(FP8X4),
-                    scales=at_scales[:, g, b * SMALL : (b + 1) * SMALL],
-                    in_=at_grp[:].rearrange("p w j -> p (w j)"),
-                )
-                nc.vector.quantize_mx(
-                    out=ar_codes[:, g, b * SMALL : (b + 1) * SMALL].bitcast(FP8X4),
-                    scales=ar_scales[:, g, b * SMALL : (b + 1) * SMALL],
-                    in_=ar_grp[:].rearrange("p w j -> p (w j)"),
+                    out=atr_codes[:, g, b, :, :].rearrange("p w n -> p (w n)").bitcast(FP8X4),
+                    scales=atr_scales[:, g, b, :, :].rearrange("p w n -> p (w n)"),
+                    in_=means_of[(b, g)][:].rearrange("p w k n j -> p (w k n j)"),
                 )
 
             def small_inputs():
@@ -384,7 +508,7 @@ def tile_layer_3d_dep_pa_kernel(tc, A, P1, P2, P3, P4, a5, gamma, beta, out):
                 nc.gpsimd.tensor_scalar(
                     out=a5_scaled[:].rearrange("o t b x -> o (t b x)"),
                     in0=a5_sb[:].rearrange("o t b x -> o (t b x)"),
-                    scalar1=2.0 * TEN, scalar2=0.0, op0=ALU.mult, op1=ALU.add,
+                    scalar1=2.0 * FORTY, scalar2=0.0, op0=ALU.mult, op1=ALU.add,
                 )
 
             def turn_gamma_beta():
@@ -409,18 +533,20 @@ def tile_layer_3d_dep_pa_kernel(tc, A, P1, P2, P3, P4, a5, gamma, beta, out):
 
             def turn_weights(ot, pair):
                 if pair == 0:
-                    w_plain = stage.tile([P, 2 * SLOT_COLS], BF16, bufs=1)
+                    w_plain = stage.tile([P, SLOT_COLS], BF16, bufs=1)
                     w_grp = stage.tile([P, N_SLOTS * P * PACK], BF16, bufs=1, align_bytes=64)
                     w_plain_of[ot] = w_plain
                     w_grp_of[ot] = w_grp
                 w_words = w_raw_of[ot][:].bitcast(F32).rearrange(
                     "o (w g p u) -> o w g p u", w=N_W, g=PASSES, u=2
                 )
-                target = w_plain_of[ot] if pair == 0 else w_grp_of[ot]
-                target_words = target[:].bitcast(F32).rearrange("p (s o u) -> p s o u", o=P, u=2)
                 for half in range(2):
                     which = 2 * pair + half
-                    first_slot = half * PASSES if pair == 0 else SLOT_P3 + half * PASSES
+                    target, first_slot = (
+                        (w_plain_of[ot], 0) if which == 0
+                        else (w_grp_of[ot], (SLOT_P2, SLOT_P3, SLOT_P4)[which - 1])
+                    )
+                    target_words = target[:].bitcast(F32).rearrange("p (s o u) -> p s o u", o=P, u=2)
                     wt_ps = psum.tile([P, PASSES, 2, P], F32, tag="turned")
                     for g in range(PASSES):
                         for u in range(2):
@@ -434,12 +560,10 @@ def tile_layer_3d_dep_pa_kernel(tc, A, P1, P2, P3, P4, a5, gamma, beta, out):
                         in_=wt_ps[:].rearrange("p g u o -> p g o u"),
                     )
                 if pair == 0:
-                    for slot, source, factor in (
-                        (SLOT_8P1, 0, 8.0), (SLOT_2P1, 0, 2.0), (SLOT_P2, 1, 1.0 / M)
-                    ):
+                    for slot, factor in ((SLOT_32P1, 32.0), (SLOT_8P1, 8.0)):
                         nc.vector.tensor_scalar_mul(
                             out=w_grp_of[ot][:, slot * P * PACK : slot * P * PACK + SLOT_COLS],
-                            in0=w_plain_of[ot][:, source * SLOT_COLS : (source + 1) * SLOT_COLS],
+                            in0=w_plain_of[ot][:],
                             scalar1=factor,
                         )
 
@@ -466,9 +590,9 @@ def tile_layer_3d_dep_pa_kernel(tc, A, P1, P2, P3, P4, a5, gamma, beta, out):
                 if sg + 2 < STEPS:
                     regroup(sg + 2)
                 if mm == 0:
-                    quantise_pairs(c)
-                if sg % 4 == 3:
-                    sum_over_m(sg // 8, (sg // 4) % 2)
+                    quantise(c)
+                if sg % 4 == 3 and sg < STEPS // 2:
+                    sum_over_m(sg // 4)
                 if sg >= 1:
                     means(sg - 1)
                 if sg >= 4 and sg % 4 == 0:
@@ -511,7 +635,7 @@ def tile_layer_3d_dep_pa_kernel(tc, A, P1, P2, P3, P4, a5, gamma, beta, out):
                 spread = work.tile([P, 1], F32)
                 nc.vector.tensor_scalar(
                     out=spread[:], in0=minus_spread[:], scalar1=-1.0,
-                    scalar2=BN_EPS * TEN * TEN * COUNT * COUNT, op0=ALU.mult, op1=ALU.max,
+                    scalar2=BN_EPS * FORTY * FORTY * COUNT * COUNT, op0=ALU.mult, op1=ALU.max,
                 )
                 w = work.tile([P, 1], F32)
                 nc.gpsimd.tensor_tensor(out=w[:], in0=spread[:], in1=minus_half[:], op=ALU.pow)

@@ -33,9 +33,8 @@ PER_TILE = TILE_POS // NT
 TP = NT // 2
 N_W = 4
 FORTY = 40.0
-SLOT_32P1, SLOT_8P1, SLOT_P2, SLOT_P3, SLOT_P4 = 0, 2, 4, 6, 8
-N_SLOTS = 10
-SLOT_COLS = PASSES * P * PACK
+SLOT_P1, SLOT_P2, SLOT_P3, SLOT_P4 = 0, 2, 4, 6
+N_SLOTS = 8
 STEPS = B * PASSES * M
 N_UNITS = 2 * B * O_TILES
 COUNT = B * POS
@@ -147,9 +146,9 @@ def tile_layer_3d_dep_pa_kernel(tc, A, P1, P2, P3, P4, a5, gamma, beta, out):
                     stop=(i == len(operands) - 1),
                 )
 
-        a43_of = {}
         a2_of = {}
-        along_r_of = {}
+        small_of = {}
+        terms_of = {}
         y_of = {}
 
         def where(n):
@@ -159,7 +158,7 @@ def tile_layer_3d_dep_pa_kernel(tc, A, P1, P2, P3, P4, a5, gamma, beta, out):
 
         def mix_pooled(stage):
             b, ot = divmod(stage, O_TILES)
-            a43_ps = psum_mix.tile([P, 2, SMALL], F32, bufs=2)
+            a43_ps = psum_mix.tile([P, 2, SMALL], F32, bufs=1)
             passes(
                 a43_ps[:, 0, :], ot,
                 [(SLOT_P4 + g, atr_codes[:, g, b, 1, :], atr_scales[:, g, b, 1, :]) for g in range(PASSES)],
@@ -173,69 +172,60 @@ def tile_layer_3d_dep_pa_kernel(tc, A, P1, P2, P3, P4, a5, gamma, beta, out):
                 out=along_r[:], in0=a43_ps[:, 0, :], scalar=0.5 * FORTY, in1=a5_scaled[:, ot, b, :],
                 op0=ALU.mult, op1=ALU.add,
             )
-            a43_of[stage] = a43_ps
-            along_r_of[stage] = along_r
+            along_t = work.tile([P, SMALL], F32)
+            nc.scalar.copy(out=along_t[:], in_=a43_ps[:, 1, :])
+            small_of[stage] = (along_r, along_t)
 
-        def a2_apart(stage):
-            return stage < O_TILES
-
-        def mix(n, a1_pool, a1_bufs):
+        def add_small_terms(n):
             stage, b, ot, hm = where(n)
-            y = y_of[stage]
-            b_slab = slice(b * SLAB, (b + 1) * SLAB)
-            a2 = [(SLOT_P2 + g, am_codes[:, g, b_slab], am_scales[:, g, b_slab]) for g in range(PASSES)]
-            if a2_apart(stage) and hm == 0:
-                a2_ps = a1_pool.tile([P, SLAB], F32, bufs=a1_bufs, tag="a1")
-                passes(a2_ps[:], ot, a2)
-                a2_sb = work.tile([P, SLAB], F32)
-                nc.scalar.copy(out=a2_sb[:], in_=a2_ps[:])
-                a2_of[stage] = a2_sb
-            for mm in range(2):
-                m = 2 * hm + mm
-                slab = slice(m * SLAB, (m + 1) * SLAB)
-                a1_ps = a1_pool.tile([P, SLAB], F32, bufs=a1_bufs, tag="a1")
-                rows = [(a_codes[:, g, b, slab], a_scales[:, g, b, slab]) for g in range(PASSES)]
-                a1_32 = [(SLOT_32P1 + g, *rows[g]) for g in range(PASSES)]
-                a1_8 = [(SLOT_8P1 + g, *rows[g]) for g in range(PASSES)]
-                if a2_apart(stage):
-                    passes(a1_ps[:], ot, a1_32)
-                    nc.vector.scalar_tensor_tensor(
-                        out=y[:, slab], in0=a1_ps[:], scalar=FORTY / 32.0, in1=a2_of[stage][:],
-                        op0=ALU.mult, op1=ALU.add,
-                    )
-                else:
-                    passes(a1_ps[:], ot, a1_32 + a1_8 + a2)
-                    nc.vector.tensor_tensor(
-                        out=y[:, slab].rearrange("o (k r t) -> o k r t", r=NR, t=NT),
-                        in0=a1_ps[:].rearrange("o (k r t) -> o k r t", r=NR, t=NT),
-                        in1=along_r_of[stage][:, m * K * NT : (m + 1) * K * NT]
-                        .rearrange("o (k t) -> o k t", t=NT)
-                        .unsqueeze(2)
-                        .to_broadcast([P, K, NR, NT]),
-                        op=ALU.add,
-                    )
-
-        def add_along_r(n):
-            stage, b, ot, hm = where(n)
-            if a2_apart(stage):
-                half = y_of[stage][:, hm * HALF : (hm + 1) * HALF].rearrange("o (x r t) -> o x r t", r=NR, t=NT)
-                nc.vector.tensor_tensor(
-                    out=half, in0=half,
-                    in1=along_r_of[stage][:, hm * (SMALL // 2) : (hm + 1) * (SMALL // 2)]
-                    .rearrange("o (x t) -> o x t", t=NT)
+            along_r, along_t = small_of[stage]
+            for m in (2 * hm, 2 * hm + 1):
+                terms = work.tile([P, K, NR, NT], F32, bufs=3)
+                mine = slice(m * K * NT, (m + 1) * K * NT)
+                nc.gpsimd.tensor_tensor(
+                    out=terms[:],
+                    in0=along_t[:, mine]
+                    .rearrange("o (k r) -> o k r", r=NR)
+                    .unsqueeze(3)
+                    .to_broadcast([P, K, NR, NT]),
+                    in1=along_r[:, mine]
+                    .rearrange("o (k t) -> o k t", t=NT)
                     .unsqueeze(2)
-                    .to_broadcast([P, 2 * K, NR, NT]),
+                    .to_broadcast([P, K, NR, NT]),
                     op=ALU.add,
                 )
+                terms_of[(n, m)] = terms
 
-        def add_along_t(n):
+        def mix(n, pool, a1_bufs, a2_bufs):
             stage, b, ot, hm = where(n)
-            half = y_of[stage][:, hm * HALF : (hm + 1) * HALF].rearrange("o (x t) -> o x t", t=NT)
+            y = y_of[stage]
+            for m in (2 * hm, 2 * hm + 1):
+                slab = slice(m * SLAB, (m + 1) * SLAB)
+                a1_ps = pool.tile([P, SLAB], F32, bufs=a1_bufs)
+                passes(
+                    a1_ps[:], ot,
+                    [(SLOT_P1 + g, a_codes[:, g, b, slab], a_scales[:, g, b, slab]) for g in range(PASSES)],
+                )
+                nc.vector.scalar_tensor_tensor(
+                    out=y[:, slab], in0=a1_ps[:], scalar=FORTY,
+                    in1=terms_of[(n, m)][:].rearrange("o k r t -> o (k r t)"),
+                    op0=ALU.mult, op1=ALU.add,
+                )
+            if hm == 0:
+                b_slab = slice(b * SLAB, (b + 1) * SLAB)
+                a2_ps = pool.tile([P, SLAB], F32, bufs=a2_bufs)
+                passes(
+                    a2_ps[:], ot,
+                    [(SLOT_P2 + g, am_codes[:, g, b_slab], am_scales[:, g, b_slab]) for g in range(PASSES)],
+                )
+                a2_of[stage] = a2_ps
+
+        def add_over_m(n):
+            stage, b, ot, hm = where(n)
+            half = y_of[stage][:, hm * HALF : (hm + 1) * HALF].rearrange("o (m x) -> o m x", x=SLAB)
             nc.vector.tensor_tensor(
                 out=half,
-                in0=a43_of[stage][:, 1, hm * (SMALL // 2) : (hm + 1) * (SMALL // 2)]
-                .unsqueeze(2)
-                .to_broadcast([P, SMALL // 2, NT]),
+                in0=a2_of[stage][:].unsqueeze(1).to_broadcast([P, 2, SLAB]),
                 in1=half, op=ALU.add,
             )
 
@@ -276,16 +266,16 @@ def tile_layer_3d_dep_pa_kernel(tc, A, P1, P2, P3, P4, a5, gamma, beta, out):
             n = step - 1
             return n if 0 <= n < N_UNITS else None
 
-        def unit_step(step, a1_pool, a1_bufs):
-            n = begun(step)
-            if n is not None and n % 2 == 0:
-                mix_pooled(n // 2)
-            if n is not None:
-                mix(n, a1_pool, a1_bufs)
+        def unit_step(step, pool, a1_bufs, a2_bufs):
+            ahead = begun(step + 1)
+            if ahead is not None and ahead % 2 == 0:
+                mix_pooled(ahead // 2)
+            if ahead is not None:
+                add_small_terms(ahead)
+            if begun(step) is not None:
+                mix(begun(step), pool, a1_bufs, a2_bufs)
             if begun(step - 1) is not None:
-                add_along_t(begun(step - 1))
-            if n is not None:
-                add_along_r(n)
+                add_over_m(begun(step - 1))
 
         with ExitStack() as first:
             stage = first.enter_context(tc.tile_pool(name="stage", bufs=2))
@@ -299,7 +289,6 @@ def tile_layer_3d_dep_pa_kernel(tc, A, P1, P2, P3, P4, a5, gamma, beta, out):
             am_of = {}
             w_raw_of = {}
             w_grp_of = {}
-            w_plain_of = {}
 
             def place(sg):
                 return sg // 8, (sg // 4) % 2, sg % 4
@@ -533,20 +522,15 @@ def tile_layer_3d_dep_pa_kernel(tc, A, P1, P2, P3, P4, a5, gamma, beta, out):
 
             def turn_weights(ot, pair):
                 if pair == 0:
-                    w_plain = stage.tile([P, SLOT_COLS], BF16, bufs=1)
                     w_grp = stage.tile([P, N_SLOTS * P * PACK], BF16, bufs=1, align_bytes=64)
-                    w_plain_of[ot] = w_plain
                     w_grp_of[ot] = w_grp
                 w_words = w_raw_of[ot][:].bitcast(F32).rearrange(
                     "o (w g p u) -> o w g p u", w=N_W, g=PASSES, u=2
                 )
+                target_words = w_grp_of[ot][:].bitcast(F32).rearrange("p (s o u) -> p s o u", o=P, u=2)
                 for half in range(2):
                     which = 2 * pair + half
-                    target, first_slot = (
-                        (w_plain_of[ot], 0) if which == 0
-                        else (w_grp_of[ot], (SLOT_P2, SLOT_P3, SLOT_P4)[which - 1])
-                    )
-                    target_words = target[:].bitcast(F32).rearrange("p (s o u) -> p s o u", o=P, u=2)
+                    first_slot = which * PASSES
                     wt_ps = psum.tile([P, PASSES, 2, P], F32, tag="turned")
                     for g in range(PASSES):
                         for u in range(2):
@@ -559,21 +543,13 @@ def tile_layer_3d_dep_pa_kernel(tc, A, P1, P2, P3, P4, a5, gamma, beta, out):
                         out=target_words[:, first_slot : first_slot + PASSES, :, :],
                         in_=wt_ps[:].rearrange("p g u o -> p g o u"),
                     )
-                if pair == 0:
-                    for slot, factor in ((SLOT_32P1, 32.0), (SLOT_8P1, 8.0)):
-                        nc.vector.tensor_scalar_mul(
-                            out=w_grp_of[ot][:, slot * P * PACK : slot * P * PACK + SLOT_COLS],
-                            in0=w_plain_of[ot][:],
-                            scalar1=factor,
-                        )
 
             def quantise_weights(ot):
-                for first, last in ((0, SLOT_P4), (SLOT_P4, N_SLOTS)):
-                    nc.vector.quantize_mx(
-                        out=w_codes[:, ot, first:last, :].rearrange("p s o -> p (s o)").bitcast(FP8X4),
-                        scales=w_scales[:, ot, first:last, :].rearrange("p s o -> p (s o)"),
-                        in_=w_grp_of[ot][:, first * P * PACK : last * P * PACK],
-                    )
+                nc.vector.quantize_mx(
+                    out=w_codes[:, ot, :, :].rearrange("p s o -> p (s o)").bitcast(FP8X4),
+                    scales=w_scales[:, ot, :, :].rearrange("p s o -> p (s o)"),
+                    in_=w_grp_of[ot][:],
+                )
 
             for ot in range(O_TILES):
                 y_of[ot] = y_first[:, ot, :]
@@ -602,7 +578,7 @@ def tile_layer_3d_dep_pa_kernel(tc, A, P1, P2, P3, P4, a5, gamma, beta, out):
                 if sg == 4:
                     turn_gamma_beta()
                 if sg >= STEPS // 2:
-                    unit_step(sg - STEPS // 2, psum, 3)
+                    unit_step(sg - STEPS // 2, psum, 3, 1)
                     relus_up_to(begun(sg - STEPS // 2 - 2), nothing)
                 if sg >= 2:
                     ot, part = divmod(sg - 2, 3)
@@ -613,9 +589,9 @@ def tile_layer_3d_dep_pa_kernel(tc, A, P1, P2, P3, P4, a5, gamma, beta, out):
                         if ot + 1 < O_TILES:
                             load_weights(ot + 1)
             means(STEPS - 1)
-            unit_step(N_UNITS // 2, psum, 3)
-            relus_up_to(begun(N_UNITS // 2 - 2), nothing)
             finish(1, 1)
+            unit_step(N_UNITS // 2, psum, 3, 1)
+            relus_up_to(begun(N_UNITS // 2 - 2), nothing)
 
         with ExitStack() as second:
             late = second.enter_context(tc.tile_pool(name="late", bufs=4))
@@ -684,6 +660,6 @@ def tile_layer_3d_dep_pa_kernel(tc, A, P1, P2, P3, P4, a5, gamma, beta, out):
                 if n is not None and n % 2 == 0:
                     y_second = late.tile([P, POS], F32)
                     y_of[n // 2] = y_second[:]
-                unit_step(step, psum, 6)
+                unit_step(step, psum, 4, 2)
                 relus_up_to(step - 2, after_square)
             normalise_and_store(O_TILES - 1, 1)

@@ -37,6 +37,7 @@ SLOT_P1, SLOT_P2, SLOT_P3, SLOT_P4 = 0, 2, 4, 6
 N_SLOTS = 8
 STEPS = B * PASSES * M
 N_UNITS = 2 * B * O_TILES
+LAG = 2
 COUNT = B * POS
 ROOT_COUNT = 64.0
 assert ROOT_COUNT * ROOT_COUNT == COUNT
@@ -48,7 +49,7 @@ FLOPS = 2 * O * C * B * (POS + SLAB + 2 * SMALL)
 def tile_layer_3d_dep_pa_kernel(tc, A, P1, P2, P3, P4, a5, gamma, beta, out):
     nc = tc.nc
     a_rows = A.rearrange("b c m k r t -> b c (m k r t)")
-    a_by_k = A.rearrange("b c m k r t -> b k (c m) (r t)")
+    a_by_cm = A.rearrange("b c m k r t -> b (c m) (k r t)")
     a5_rows = a5.rearrange("b o m k t -> b o (m k t)")
     out_rows = out.rearrange("b o m k r t -> b o (m k r t)")
     weights = (P1, P2, P3, P4)
@@ -131,7 +132,6 @@ def tile_layer_3d_dep_pa_kernel(tc, A, P1, P2, P3, P4, a5, gamma, beta, out):
         gb_rows = keep.tile([P, P], BF16)
         nc.vector.memset(gb_rows[:], 0.0)
         gamma_beta = keep.tile([P, 2 * O_TILES], F32)
-        a5_sb = keep.tile([P, O_TILES, B, SMALL], BF16)
         a5_scaled = keep.tile([P, O_TILES, B, SMALL], F32)
 
         def passes(acc, ot, operands):
@@ -167,12 +167,12 @@ def tile_layer_3d_dep_pa_kernel(tc, A, P1, P2, P3, P4, a5, gamma, beta, out):
                 a43_ps[:, 1, :], ot,
                 [(SLOT_P3 + g, atr_codes[:, g, b, 0, :], atr_scales[:, g, b, 0, :]) for g in range(PASSES)],
             )
-            along_r = work.tile([P, SMALL], F32)
+            along_r = work.tile([P, SMALL], F32, bufs=4)
             nc.vector.scalar_tensor_tensor(
                 out=along_r[:], in0=a43_ps[:, 0, :], scalar=0.5 * FORTY, in1=a5_scaled[:, ot, b, :],
                 op0=ALU.mult, op1=ALU.add,
             )
-            along_t = work.tile([P, SMALL], F32)
+            along_t = work.tile([P, SMALL], F32, bufs=4)
             nc.scalar.copy(out=along_t[:], in_=a43_ps[:, 1, :])
             small_of[stage] = (along_r, along_t)
 
@@ -180,7 +180,7 @@ def tile_layer_3d_dep_pa_kernel(tc, A, P1, P2, P3, P4, a5, gamma, beta, out):
             stage, b, ot, hm = where(n)
             along_r, along_t = small_of[stage]
             for m in (2 * hm, 2 * hm + 1):
-                terms = work.tile([P, K, NR, NT], F32, bufs=3)
+                terms = work.tile([P, K, NR, NT], F32, bufs=4)
                 mine = slice(m * K * NT, (m + 1) * K * NT)
                 nc.gpsimd.tensor_tensor(
                     out=terms[:],
@@ -196,7 +196,7 @@ def tile_layer_3d_dep_pa_kernel(tc, A, P1, P2, P3, P4, a5, gamma, beta, out):
                 )
                 terms_of[(n, m)] = terms
 
-        def mix(n, pool, a1_bufs, a2_bufs):
+        def mix(n, pool, a1_bufs):
             stage, b, ot, hm = where(n)
             y = y_of[stage]
             for m in (2 * hm, 2 * hm + 1):
@@ -213,7 +213,7 @@ def tile_layer_3d_dep_pa_kernel(tc, A, P1, P2, P3, P4, a5, gamma, beta, out):
                 )
             if hm == 0:
                 b_slab = slice(b * SLAB, (b + 1) * SLAB)
-                a2_ps = pool.tile([P, SLAB], F32, bufs=a2_bufs)
+                a2_ps = psum_mix.tile([P, SLAB], F32, bufs=1)
                 passes(
                     a2_ps[:], ot,
                     [(SLOT_P2 + g, am_codes[:, g, b_slab], am_scales[:, g, b_slab]) for g in range(PASSES)],
@@ -239,7 +239,7 @@ def tile_layer_3d_dep_pa_kernel(tc, A, P1, P2, P3, P4, a5, gamma, beta, out):
 
         def square(n):
             stage, b, ot, hm = where(n)
-            squares = work.tile([P, HALF], BF16)
+            squares = work.tile([P, HALF], BF16, bufs=1)
             nc.scalar.activation(
                 out=squares[:], in_=y_of[stage][:, hm * HALF : (hm + 1) * HALF], func=ACT.Square,
                 scale=ROOT_COUNT,
@@ -263,17 +263,17 @@ def tile_layer_3d_dep_pa_kernel(tc, A, P1, P2, P3, P4, a5, gamma, beta, out):
             return
 
         def begun(step):
-            n = step - 1
+            n = step - LAG
             return n if 0 <= n < N_UNITS else None
 
-        def unit_step(step, pool, a1_bufs, a2_bufs):
+        def unit_step(step, pool, a1_bufs):
             ahead = begun(step + 1)
             if ahead is not None and ahead % 2 == 0:
                 mix_pooled(ahead // 2)
             if ahead is not None:
                 add_small_terms(ahead)
             if begun(step) is not None:
-                mix(begun(step), pool, a1_bufs, a2_bufs)
+                mix(begun(step), pool, a1_bufs)
             if begun(step - 1) is not None:
                 add_over_m(begun(step - 1))
 
@@ -283,9 +283,11 @@ def tile_layer_3d_dep_pa_kernel(tc, A, P1, P2, P3, P4, a5, gamma, beta, out):
 
             raw_of = {}
             grouped_of = {}
+            by_k_of = {}
             flipped_of = {}
             means_of = {}
-            pairs_of = {}
+            m_sum_of = {}
+            last_of = {}
             am_of = {}
             w_raw_of = {}
             w_grp_of = {}
@@ -307,14 +309,24 @@ def tile_layer_3d_dep_pa_kernel(tc, A, P1, P2, P3, P4, a5, gamma, beta, out):
                         ].rearrange("(p j) w -> p j w", j=PACK),
                     )
                 elif mm == 0:
-                    for kk in range(CHUNK_K):
-                        k = (part // 2) * CHUNK_K + kk
-                        nc.sync.dma_start(
-                            out=raw_of[c][:].rearrange("p (k q x) -> p k q x", k=CHUNK_K, x=POS_K)[:, kk],
-                            in_=a_by_k[
-                                b, k, g * K_PASS * M : (g + 1) * K_PASS * M, :
-                            ].rearrange("(p q) x -> p q x", q=PACK * M),
-                        )
+                    first = (part // 2) * CHUNK_K * POS_K
+                    nc.sync.dma_start(
+                        out=raw_of[c][:].rearrange("p (q x) -> p q x", q=PACK * M),
+                        in_=a_by_cm[
+                            b, g * K_PASS * M : (g + 1) * K_PASS * M, first : first + CHUNK_K * POS_K
+                        ].rearrange("(p q) x -> p q x", q=PACK * M),
+                    )
+
+            def gather_m(sg):
+                b, g, part = place(sg)
+                c, mm = divmod(sg, 2)
+                if b == 1 and mm == 0:
+                    by_k = stage.tile([P, CHUNK_K, PACK * M, POS_K], BF16, bufs=2)
+                    nc.vector.tensor_copy(
+                        out=by_k[:],
+                        in_=raw_of[c][:].rearrange("p (q k x) -> p k q x", q=PACK * M, k=CHUNK_K),
+                    )
+                    by_k_of[c] = by_k
 
             def regroup(sg):
                 c, mm = divmod(sg, 2)
@@ -339,8 +351,8 @@ def tile_layer_3d_dep_pa_kernel(tc, A, P1, P2, P3, P4, a5, gamma, beta, out):
                                 :, m * CHUNK_K * POS_K : (m + 1) * CHUNK_K * POS_K, :
                             ].rearrange("p (k x) j -> p k x j", k=CHUNK_K),
                             in_=raw_of[c][:]
-                            .rearrange("p (k j m x) -> p k j m x", k=CHUNK_K, j=PACK, m=M)[:, :, :, m]
-                            .rearrange("p k j x -> p k x j"),
+                            .rearrange("p (j m k x) -> p j m k x", j=PACK, m=M, k=CHUNK_K)[:, :, m]
+                            .rearrange("p j k x -> p k x j"),
                         )
 
             def quantise(c):
@@ -362,31 +374,35 @@ def tile_layer_3d_dep_pa_kernel(tc, A, P1, P2, P3, P4, a5, gamma, beta, out):
                     scales=a_scales[:, g, b, cols],
                     in_=flat,
                 )
-                pair_sum = stage.tile([P, SLAB * PACK], F32, bufs=2)
-                nc.vector.tensor_tensor(
-                    out=pair_sum[:],
-                    in0=flat[:, 0 : SLAB * PACK],
-                    in1=flat[:, SLAB * PACK : 2 * SLAB * PACK],
-                    op=ALU.add,
-                )
-                pairs_of.setdefault(g, []).append(pair_sum)
+                slabs = [flat[:, i * SLAB * PACK : (i + 1) * SLAB * PACK] for i in range(2)]
+                if part == 0:
+                    m_sum = stage.tile([P, SLAB * PACK], F32, bufs=1)
+                    m_sum_of[g] = m_sum
+                    nc.vector.tensor_tensor(out=m_sum[:], in0=slabs[0], in1=slabs[1], op=ALU.add)
+                else:
+                    nc.vector.tensor_tensor(
+                        out=m_sum_of[g][:], in0=m_sum_of[g][:], in1=slabs[0], op=ALU.add
+                    )
+                    last_of[g] = slabs[1]
 
             def am_tile(b, g):
-                am_grp = stage.tile([P, SLAB * PACK], BF16, bufs=1, align_bytes=64)
+                am_grp = stage.tile([P, SLAB * PACK], BF16, bufs=1, tag="am", align_bytes=64)
                 am_of[(b, g)] = am_grp
                 return am_grp
 
             def sum_over_m(g):
-                pairs = pairs_of[g]
                 am_grp = am_tile(0, g)
                 nc.vector.tensor_tensor(
-                    out=am_grp[:], in0=pairs[0][:], in1=pairs[1][:], op=ALU.add
+                    out=am_grp[:], in0=m_sum_of[g][:], in1=last_of[g], op=ALU.add
                 )
 
             def turn(sg):
                 b, g, part = place(sg)
                 c, mm = divmod(sg, 2)
-                raw_words = raw_of[c][:].bitcast(F32)
+                if b == 0:
+                    raw_words = raw_of[c][:].bitcast(F32)
+                else:
+                    raw_words = by_k_of[c][:].rearrange("p k q x -> p (k q x)").bitcast(F32)
                 flipped_of[sg] = []
                 for tl in range(TILES):
                     flipped_ps = psum.tile([P, PACK, P], F32, tag="turned")
@@ -415,7 +431,7 @@ def tile_layer_3d_dep_pa_kernel(tc, A, P1, P2, P3, P4, a5, gamma, beta, out):
             def means(sg):
                 b, g, part = place(sg)
                 if part == 0:
-                    atr_grp = stage.tile([P, 2 * M, K, NR, PACK], BF16, align_bytes=64)
+                    atr_grp = stage.tile([P, 2 * M, K, NR, PACK], BF16, bufs=1, align_bytes=64)
                     means_of[(b, g)] = atr_grp
                     if b == 1:
                         am_tile(b, g)
@@ -484,6 +500,7 @@ def tile_layer_3d_dep_pa_kernel(tc, A, P1, P2, P3, P4, a5, gamma, beta, out):
                 )
 
             def small_inputs():
+                a5_sb = stage.tile([P, O_TILES, B, SMALL], BF16, bufs=1, tag="am", align_bytes=64)
                 nc.sync.dma_start(
                     out=gb_rows[0:O_TILES, :], in_=gamma.rearrange("(t o) -> t o", o=P)
                 )
@@ -564,6 +581,7 @@ def tile_layer_3d_dep_pa_kernel(tc, A, P1, P2, P3, P4, a5, gamma, beta, out):
                     load(sg + 4)
                 turn(sg)
                 if sg + 2 < STEPS:
+                    gather_m(sg + 2)
                     regroup(sg + 2)
                 if mm == 0:
                     quantise(c)
@@ -578,7 +596,7 @@ def tile_layer_3d_dep_pa_kernel(tc, A, P1, P2, P3, P4, a5, gamma, beta, out):
                 if sg == 4:
                     turn_gamma_beta()
                 if sg >= STEPS // 2:
-                    unit_step(sg - STEPS // 2, psum, 3, 1)
+                    unit_step(sg - STEPS // 2, psum, 3)
                     relus_up_to(begun(sg - STEPS // 2 - 2), nothing)
                 if sg >= 2:
                     ot, part = divmod(sg - 2, 3)
@@ -590,7 +608,7 @@ def tile_layer_3d_dep_pa_kernel(tc, A, P1, P2, P3, P4, a5, gamma, beta, out):
                             load_weights(ot + 1)
             means(STEPS - 1)
             finish(1, 1)
-            unit_step(N_UNITS // 2, psum, 3, 1)
+            unit_step(N_UNITS // 2, psum, 3)
             relus_up_to(begun(N_UNITS // 2 - 2), nothing)
 
         with ExitStack() as second:
@@ -631,7 +649,7 @@ def tile_layer_3d_dep_pa_kernel(tc, A, P1, P2, P3, P4, a5, gamma, beta, out):
             def normalise_and_store(ot, b):
                 gain, shift = affine_of[ot]
                 y = y_of[b * O_TILES + ot]
-                on_vector = ot + b == O_TILES - 1 and ot >= O_TILES - 2
+                on_vector = b == 0 or ot == O_TILES - 2
                 for hm in range(2):
                     half = slice(hm * HALF, (hm + 1) * HALF)
                     if b == 1 and not on_vector:
@@ -655,11 +673,11 @@ def tile_layer_3d_dep_pa_kernel(tc, A, P1, P2, P3, P4, a5, gamma, beta, out):
                     statistics(ot)
                     normalise_and_store(ot, 0)
 
-            for step in range(N_UNITS // 2 + 1, N_UNITS + 3):
+            for step in range(N_UNITS // 2 + 1, N_UNITS + LAG + 2):
                 n = begun(step)
                 if n is not None and n % 2 == 0:
                     y_second = late.tile([P, POS], F32)
                     y_of[n // 2] = y_second[:]
-                unit_step(step, psum, 4, 2)
-                relus_up_to(step - 2, after_square)
+                unit_step(step, psum, 6)
+                relus_up_to(step - LAG - 1, after_square)
             normalise_and_store(O_TILES - 1, 1)

@@ -19,6 +19,7 @@ P = 128
 PACK = 4
 K_PASS = P * PACK
 PASSES = C // K_PASS
+LATER_FIRST = tuple(reversed(range(PASSES)))
 POS = M * K * NR * NT
 HALF = POS // 2
 SLAB = K * NR * NT
@@ -49,7 +50,7 @@ FLOPS = 2 * O * C * B * (POS + SLAB + 2 * SMALL)
 def tile_layer_3d_dep_pa_kernel(tc, A, P1, P2, P3, P4, a5, gamma, beta, out):
     nc = tc.nc
     a_rows = A.rearrange("b c m k r t -> b c (m k r t)")
-    a_by_cm = A.rearrange("b c m k r t -> b (c m) (k r t)")
+    a_by_k = A.rearrange("b c m k r t -> b k (c m) (r t)")
     a5_rows = a5.rearrange("b o m k t -> b o (m k t)")
     out_rows = out.rearrange("b o m k r t -> b o (m k r t)")
     weights = (P1, P2, P3, P4)
@@ -121,8 +122,6 @@ def tile_layer_3d_dep_pa_kernel(tc, A, P1, P2, P3, P4, a5, gamma, beta, out):
                 out=rm_w[:, first:last], in0=rm_member[:, first:last], scalar1=factor
             )
 
-        minus_half = keep.tile([P, 1], F32)
-        nc.gpsimd.memset(minus_half[:], -0.5)
         nc.vector.memset(sums[:, :, :, UNITS], 0.0)
         nc.vector.tensor_scalar_add(
             out=sums[:, :, 1, UNITS], in0=sums[:, :, 1, UNITS],
@@ -161,11 +160,11 @@ def tile_layer_3d_dep_pa_kernel(tc, A, P1, P2, P3, P4, a5, gamma, beta, out):
             a43_ps = psum_mix.tile([P, 2, SMALL], F32, bufs=1)
             passes(
                 a43_ps[:, 0, :], ot,
-                [(SLOT_P4 + g, atr_codes[:, g, b, 1, :], atr_scales[:, g, b, 1, :]) for g in range(PASSES)],
+                [(SLOT_P4 + g, atr_codes[:, g, b, 1, :], atr_scales[:, g, b, 1, :]) for g in LATER_FIRST],
             )
             passes(
                 a43_ps[:, 1, :], ot,
-                [(SLOT_P3 + g, atr_codes[:, g, b, 0, :], atr_scales[:, g, b, 0, :]) for g in range(PASSES)],
+                [(SLOT_P3 + g, atr_codes[:, g, b, 0, :], atr_scales[:, g, b, 0, :]) for g in LATER_FIRST],
             )
             along_r = work.tile([P, SMALL], F32, bufs=4)
             nc.vector.scalar_tensor_tensor(
@@ -204,7 +203,7 @@ def tile_layer_3d_dep_pa_kernel(tc, A, P1, P2, P3, P4, a5, gamma, beta, out):
                 a1_ps = pool.tile([P, SLAB], F32, bufs=a1_bufs)
                 passes(
                     a1_ps[:], ot,
-                    [(SLOT_P1 + g, a_codes[:, g, b, slab], a_scales[:, g, b, slab]) for g in range(PASSES)],
+                    [(SLOT_P1 + g, a_codes[:, g, b, slab], a_scales[:, g, b, slab]) for g in LATER_FIRST],
                 )
                 nc.vector.scalar_tensor_tensor(
                     out=y[:, slab], in0=a1_ps[:], scalar=FORTY,
@@ -216,7 +215,7 @@ def tile_layer_3d_dep_pa_kernel(tc, A, P1, P2, P3, P4, a5, gamma, beta, out):
                 a2_ps = psum_mix.tile([P, SLAB], F32, bufs=1)
                 passes(
                     a2_ps[:], ot,
-                    [(SLOT_P2 + g, am_codes[:, g, b_slab], am_scales[:, g, b_slab]) for g in range(PASSES)],
+                    [(SLOT_P2 + g, am_codes[:, g, b_slab], am_scales[:, g, b_slab]) for g in LATER_FIRST],
                 )
                 a2_of[stage] = a2_ps
 
@@ -283,7 +282,6 @@ def tile_layer_3d_dep_pa_kernel(tc, A, P1, P2, P3, P4, a5, gamma, beta, out):
 
             raw_of = {}
             grouped_of = {}
-            by_k_of = {}
             flipped_of = {}
             means_of = {}
             m_sum_of = {}
@@ -309,24 +307,14 @@ def tile_layer_3d_dep_pa_kernel(tc, A, P1, P2, P3, P4, a5, gamma, beta, out):
                         ].rearrange("(p j) w -> p j w", j=PACK),
                     )
                 elif mm == 0:
-                    first = (part // 2) * CHUNK_K * POS_K
-                    nc.sync.dma_start(
-                        out=raw_of[c][:].rearrange("p (q x) -> p q x", q=PACK * M),
-                        in_=a_by_cm[
-                            b, g * K_PASS * M : (g + 1) * K_PASS * M, first : first + CHUNK_K * POS_K
-                        ].rearrange("(p q) x -> p q x", q=PACK * M),
-                    )
-
-            def gather_m(sg):
-                b, g, part = place(sg)
-                c, mm = divmod(sg, 2)
-                if b == 1 and mm == 0:
-                    by_k = stage.tile([P, CHUNK_K, PACK * M, POS_K], BF16, bufs=2)
-                    nc.vector.tensor_copy(
-                        out=by_k[:],
-                        in_=raw_of[c][:].rearrange("p (q k x) -> p k q x", q=PACK * M, k=CHUNK_K),
-                    )
-                    by_k_of[c] = by_k
+                    for kk in range(CHUNK_K):
+                        k = (part // 2) * CHUNK_K + kk
+                        nc.sync.dma_start(
+                            out=raw_of[c][:].rearrange("p (k q x) -> p k q x", k=CHUNK_K, x=POS_K)[:, kk],
+                            in_=a_by_k[
+                                b, k, g * K_PASS * M : (g + 1) * K_PASS * M, :
+                            ].rearrange("(p q) x -> p q x", q=PACK * M),
+                        )
 
             def regroup(sg):
                 c, mm = divmod(sg, 2)
@@ -351,8 +339,8 @@ def tile_layer_3d_dep_pa_kernel(tc, A, P1, P2, P3, P4, a5, gamma, beta, out):
                                 :, m * CHUNK_K * POS_K : (m + 1) * CHUNK_K * POS_K, :
                             ].rearrange("p (k x) j -> p k x j", k=CHUNK_K),
                             in_=raw_of[c][:]
-                            .rearrange("p (j m k x) -> p j m k x", j=PACK, m=M, k=CHUNK_K)[:, :, m]
-                            .rearrange("p j k x -> p k x j"),
+                            .rearrange("p (k j m x) -> p k j m x", k=CHUNK_K, j=PACK, m=M)[:, :, :, m]
+                            .rearrange("p k j x -> p k x j"),
                         )
 
             def quantise(c):
@@ -399,10 +387,7 @@ def tile_layer_3d_dep_pa_kernel(tc, A, P1, P2, P3, P4, a5, gamma, beta, out):
             def turn(sg):
                 b, g, part = place(sg)
                 c, mm = divmod(sg, 2)
-                if b == 0:
-                    raw_words = raw_of[c][:].bitcast(F32)
-                else:
-                    raw_words = by_k_of[c][:].rearrange("p k q x -> p (k q x)").bitcast(F32)
+                raw_words = raw_of[c][:].bitcast(F32)
                 flipped_of[sg] = []
                 for tl in range(TILES):
                     flipped_ps = psum.tile([P, PACK, P], F32, tag="turned")
@@ -437,7 +422,7 @@ def tile_layer_3d_dep_pa_kernel(tc, A, P1, P2, P3, P4, a5, gamma, beta, out):
                         am_tile(b, g)
                 atr_grp = means_of[(b, g)]
                 if b == 0:
-                    mean_ps = psum.tile([P, PACK, 2, TILES, PER_TILE], F32, bufs=1, tag="means")
+                    mean_ps = psum.tile([P, PACK, 2, TILES, PER_TILE], F32, bufs=2, tag="means")
                     for tl in range(TILES):
                         halves = halves_of(sg, tl)
                         for j in range(PACK):
@@ -457,7 +442,7 @@ def tile_layer_3d_dep_pa_kernel(tc, A, P1, P2, P3, P4, a5, gamma, beta, out):
                 for tl in range(STEP_K):
                     k = part * STEP_K + tl
                     halves = halves_of(sg, tl)
-                    sums_ps = psum.tile([P, PACK, P], F32, bufs=1, tag="means")
+                    sums_ps = psum.tile([P, PACK, P], F32, bufs=2, tag="means")
                     for j in range(PACK):
                         for e in range(2):
                             nc.tensor.matmul(
@@ -581,7 +566,6 @@ def tile_layer_3d_dep_pa_kernel(tc, A, P1, P2, P3, P4, a5, gamma, beta, out):
                     load(sg + 4)
                 turn(sg)
                 if sg + 2 < STEPS:
-                    gather_m(sg + 2)
                     regroup(sg + 2)
                 if mm == 0:
                     quantise(c)
@@ -596,7 +580,7 @@ def tile_layer_3d_dep_pa_kernel(tc, A, P1, P2, P3, P4, a5, gamma, beta, out):
                 if sg == 4:
                     turn_gamma_beta()
                 if sg >= STEPS // 2:
-                    unit_step(sg - STEPS // 2, psum, 3)
+                    unit_step(sg - STEPS // 2, psum, 2)
                     relus_up_to(begun(sg - STEPS // 2 - 2), nothing)
                 if sg >= 2:
                     ot, part = divmod(sg - 2, 3)
@@ -608,7 +592,7 @@ def tile_layer_3d_dep_pa_kernel(tc, A, P1, P2, P3, P4, a5, gamma, beta, out):
                             load_weights(ot + 1)
             means(STEPS - 1)
             finish(1, 1)
-            unit_step(N_UNITS // 2, psum, 3)
+            unit_step(N_UNITS // 2, psum, 2)
             relus_up_to(begun(N_UNITS // 2 - 2), nothing)
 
         with ExitStack() as second:
@@ -632,14 +616,11 @@ def tile_layer_3d_dep_pa_kernel(tc, A, P1, P2, P3, P4, a5, gamma, beta, out):
                     scalar2=BN_EPS * FORTY * FORTY * COUNT * COUNT, op0=ALU.mult, op1=ALU.max,
                 )
                 w = work.tile([P, 1], F32)
-                nc.gpsimd.tensor_tensor(out=w[:], in0=spread[:], in1=minus_half[:], op=ALU.pow)
+                nc.scalar.activation(out=w[:], in_=spread[:], func=ACT.Abs_reciprocal_sqrt)
                 gains = work.tile([P, 2], F32)
-                nc.gpsimd.tensor_tensor(
-                    out=gains[:], in0=gamma_pair[:, ot, :], in1=w[:].to_broadcast([P, 2]),
-                    op=ALU.mult,
-                )
+                nc.vector.tensor_scalar_mul(out=gains[:], in0=gamma_pair[:, ot, :], scalar1=w[:])
                 shift = work.tile([P, 1], F32)
-                nc.gpsimd.tensor_scalar(
+                nc.vector.tensor_scalar(
                     out=shift[:], in0=total[:, 0:1], scalar1=gains[:, 1:2],
                     scalar2=gamma_beta[:, O_TILES + ot : O_TILES + ot + 1],
                     op0=ALU.mult, op1=ALU.add,

@@ -19,7 +19,6 @@ P = 128
 PACK = 4
 K_PASS = P * PACK
 PASSES = C // K_PASS
-LATER_FIRST = tuple(reversed(range(PASSES)))
 POS = M * K * NR * NT
 HALF = POS // 2
 SLAB = K * NR * NT
@@ -160,11 +159,11 @@ def tile_layer_3d_dep_pa_kernel(tc, A, P1, P2, P3, P4, a5, gamma, beta, out):
             a43_ps = psum_mix.tile([P, 2, SMALL], F32, bufs=1)
             passes(
                 a43_ps[:, 0, :], ot,
-                [(SLOT_P4 + g, atr_codes[:, g, b, 1, :], atr_scales[:, g, b, 1, :]) for g in LATER_FIRST],
+                [(SLOT_P4 + g, atr_codes[:, g, b, 1, :], atr_scales[:, g, b, 1, :]) for g in range(PASSES)],
             )
             passes(
                 a43_ps[:, 1, :], ot,
-                [(SLOT_P3 + g, atr_codes[:, g, b, 0, :], atr_scales[:, g, b, 0, :]) for g in LATER_FIRST],
+                [(SLOT_P3 + g, atr_codes[:, g, b, 0, :], atr_scales[:, g, b, 0, :]) for g in range(PASSES)],
             )
             along_r = work.tile([P, SMALL], F32, bufs=4)
             nc.vector.scalar_tensor_tensor(
@@ -203,7 +202,7 @@ def tile_layer_3d_dep_pa_kernel(tc, A, P1, P2, P3, P4, a5, gamma, beta, out):
                 a1_ps = pool.tile([P, SLAB], F32, bufs=a1_bufs)
                 passes(
                     a1_ps[:], ot,
-                    [(SLOT_P1 + g, a_codes[:, g, b, slab], a_scales[:, g, b, slab]) for g in LATER_FIRST],
+                    [(SLOT_P1 + g, a_codes[:, g, b, slab], a_scales[:, g, b, slab]) for g in range(PASSES)],
                 )
                 nc.vector.scalar_tensor_tensor(
                     out=y[:, slab], in0=a1_ps[:], scalar=FORTY,
@@ -215,7 +214,7 @@ def tile_layer_3d_dep_pa_kernel(tc, A, P1, P2, P3, P4, a5, gamma, beta, out):
                 a2_ps = psum_mix.tile([P, SLAB], F32, bufs=1)
                 passes(
                     a2_ps[:], ot,
-                    [(SLOT_P2 + g, am_codes[:, g, b_slab], am_scales[:, g, b_slab]) for g in LATER_FIRST],
+                    [(SLOT_P2 + g, am_codes[:, g, b_slab], am_scales[:, g, b_slab]) for g in range(PASSES)],
                 )
                 a2_of[stage] = a2_ps
 
@@ -514,7 +513,7 @@ def tile_layer_3d_dep_pa_kernel(tc, A, P1, P2, P3, P4, a5, gamma, beta, out):
                 )
 
             def load_weights(ot):
-                w_raw = stage.tile([P, N_W * C], BF16, bufs=1)
+                w_raw = stage.tile([P, N_W * C], BF16, bufs=2)
                 for which in range(N_W):
                     nc.sync.dma_start(
                         out=w_raw[:, which * C : (which + 1) * C],
@@ -586,10 +585,10 @@ def tile_layer_3d_dep_pa_kernel(tc, A, P1, P2, P3, P4, a5, gamma, beta, out):
                     ot, part = divmod(sg - 2, 3)
                     if ot < O_TILES and part < 2:
                         turn_weights(ot, part)
+                    if part == 0 and ot + 1 < O_TILES:
+                        load_weights(ot + 1)
                     if ot < O_TILES and part == 1:
                         quantise_weights(ot)
-                        if ot + 1 < O_TILES:
-                            load_weights(ot + 1)
             means(STEPS - 1)
             finish(1, 1)
             unit_step(N_UNITS // 2, psum, 2)

@@ -32,9 +32,10 @@ CHUNK_K = 2 * STEP_K
 PER_TILE = TILE_POS // NT
 TP = NT // 2
 N_W = 4
-FORTY = 40.0
-SLOT_P1, SLOT_P2, SLOT_P3, SLOT_P4 = 0, 2, 4, 6
-N_SLOTS = 8
+FIVE = 5.0
+SLOT_P1, SLOT_P2, SLOT_P3, SLOT_P4, SLOT_4P1 = 0, 2, 4, 6, 8
+N_SLOTS = 10
+AM_SCALE = FIVE * 0.1 / M
 STEPS = B * PASSES * M
 N_UNITS = 2 * B * O_TILES
 LAG = 2
@@ -95,7 +96,7 @@ def tile_layer_3d_dep_pa_kernel(tc, A, P1, P2, P3, P4, a5, gamma, beta, out):
                 op=ALU.add,
             )
         mean_w = keep.tile([P, 2, 2 * PER_TILE], BF16)
-        for first, factor in ((0, M / NT), (PER_TILE, 1.0 / NR)):
+        for first, factor in ((0, 0.1 * FIVE / NT), (PER_TILE, 1.0 / NR)):
             nc.vector.tensor_scalar_mul(
                 out=mean_w[:, :, first : first + PER_TILE],
                 in0=member[:, :, first : first + PER_TILE],
@@ -115,17 +116,25 @@ def tile_layer_3d_dep_pa_kernel(tc, A, P1, P2, P3, P4, a5, gamma, beta, out):
             axis=AXIS_X,
             op=ALU.add,
         )
-        rm_w = keep.tile([P, 3 * PER_TILE // 2], BF16)
-        for first, last, factor in ((0, PER_TILE // 2, 1.0 / NR), (PER_TILE // 2, 3 * PER_TILE // 2, 1.0)):
-            nc.vector.tensor_scalar_mul(
-                out=rm_w[:, first:last], in0=rm_member[:, first:last], scalar1=factor
-            )
+        rm_w = keep.tile([P, B, 3 * PER_TILE // 2], BF16)
+        for b in range(B):
+            for first, last, factor in (
+                (0, PER_TILE // 2, 1.0 / NR), (PER_TILE // 2, 3 * PER_TILE // 2, (1.0, AM_SCALE)[b])
+            ):
+                nc.vector.tensor_scalar_mul(
+                    out=rm_w[:, b, first:last], in0=rm_member[:, first:last], scalar1=factor
+                )
 
         nc.vector.memset(sums[:, :, :, UNITS], 0.0)
         nc.vector.tensor_scalar_add(
             out=sums[:, :, 1, UNITS], in0=sums[:, :, 1, UNITS],
-            scalar1=BN_EPS * FORTY * FORTY * COUNT * COUNT,
+            scalar1=BN_EPS * FIVE * FIVE * COUNT * COUNT,
         )
+
+        one = keep.tile([P, 1], F32)
+        nc.gpsimd.memset(one[:], 1.0)
+        root_of_one = keep.tile([P, 1], F32)
+        nc.scalar.activation(out=root_of_one[:], in_=one[:], func=ACT.Abs_reciprocal_sqrt)
 
         gb_rows = keep.tile([P, P], BF16)
         nc.vector.memset(gb_rows[:], 0.0)
@@ -154,9 +163,9 @@ def tile_layer_3d_dep_pa_kernel(tc, A, P1, P2, P3, P4, a5, gamma, beta, out):
             b, ot = divmod(stage, O_TILES)
             return stage, b, ot, hm
 
-        def mix_pooled(stage):
+        def mix_pooled(stage, pool, pooled_tag, pooled_bufs):
             b, ot = divmod(stage, O_TILES)
-            a43_ps = psum_mix.tile([P, 2, SMALL], F32, bufs=1)
+            a43_ps = pool.tile([P, 2, SMALL], F32, bufs=pooled_bufs, tag=pooled_tag)
             passes(
                 a43_ps[:, 0, :], ot,
                 [(SLOT_P4 + g, atr_codes[:, g, b, 1, :], atr_scales[:, g, b, 1, :]) for g in range(PASSES)],
@@ -167,7 +176,7 @@ def tile_layer_3d_dep_pa_kernel(tc, A, P1, P2, P3, P4, a5, gamma, beta, out):
             )
             along_r = work.tile([P, SMALL], F32, bufs=4)
             nc.vector.scalar_tensor_tensor(
-                out=along_r[:], in0=a43_ps[:, 0, :], scalar=0.5 * FORTY, in1=a5_scaled[:, ot, b, :],
+                out=along_r[:], in0=a43_ps[:, 0, :], scalar=0.5 * FIVE, in1=a5_scaled[:, ot, b, :],
                 op0=ALU.mult, op1=ALU.add,
             )
             along_t = work.tile([P, SMALL], F32, bufs=4)
@@ -194,37 +203,46 @@ def tile_layer_3d_dep_pa_kernel(tc, A, P1, P2, P3, P4, a5, gamma, beta, out):
                 )
                 terms_of[(n, m)] = terms
 
+        def a2_apart(stage):
+            return stage < 2 * O_TILES - 3
+
         def mix(n, pool, a1_bufs):
             stage, b, ot, hm = where(n)
             y = y_of[stage]
+            b_slab = slice(b * SLAB, (b + 1) * SLAB)
+            a2 = [(SLOT_P2 + g, am_codes[:, g, b_slab], am_scales[:, g, b_slab]) for g in range(PASSES)]
+            apart = a2_apart(stage)
             for m in (2 * hm, 2 * hm + 1):
                 slab = slice(m * SLAB, (m + 1) * SLAB)
                 a1_ps = pool.tile([P, SLAB], F32, bufs=a1_bufs)
-                passes(
-                    a1_ps[:], ot,
-                    [(SLOT_P1 + g, a_codes[:, g, b, slab], a_scales[:, g, b, slab]) for g in range(PASSES)],
-                )
-                nc.vector.scalar_tensor_tensor(
-                    out=y[:, slab], in0=a1_ps[:], scalar=FORTY,
-                    in1=terms_of[(n, m)][:].rearrange("o k r t -> o (k r t)"),
-                    op0=ALU.mult, op1=ALU.add,
-                )
-            if hm == 0:
-                b_slab = slice(b * SLAB, (b + 1) * SLAB)
+                a1 = [
+                    (slot + g, a_codes[:, g, b, slab], a_scales[:, g, b, slab])
+                    for slot in ((SLOT_P1,) if apart else (SLOT_P1, SLOT_4P1))
+                    for g in range(PASSES)
+                ]
+                passes(a1_ps[:], ot, a1 if apart else a2 + a1)
+                terms = terms_of[(n, m)][:].rearrange("o k r t -> o (k r t)")
+                if apart:
+                    nc.vector.scalar_tensor_tensor(
+                        out=y[:, slab], in0=a1_ps[:], scalar=FIVE, in1=terms, op0=ALU.mult, op1=ALU.add,
+                    )
+                else:
+                    nc.vector.tensor_tensor(out=y[:, slab], in0=a1_ps[:], in1=terms, op=ALU.add)
+            if apart and hm == 0:
                 a2_ps = psum_mix.tile([P, SLAB], F32, bufs=1)
-                passes(
-                    a2_ps[:], ot,
-                    [(SLOT_P2 + g, am_codes[:, g, b_slab], am_scales[:, g, b_slab]) for g in range(PASSES)],
-                )
+                passes(a2_ps[:], ot, a2)
                 a2_of[stage] = a2_ps
 
         def add_over_m(n):
             stage, b, ot, hm = where(n)
+            if not a2_apart(stage):
+                return
             half = y_of[stage][:, hm * HALF : (hm + 1) * HALF].rearrange("o (m x) -> o m x", x=SLAB)
-            nc.vector.tensor_tensor(
+            nc.vector.scalar_tensor_tensor(
                 out=half,
                 in0=a2_of[stage][:].unsqueeze(1).to_broadcast([P, 2, SLAB]),
-                in1=half, op=ALU.add,
+                scalar=(AM_SCALE, 1.0)[b],
+                in1=half, op0=ALU.mult, op1=ALU.add,
             )
 
         def relu(n):
@@ -264,10 +282,10 @@ def tile_layer_3d_dep_pa_kernel(tc, A, P1, P2, P3, P4, a5, gamma, beta, out):
             n = step - LAG
             return n if 0 <= n < N_UNITS else None
 
-        def unit_step(step, pool, a1_bufs):
+        def unit_step(step, pool, a1_bufs, pooled_tag, pooled_bufs):
             ahead = begun(step + 1)
             if ahead is not None and ahead % 2 == 0:
-                mix_pooled(ahead // 2)
+                mix_pooled(ahead // 2, pool, pooled_tag, pooled_bufs)
             if ahead is not None:
                 add_small_terms(ahead)
             if begun(step) is not None:
@@ -389,7 +407,7 @@ def tile_layer_3d_dep_pa_kernel(tc, A, P1, P2, P3, P4, a5, gamma, beta, out):
                 raw_words = raw_of[c][:].bitcast(F32)
                 flipped_of[sg] = []
                 for tl in range(TILES):
-                    flipped_ps = psum.tile([P, PACK, P], F32, tag="turned")
+                    flipped_ps = psum.tile([P, PACK, P], F32, tag="turned", bufs=3)
                     for j in range(PACK):
                         if b == 0:
                             first = ((mm * PACK + j) * TILES + tl) * P
@@ -401,7 +419,7 @@ def tile_layer_3d_dep_pa_kernel(tc, A, P1, P2, P3, P4, a5, gamma, beta, out):
                             identity=ident_f32[:],
                         )
                     flipped = stage.tile([P, PACK, P], F32, bufs=4)
-                    nc.scalar.copy(out=flipped[:], in_=flipped_ps[:])
+                    (nc.vector.tensor_copy if sg >= STEPS // 2 and tl == 1 and sg % 2 == 1 else nc.scalar.copy)(out=flipped[:], in_=flipped_ps[:])
                     flipped_of[sg].append(flipped)
 
             def halves_of(sg, tl):
@@ -455,7 +473,7 @@ def tile_layer_3d_dep_pa_kernel(tc, A, P1, P2, P3, P4, a5, gamma, beta, out):
                             nc.tensor.matmul(
                                 out=sums_ps[:, j, PER_TILE + e : P : 2],
                                 lhsT=halves[:, j, :, e],
-                                rhs=rm_w[:],
+                                rhs=rm_w[:, b, :],
                                 start=True,
                                 stop=True,
                             )
@@ -471,16 +489,16 @@ def tile_layer_3d_dep_pa_kernel(tc, A, P1, P2, P3, P4, a5, gamma, beta, out):
                     )
 
             def finish(b, g):
+                nc.vector.quantize_mx(
+                    out=atr_codes[:, g, b, :, :].rearrange("p w n -> p (w n)").bitcast(FP8X4),
+                    scales=atr_scales[:, g, b, :, :].rearrange("p w n -> p (w n)"),
+                    in_=means_of[(b, g)][:].rearrange("p w k n j -> p (w k n j)"),
+                )
                 am_grp = am_of[(b, g)]
                 nc.vector.quantize_mx(
                     out=am_codes[:, g, b * SLAB : (b + 1) * SLAB].bitcast(FP8X4),
                     scales=am_scales[:, g, b * SLAB : (b + 1) * SLAB],
                     in_=am_grp[:],
-                )
-                nc.vector.quantize_mx(
-                    out=atr_codes[:, g, b, :, :].rearrange("p w n -> p (w n)").bitcast(FP8X4),
-                    scales=atr_scales[:, g, b, :, :].rearrange("p w n -> p (w n)"),
-                    in_=means_of[(b, g)][:].rearrange("p w k n j -> p (w k n j)"),
                 )
 
             def small_inputs():
@@ -498,11 +516,11 @@ def tile_layer_3d_dep_pa_kernel(tc, A, P1, P2, P3, P4, a5, gamma, beta, out):
                 nc.gpsimd.tensor_scalar(
                     out=a5_scaled[:].rearrange("o t b x -> o (t b x)"),
                     in0=a5_sb[:].rearrange("o t b x -> o (t b x)"),
-                    scalar1=2.0 * FORTY, scalar2=0.0, op0=ALU.mult, op1=ALU.add,
+                    scalar1=2.0 * FIVE, scalar2=0.0, op0=ALU.mult, op1=ALU.add,
                 )
 
             def turn_gamma_beta():
-                gb_ps = psum.tile([P, P], BF16, tag="turned")
+                gb_ps = psum.tile([P, P], BF16, tag="turned", bufs=3)
                 nc.tensor.transpose(out=gb_ps[:], in_=gb_rows[:], identity=ident_bf[:])
                 nc.vector.tensor_copy(out=gamma_beta[:], in_=gb_ps[:, 0 : 2 * O_TILES])
                 nc.vector.tensor_scalar_mul(
@@ -532,7 +550,7 @@ def tile_layer_3d_dep_pa_kernel(tc, A, P1, P2, P3, P4, a5, gamma, beta, out):
                 for half in range(2):
                     which = 2 * pair + half
                     first_slot = which * PASSES
-                    wt_ps = psum.tile([P, PASSES, 2, P], F32, tag="turned")
+                    wt_ps = psum.tile([P, PASSES, 2, P], F32, tag="turned", bufs=3)
                     for g in range(PASSES):
                         for u in range(2):
                             nc.tensor.transpose(
@@ -544,13 +562,21 @@ def tile_layer_3d_dep_pa_kernel(tc, A, P1, P2, P3, P4, a5, gamma, beta, out):
                         out=target_words[:, first_slot : first_slot + PASSES, :, :],
                         in_=wt_ps[:].rearrange("p g u o -> p g o u"),
                     )
+                if pair == 0 and ot >= 1:
+                    cols = PASSES * P * PACK
+                    nc.vector.tensor_scalar_mul(
+                        out=w_grp_of[ot][:, SLOT_4P1 * P * PACK : SLOT_4P1 * P * PACK + cols],
+                        in0=w_grp_of[ot][:, SLOT_P1 * P * PACK : SLOT_P1 * P * PACK + cols],
+                        scalar1=4.0,
+                    )
 
             def quantise_weights(ot):
-                nc.vector.quantize_mx(
-                    out=w_codes[:, ot, :, :].rearrange("p s o -> p (s o)").bitcast(FP8X4),
-                    scales=w_scales[:, ot, :, :].rearrange("p s o -> p (s o)"),
-                    in_=w_grp_of[ot][:],
-                )
+                for first, last in ((0, SLOT_4P1), (SLOT_4P1, N_SLOTS))[: 2 if ot >= 1 else 1]:
+                    nc.vector.quantize_mx(
+                        out=w_codes[:, ot, first:last, :].rearrange("p s o -> p (s o)").bitcast(FP8X4),
+                        scales=w_scales[:, ot, first:last, :].rearrange("p s o -> p (s o)"),
+                        in_=w_grp_of[ot][:, first * P * PACK : last * P * PACK],
+                    )
 
             for ot in range(O_TILES):
                 y_of[ot] = y_first[:, ot, :]
@@ -579,7 +605,7 @@ def tile_layer_3d_dep_pa_kernel(tc, A, P1, P2, P3, P4, a5, gamma, beta, out):
                 if sg == 4:
                     turn_gamma_beta()
                 if sg >= STEPS // 2:
-                    unit_step(sg - STEPS // 2, psum, 2)
+                    unit_step(sg - STEPS // 2, psum, 2, "means", 2)
                     relus_up_to(begun(sg - STEPS // 2 - 2), nothing)
                 if sg >= 2:
                     ot, part = divmod(sg - 2, 3)
@@ -591,7 +617,7 @@ def tile_layer_3d_dep_pa_kernel(tc, A, P1, P2, P3, P4, a5, gamma, beta, out):
                         quantise_weights(ot)
             means(STEPS - 1)
             finish(1, 1)
-            unit_step(N_UNITS // 2, psum, 2)
+            unit_step(N_UNITS // 2, psum, 2, "means", 2)
             relus_up_to(begun(N_UNITS // 2 - 2), nothing)
 
         with ExitStack() as second:
@@ -612,34 +638,37 @@ def tile_layer_3d_dep_pa_kernel(tc, A, P1, P2, P3, P4, a5, gamma, beta, out):
                 spread = work.tile([P, 1], F32)
                 nc.vector.tensor_scalar(
                     out=spread[:], in0=minus_spread[:], scalar1=-1.0,
-                    scalar2=BN_EPS * FORTY * FORTY * COUNT * COUNT, op0=ALU.mult, op1=ALU.max,
+                    scalar2=BN_EPS * FIVE * FIVE * COUNT * COUNT, op0=ALU.mult, op1=ALU.max,
                 )
                 w = work.tile([P, 1], F32)
                 nc.scalar.activation(out=w[:], in_=spread[:], func=ACT.Abs_reciprocal_sqrt)
-                gains = work.tile([P, 2], F32)
-                nc.vector.tensor_scalar_mul(out=gains[:], in0=gamma_pair[:, ot, :], scalar1=w[:])
+                minus_mean = work.tile([P, 1], F32)
+                nc.vector.tensor_scalar_mul(
+                    out=minus_mean[:], in0=total[:, 0:1], scalar1=gamma_pair[:, ot, 1:2]
+                )
+                gain = work.tile([P, 1], F32)
+                nc.vector.tensor_scalar_mul(out=gain[:], in0=w[:], scalar1=gamma_pair[:, ot, 0:1])
                 shift = work.tile([P, 1], F32)
                 nc.vector.tensor_scalar(
-                    out=shift[:], in0=total[:, 0:1], scalar1=gains[:, 1:2],
+                    out=shift[:], in0=w[:], scalar1=minus_mean[:],
                     scalar2=gamma_beta[:, O_TILES + ot : O_TILES + ot + 1],
                     op0=ALU.mult, op1=ALU.add,
                 )
-                affine_of[ot] = (gains[:, 0:1], shift[:])
+                affine_of[ot] = (gain[:], shift[:])
 
             def normalise_and_store(ot, b):
                 gain, shift = affine_of[ot]
                 y = y_of[b * O_TILES + ot]
-                on_vector = b == 0 or ot == O_TILES - 2
+                engine = "V" if b == 0 or ot < O_TILES - 1 else "S"
                 for hm in range(2):
                     half = slice(hm * HALF, (hm + 1) * HALF)
-                    if b == 1 and not on_vector:
+                    if engine == "S":
                         nc.scalar.activation(
                             out=y[:, half], in_=y[:, half], func=ACT.Identity,
                             scale=gain, bias=shift,
                         )
                     else:
-                        engine = nc.vector if on_vector else nc.gpsimd
-                        engine.tensor_scalar(
+                        (nc.vector if engine == "V" else nc.gpsimd).tensor_scalar(
                             out=y[:, half], in0=y[:, half],
                             scalar1=gain, scalar2=shift, op0=ALU.mult, op1=ALU.add,
                         )
@@ -658,6 +687,6 @@ def tile_layer_3d_dep_pa_kernel(tc, A, P1, P2, P3, P4, a5, gamma, beta, out):
                 if n is not None and n % 2 == 0:
                     y_second = late.tile([P, POS], F32)
                     y_of[n // 2] = y_second[:]
-                unit_step(step, psum, 6)
+                unit_step(step, psum, 7, "a1_ps", 7)
                 relus_up_to(step - LAG - 1, after_square)
             normalise_and_store(O_TILES - 1, 1)

@@ -36,6 +36,7 @@ FIVE = 5.0
 SLOT_P1, SLOT_P2, SLOT_P3, SLOT_P4, SLOT_4P1 = 0, 2, 4, 6, 8
 N_SLOTS = 10
 AM_SCALE = FIVE * 0.1 / M
+A2_IN_BANK = 3
 STEPS = B * PASSES * M
 N_UNITS = 2 * B * O_TILES
 LAG = 2
@@ -116,14 +117,13 @@ def tile_layer_3d_dep_pa_kernel(tc, A, P1, P2, P3, P4, a5, gamma, beta, out):
             axis=AXIS_X,
             op=ALU.add,
         )
-        rm_w = keep.tile([P, B, 3 * PER_TILE // 2], BF16)
-        for b in range(B):
-            for first, last, factor in (
-                (0, PER_TILE // 2, 1.0 / NR), (PER_TILE // 2, 3 * PER_TILE // 2, (1.0, AM_SCALE)[b])
-            ):
-                nc.vector.tensor_scalar_mul(
-                    out=rm_w[:, b, first:last], in0=rm_member[:, first:last], scalar1=factor
-                )
+        rm_w = keep.tile([P, 3 * PER_TILE // 2], BF16)
+        for first, last, factor in (
+            (0, PER_TILE // 2, 1.0 / NR), (PER_TILE // 2, 3 * PER_TILE // 2, AM_SCALE)
+        ):
+            nc.vector.tensor_scalar_mul(
+                out=rm_w[:, first:last], in0=rm_member[:, first:last], scalar1=factor
+            )
 
         nc.vector.memset(sums[:, :, :, UNITS], 0.0)
         nc.vector.tensor_scalar_add(
@@ -204,7 +204,7 @@ def tile_layer_3d_dep_pa_kernel(tc, A, P1, P2, P3, P4, a5, gamma, beta, out):
                 terms_of[(n, m)] = terms
 
         def a2_apart(stage):
-            return stage < 2 * O_TILES - 3
+            return stage < B * O_TILES - A2_IN_BANK
 
         def mix(n, pool, a1_bufs):
             stage, b, ot, hm = where(n)
@@ -419,7 +419,10 @@ def tile_layer_3d_dep_pa_kernel(tc, A, P1, P2, P3, P4, a5, gamma, beta, out):
                             identity=ident_f32[:],
                         )
                     flipped = stage.tile([P, PACK, P], F32, bufs=4)
-                    (nc.vector.tensor_copy if sg >= STEPS // 2 and tl == 1 and sg % 2 == 1 else nc.scalar.copy)(out=flipped[:], in_=flipped_ps[:])
+                    on_vector = b == 1 and sg % 2 == 1 and tl == 1
+                    (nc.vector.tensor_copy if on_vector else nc.scalar.copy)(
+                        out=flipped[:], in_=flipped_ps[:]
+                    )
                     flipped_of[sg].append(flipped)
 
             def halves_of(sg, tl):
@@ -473,7 +476,7 @@ def tile_layer_3d_dep_pa_kernel(tc, A, P1, P2, P3, P4, a5, gamma, beta, out):
                             nc.tensor.matmul(
                                 out=sums_ps[:, j, PER_TILE + e : P : 2],
                                 lhsT=halves[:, j, :, e],
-                                rhs=rm_w[:, b, :],
+                                rhs=rm_w[:],
                                 start=True,
                                 stop=True,
                             )
@@ -530,6 +533,9 @@ def tile_layer_3d_dep_pa_kernel(tc, A, P1, P2, P3, P4, a5, gamma, beta, out):
                     out=gamma_pair[:, :, 1], in0=gamma_beta[:, 0:O_TILES], scalar1=-1.0
                 )
 
+            def has_4p1(ot):
+                return not a2_apart(O_TILES + ot)
+
             def load_weights(ot):
                 w_raw = stage.tile([P, N_W * C], BF16, bufs=2)
                 for which in range(N_W):
@@ -562,7 +568,7 @@ def tile_layer_3d_dep_pa_kernel(tc, A, P1, P2, P3, P4, a5, gamma, beta, out):
                         out=target_words[:, first_slot : first_slot + PASSES, :, :],
                         in_=wt_ps[:].rearrange("p g u o -> p g o u"),
                     )
-                if pair == 0 and ot >= 1:
+                if pair == 0 and has_4p1(ot):
                     cols = PASSES * P * PACK
                     nc.vector.tensor_scalar_mul(
                         out=w_grp_of[ot][:, SLOT_4P1 * P * PACK : SLOT_4P1 * P * PACK + cols],
@@ -571,7 +577,7 @@ def tile_layer_3d_dep_pa_kernel(tc, A, P1, P2, P3, P4, a5, gamma, beta, out):
                     )
 
             def quantise_weights(ot):
-                for first, last in ((0, SLOT_4P1), (SLOT_4P1, N_SLOTS))[: 2 if ot >= 1 else 1]:
+                for first, last in [(0, SLOT_4P1)] + [(SLOT_4P1, N_SLOTS)] * has_4p1(ot):
                     nc.vector.quantize_mx(
                         out=w_codes[:, ot, first:last, :].rearrange("p s o -> p (s o)").bitcast(FP8X4),
                         scales=w_scales[:, ot, first:last, :].rearrange("p s o -> p (s o)"),
@@ -659,16 +665,16 @@ def tile_layer_3d_dep_pa_kernel(tc, A, P1, P2, P3, P4, a5, gamma, beta, out):
             def normalise_and_store(ot, b):
                 gain, shift = affine_of[ot]
                 y = y_of[b * O_TILES + ot]
-                engine = "V" if b == 0 or ot < O_TILES - 1 else "S"
+                on_scalar = b == 1 and ot == O_TILES - 1
                 for hm in range(2):
                     half = slice(hm * HALF, (hm + 1) * HALF)
-                    if engine == "S":
+                    if on_scalar:
                         nc.scalar.activation(
                             out=y[:, half], in_=y[:, half], func=ACT.Identity,
                             scale=gain, bias=shift,
                         )
                     else:
-                        (nc.vector if engine == "V" else nc.gpsimd).tensor_scalar(
+                        nc.vector.tensor_scalar(
                             out=y[:, half], in0=y[:, half],
                             scalar1=gain, scalar2=shift, op0=ALU.mult, op1=ALU.add,
                         )

from contextlib import ExitStack

import concourse.mybir as mybir
from concourse.masks import make_identity

F32 = mybir.dt.float32
BF16 = mybir.dt.bfloat16
U32 = mybir.dt.uint32
U8 = mybir.dt.uint8
FP8X4 = mybir.dt.float8_e4m3fn_x4
ALU = mybir.AluOpType
ACT = mybir.ActivationFunctionType
AXIS_X = mybir.AxisListType.X

B, C, O, M, K, NR, NT = 2, 1024, 512, 4, 8, 8, 8
BN_EPS = 1e-5

P = 128
PACK = 4
K_PASS = P * PACK
PASSES = C // K_PASS
POS = M * K * NR * NT
HALF = POS // 2
SLAB = K * NR * NT
SMALL = M * K * NT
O_TILES = O // P
TILE_POS = 2 * P
TILES = SLAB // TILE_POS
POS_K = NR * NT
STEP_K = TILES
CHUNK_K = 2 * STEP_K
PER_TILE = TILE_POS // NT
TP = NT // 2
N_W = 4
FIVE = 5.0
SLOT_P1, SLOT_P2, SLOT_P3, SLOT_P4, SLOT_4P1 = 0, 2, 4, 6, 8
N_SLOTS = 10
AM_SCALE = FIVE * 0.1 / M
A2_IN_BANK = 3
STEPS = B * PASSES * M
N_UNITS = 2 * B * O_TILES
LAG = 2
COUNT = B * POS
ROOT_COUNT = 64.0
assert ROOT_COUNT * ROOT_COUNT == COUNT
UNITS = 2 * B

FLOPS = 2 * O * C * B * (POS + SLAB + 2 * SMALL)


def tile_layer_3d_dep_pa_kernel(tc, A, P1, P2, P3, P4, a5, gamma, beta, out):
    nc = tc.nc
    a_rows = A.rearrange("b c m k r t -> b c (m k r t)")
    a_by_k = A.rearrange("b c m k r t -> b k (c m) (r t)")
    a5_rows = a5.rearrange("b o m k t -> b o (m k t)")
    out_rows = out.rearrange("b o m k r t -> b o (m k r t)")
    weights = (P1, P2, P3, P4)

    with ExitStack() as whole:
        keep = whole.enter_context(tc.tile_pool(name="keep", bufs=1))
        work = whole.enter_context(tc.tile_pool(name="work", bufs=2))
        psum_mix = whole.enter_context(tc.psum_pool(name="psum_mix", bufs=1))

        a_codes = keep.tile([P, PASSES, B, POS], U32, align_bytes=64)
        a_scales = keep.tile([P, PASSES, B, POS], U8, align_bytes=64)
        am_codes = keep.tile([P, PASSES, B * SLAB], U32, align_bytes=64)
        am_scales = keep.tile([P, PASSES, B * SLAB], U8, align_bytes=64)
        atr_codes = keep.tile([P, PASSES, B, 2, SMALL], U32, align_bytes=64)
        atr_scales = keep.tile([P, PASSES, B, 2, SMALL], U8, align_bytes=64)
        w_codes = keep.tile([P, O_TILES, N_SLOTS, P], U32, align_bytes=64)
        w_scales = keep.tile([P, O_TILES, N_SLOTS, P], U8, align_bytes=64)

        y_first = keep.tile([P, O_TILES, POS], F32)
        sums = keep.tile([P, O_TILES, 2, UNITS + 1], F32)
        gamma_pair = keep.tile([P, O_TILES, 2], F32)

        ident_f32 = keep.tile([P, P], F32)
        make_identity(nc, ident_f32[:])
        ident_bf = keep.tile([P, P], BF16)
        nc.vector.tensor_copy(out=ident_bf[:], in_=ident_f32[:])

        member = keep.tile([P, 2, 2 * PER_TILE], F32)
        nc.vector.memset(member[:], 0.0)
        for e in range(2):
            nc.vector.tensor_reduce(
                out=member[:, e, 0:PER_TILE],
                in_=ident_f32[:].rearrange("q (n tp) -> q n tp", tp=TP),
                axis=AXIS_X,
                op=ALU.add,
            )
            nc.vector.tensor_reduce(
                out=member[:, e, PER_TILE : 2 * PER_TILE].rearrange(
                    "q (k tp e2) -> q k tp e2", tp=TP, e2=2
                )[:, :, :, e],
                in_=ident_f32[:].rearrange("q (k r tp) -> q k tp r", r=NR, tp=TP),
                axis=AXIS_X,
                op=ALU.add,
            )
        mean_w = keep.tile([P, 2, 2 * PER_TILE], BF16)
        for first, factor in ((0, 0.1 * FIVE / NT), (PER_TILE, 1.0 / NR)):
            nc.vector.tensor_scalar_mul(
                out=mean_w[:, :, first : first + PER_TILE],
                in0=member[:, :, first : first + PER_TILE],
                scalar1=factor,
            )

        rm_member = keep.tile([P, 3 * PER_TILE // 2], F32)
        nc.vector.tensor_reduce(
            out=rm_member[:, 0 : PER_TILE // 2].rearrange("q (m tp) -> q m tp", tp=TP),
            in_=ident_f32[:].rearrange("q (m r tp) -> q m tp r", r=NR, tp=TP),
            axis=AXIS_X,
            op=ALU.add,
        )
        nc.vector.tensor_reduce(
            out=rm_member[:, PER_TILE // 2 : 3 * PER_TILE // 2],
            in_=ident_f32[:].rearrange("q (m x) -> q x m", m=M),
            axis=AXIS_X,
            op=ALU.add,
        )
        rm_w = keep.tile([P, 3 * PER_TILE // 2], BF16)
        for first, last, factor in (
            (0, PER_TILE // 2, 1.0 / NR), (PER_TILE // 2, 3 * PER_TILE // 2, AM_SCALE)
        ):
            nc.vector.tensor_scalar_mul(
                out=rm_w[:, first:last], in0=rm_member[:, first:last], scalar1=factor
            )

        nc.vector.memset(sums[:, :, :, UNITS], 0.0)
        nc.vector.tensor_scalar_add(
            out=sums[:, :, 1, UNITS], in0=sums[:, :, 1, UNITS],
            scalar1=BN_EPS * FIVE * FIVE * COUNT * COUNT,
        )

        one = keep.tile([P, 1], F32)
        nc.gpsimd.memset(one[:], 1.0)
        root_of_one = keep.tile([P, 1], F32)
        nc.scalar.activation(out=root_of_one[:], in_=one[:], func=ACT.Abs_reciprocal_sqrt)

        gb_rows = keep.tile([P, P], BF16)
        nc.vector.memset(gb_rows[:], 0.0)
        gamma_beta = keep.tile([P, 2 * O_TILES], F32)
        a5_scaled = keep.tile([P, O_TILES, B, SMALL], F32)

        def passes(acc, ot, operands):
            for i, (slot, x_codes, x_scales) in enumerate(operands):
                nc.tensor.matmul_mx(
                    out=acc,
                    lhsT=w_codes[:, ot, slot, :].bitcast(FP8X4),
                    lhsT_scale=w_scales[:, ot, slot, :],
                    rhs=x_codes.bitcast(FP8X4),
                    rhs_scale=x_scales,
                    start=(i == 0),
                    stop=(i == len(operands) - 1),
                )

        a2_of = {}
        small_of = {}
        terms_of = {}
        y_of = {}

        def where(n):
            stage, hm = divmod(n, 2)
            b, ot = divmod(stage, O_TILES)
            return stage, b, ot, hm

        def mix_pooled(stage, pool, pooled_tag, pooled_bufs):
            b, ot = divmod(stage, O_TILES)
            a43_ps = pool.tile([P, 2, SMALL], F32, bufs=pooled_bufs, tag=pooled_tag)
            passes(
                a43_ps[:, 0, :], ot,
                [(SLOT_P4 + g, atr_codes[:, g, b, 1, :], atr_scales[:, g, b, 1, :]) for g in range(PASSES)],
            )
            passes(
                a43_ps[:, 1, :], ot,
                [(SLOT_P3 + g, atr_codes[:, g, b, 0, :], atr_scales[:, g, b, 0, :]) for g in range(PASSES)],
            )
            along_r = work.tile([P, SMALL], F32, bufs=4)
            nc.vector.scalar_tensor_tensor(
                out=along_r[:], in0=a43_ps[:, 0, :], scalar=0.5 * FIVE, in1=a5_scaled[:, ot, b, :],
                op0=ALU.mult, op1=ALU.add,
            )
            along_t = work.tile([P, SMALL], F32, bufs=4)
            nc.scalar.copy(out=along_t[:], in_=a43_ps[:, 1, :])
            small_of[stage] = (along_r, along_t)

        def add_small_terms(n):
            stage, b, ot, hm = where(n)
            along_r, along_t = small_of[stage]
            for m in (2 * hm, 2 * hm + 1):
                terms = work.tile([P, K, NR, NT], F32, bufs=4)
                mine = slice(m * K * NT, (m + 1) * K * NT)
                nc.gpsimd.tensor_tensor(
                    out=terms[:],
                    in0=along_t[:, mine]
                    .rearrange("o (k r) -> o k r", r=NR)
                    .unsqueeze(3)
                    .to_broadcast([P, K, NR, NT]),
                    in1=along_r[:, mine]
                    .rearrange("o (k t) -> o k t", t=NT)
                    .unsqueeze(2)
                    .to_broadcast([P, K, NR, NT]),
                    op=ALU.add,
                )
                terms_of[(n, m)] = terms

        def a2_apart(stage):
            return stage < B * O_TILES - A2_IN_BANK

        def mix(n, pool, a1_bufs):
            stage, b, ot, hm = where(n)
            y = y_of[stage]
            b_slab = slice(b * SLAB, (b + 1) * SLAB)
            a2 = [(SLOT_P2 + g, am_codes[:, g, b_slab], am_scales[:, g, b_slab]) for g in range(PASSES)]
            apart = a2_apart(stage)
            for m in (2 * hm, 2 * hm + 1):
                slab = slice(m * SLAB, (m + 1) * SLAB)
                a1_ps = pool.tile([P, SLAB], F32, bufs=a1_bufs)
                a1 = [
                    (slot + g, a_codes[:, g, b, slab], a_scales[:, g, b, slab])
                    for slot in ((SLOT_P1,) if apart else (SLOT_P1, SLOT_4P1))
                    for g in range(PASSES)
                ]
                passes(a1_ps[:], ot, a1 if apart else a2 + a1)
                terms = terms_of[(n, m)][:].rearrange("o k r t -> o (k r t)")
                if apart:
                    nc.vector.scalar_tensor_tensor(
                        out=y[:, slab], in0=a1_ps[:], scalar=FIVE, in1=terms, op0=ALU.mult, op1=ALU.add,
                    )
                else:
                    nc.vector.tensor_tensor(out=y[:, slab], in0=a1_ps[:], in1=terms, op=ALU.add)
            if apart and hm == 0:
                a2_ps = psum_mix.tile([P, SLAB], F32, bufs=1)
                passes(a2_ps[:], ot, a2)
                a2_of[stage] = a2_ps

        def add_over_m(n):
            stage, b, ot, hm = where(n)
            if not a2_apart(stage):
                return
            half = y_of[stage][:, hm * HALF : (hm + 1) * HALF].rearrange("o (m x) -> o m x", x=SLAB)
            nc.vector.scalar_tensor_tensor(
                out=half,
                in0=a2_of[stage][:].unsqueeze(1).to_broadcast([P, 2, SLAB]),
                scalar=(AM_SCALE, 1.0)[b],
                in1=half, op0=ALU.mult, op1=ALU.add,
            )

        def relu(n):
            stage, b, ot, hm = where(n)
            half = y_of[stage][:, hm * HALF : (hm + 1) * HALF]
            nc.scalar.activation(
                out=half, in_=half, func=ACT.Relu,
                accum_out=sums[:, ot, 0, 2 * b + hm : 2 * b + hm + 1],
            )

        def square(n):
            stage, b, ot, hm = where(n)
            squares = work.tile([P, HALF], BF16, bufs=1)
            nc.scalar.activation(
                out=squares[:], in_=y_of[stage][:, hm * HALF : (hm + 1) * HALF], func=ACT.Square,
                scale=ROOT_COUNT,
                accum_out=sums[:, ot, 1, 2 * b + hm : 2 * b + hm + 1],
            )

        relus = []

        def relus_up_to(n, after_square):
            if n is None:
                return
            for unit in range(len(relus), min(n, N_UNITS) + 1):
                if unit >= 1:
                    square(unit - 1)
                    after_square(unit - 1)
                if unit < N_UNITS:
                    relu(unit)
                relus.append(unit)

        def nothing(unit):
            return

        def begun(step):
            n = step - LAG
            return n if 0 <= n < N_UNITS else None

        def unit_step(step, pool, a1_bufs, pooled_tag, pooled_bufs):
            ahead = begun(step + 1)
            if ahead is not None and ahead % 2 == 0:
                mix_pooled(ahead // 2, pool, pooled_tag, pooled_bufs)
            if ahead is not None:
                add_small_terms(ahead)
            if begun(step) is not None:
                mix(begun(step), pool, a1_bufs)
            if begun(step - 1) is not None:
                add_over_m(begun(step - 1))

        with ExitStack() as first:
            stage = first.enter_context(tc.tile_pool(name="stage", bufs=2))
            psum = first.enter_context(tc.psum_pool(name="psum_first", bufs=2))

            raw_of = {}
            grouped_of = {}
            flipped_of = {}
            means_of = {}
            m_sum_of = {}
            last_of = {}
            am_of = {}
            w_raw_of = {}
            w_grp_of = {}

            def place(sg):
                return sg // 8, (sg // 4) % 2, sg % 4

            def load(sg):
                b, g, part = place(sg)
                c, mm = divmod(sg, 2)
                if mm == 0:
                    raw = stage.tile([P, 2 * PACK * SLAB], BF16, bufs=3)
                    raw_of[c] = raw
                if b == 0:
                    nc.sync.dma_start(
                        out=raw_of[c][:].rearrange("p (s j w) -> p s j w", s=2, j=PACK)[:, mm],
                        in_=a_rows[
                            b, g * K_PASS : (g + 1) * K_PASS, part * SLAB : (part + 1) * SLAB
                        ].rearrange("(p j) w -> p j w", j=PACK),
                    )
                elif mm == 0:
                    for kk in range(CHUNK_K):
                        k = (part // 2) * CHUNK_K + kk
                        nc.sync.dma_start(
                            out=raw_of[c][:].rearrange("p (k q x) -> p k q x", k=CHUNK_K, x=POS_K)[:, kk],
                            in_=a_by_k[
                                b, k, g * K_PASS * M : (g + 1) * K_PASS * M, :
                            ].rearrange("(p q) x -> p q x", q=PACK * M),
                        )

            def regroup(sg):
                c, mm = divmod(sg, 2)
                b, g, part = place(sg)
                if mm == 0:
                    grouped = stage.tile([P, HALF, PACK], BF16, bufs=2, align_bytes=64)
                    grouped_of[c] = grouped
                if b == 0:
                    copy = nc.vector.tensor_copy if part < 2 else nc.scalar.copy
                    copy(
                        out=grouped_of[c][:, mm * SLAB : (mm + 1) * SLAB, :].rearrange(
                            "p (c i) j -> p c j i", i=4
                        ),
                        in_=raw_of[c][:]
                        .rearrange("p (s j w) -> p s j w", s=2, j=PACK)[:, mm]
                        .rearrange("p j (c i) -> p c j i", i=4),
                    )
                else:
                    for m in (2 * mm, 2 * mm + 1):
                        nc.vector.tensor_copy(
                            out=grouped_of[c][
                                :, m * CHUNK_K * POS_K : (m + 1) * CHUNK_K * POS_K, :
                            ].rearrange("p (k x) j -> p k x j", k=CHUNK_K),
                            in_=raw_of[c][:]
                            .rearrange("p (k j m x) -> p k j m x", k=CHUNK_K, j=PACK, m=M)[:, :, :, m]
                            .rearrange("p k j x -> p k x j"),
                        )

            def quantise(c):
                b, g, part = place(2 * c)
                flat = grouped_of[c][:].rearrange("p w j -> p (w j)")
                if b == 1:
                    width = CHUNK_K * POS_K
                    for m in range(M):
                        first = m * SLAB + (part // 2) * width
                        nc.vector.quantize_mx(
                            out=a_codes[:, g, b, first : first + width].bitcast(FP8X4),
                            scales=a_scales[:, g, b, first : first + width],
                            in_=flat[:, m * width * PACK : (m + 1) * width * PACK],
                        )
                    return
                cols = slice(part * SLAB, (part + 2) * SLAB)
                nc.vector.quantize_mx(
                    out=a_codes[:, g, b, cols].bitcast(FP8X4),
                    scales=a_scales[:, g, b, cols],
                    in_=flat,
                )
                slabs = [flat[:, i * SLAB * PACK : (i + 1) * SLAB * PACK] for i in range(2)]
                if part == 0:
                    m_sum = stage.tile([P, SLAB * PACK], F32, bufs=1)
                    m_sum_of[g] = m_sum
                    nc.vector.tensor_tensor(out=m_sum[:], in0=slabs[0], in1=slabs[1], op=ALU.add)
                else:
                    nc.vector.tensor_tensor(
                        out=m_sum_of[g][:], in0=m_sum_of[g][:], in1=slabs[0], op=ALU.add
                    )
                    last_of[g] = slabs[1]

            def am_tile(b, g):
                am_grp = stage.tile([P, SLAB * PACK], BF16, bufs=1, tag="am", align_bytes=64)
                am_of[(b, g)] = am_grp
                return am_grp

            def sum_over_m(g):
                am_grp = am_tile(0, g)
                nc.vector.tensor_tensor(
                    out=am_grp[:], in0=m_sum_of[g][:], in1=last_of[g], op=ALU.add
                )

            def turn(sg):
                b, g, part = place(sg)
                c, mm = divmod(sg, 2)
                raw_words = raw_of[c][:].bitcast(F32)
                flipped_of[sg] = []
                for tl in range(TILES):
                    flipped_ps = psum.tile([P, PACK, P], F32, tag="turned", bufs=3)
                    for j in range(PACK):
                        if b == 0:
                            first = ((mm * PACK + j) * TILES + tl) * P
                        else:
                            first = ((mm * STEP_K + tl) * PACK + j) * P
                        nc.tensor.transpose(
                            out=flipped_ps[:, j, :],
                            in_=raw_words[:, first : first + P],
                            identity=ident_f32[:],
                        )
                    flipped = stage.tile([P, PACK, P], F32, bufs=4)
                    on_vector = b == 1 and sg % 2 == 1 and tl == 1
                    (nc.vector.tensor_copy if on_vector else nc.scalar.copy)(
                        out=flipped[:], in_=flipped_ps[:]
                    )
                    flipped_of[sg].append(flipped)

            def halves_of(sg, tl):
                return (
                    flipped_of[sg][tl][:]
                    .rearrange("q j p -> q (j p)")
                    .bitcast(BF16)
                    .rearrange("q (j p e) -> q j p e", j=PACK, e=2)
                )

            def means(sg):
                b, g, part = place(sg)
                if part == 0:
                    atr_grp = stage.tile([P, 2 * M, K, NR, PACK], BF16, bufs=1, align_bytes=64)
                    means_of[(b, g)] = atr_grp
                    if b == 1:
                        am_tile(b, g)
                atr_grp = means_of[(b, g)]
                if b == 0:
                    mean_ps = psum.tile([P, PACK, 2, TILES, PER_TILE], F32, bufs=2, tag="means")
                    for tl in range(TILES):
                        halves = halves_of(sg, tl)
                        for j in range(PACK):
                            for e in range(2):
                                nc.tensor.matmul(
                                    out=mean_ps[:, j, :, tl, :],
                                    lhsT=halves[:, j, :, e],
                                    rhs=mean_w[:, e, :].rearrange("q (w n) -> q w n", w=2),
                                    start=(e == 0),
                                    stop=(e == 1),
                                )
                    nc.scalar.copy(
                        out=atr_grp[:, part : 2 * M : M].rearrange("p w k n j -> p w (k n) j"),
                        in_=mean_ps[:].rearrange("p j w k n -> p w (k n) j"),
                    )
                    return
                for tl in range(STEP_K):
                    k = part * STEP_K + tl
                    halves = halves_of(sg, tl)
                    sums_ps = psum.tile([P, PACK, P], F32, bufs=2, tag="means")
                    for j in range(PACK):
                        for e in range(2):
                            nc.tensor.matmul(
                                out=sums_ps[:, j, 0:PER_TILE],
                                lhsT=halves[:, j, :, e],
                                rhs=mean_w[:, e, 0:PER_TILE],
                                start=(e == 0),
                                stop=(e == 1),
                            )
                        for e in range(2):
                            nc.tensor.matmul(
                                out=sums_ps[:, j, PER_TILE + e : P : 2],
                                lhsT=halves[:, j, :, e],
                                rhs=rm_w[:],
                                start=True,
                                stop=True,
                            )
                    nc.scalar.copy(
                        out=atr_grp[:, :, k],
                        in_=sums_ps[:, :, 0:POS_K].rearrange("p j (q x) -> p q x j", x=NR),
                    )
                    nc.scalar.copy(
                        out=am_of[(b, g)][:, k * POS_K * PACK : (k + 1) * POS_K * PACK].rearrange(
                            "p (x j) -> p x j", j=PACK
                        ),
                        in_=sums_ps[:, :, POS_K:P].rearrange("p j x -> p x j"),
                    )

            def finish(b, g):
                nc.vector.quantize_mx(
                    out=atr_codes[:, g, b, :, :].rearrange("p w n -> p (w n)").bitcast(FP8X4),
                    scales=atr_scales[:, g, b, :, :].rearrange("p w n -> p (w n)"),
                    in_=means_of[(b, g)][:].rearrange("p w k n j -> p (w k n j)"),
                )
                am_grp = am_of[(b, g)]
                nc.vector.quantize_mx(
                    out=am_codes[:, g, b * SLAB : (b + 1) * SLAB].bitcast(FP8X4),
                    scales=am_scales[:, g, b * SLAB : (b + 1) * SLAB],
                    in_=am_grp[:],
                )

            def small_inputs():
                a5_sb = stage.tile([P, O_TILES, B, SMALL], BF16, bufs=1, tag="am", align_bytes=64)
                nc.sync.dma_start(
                    out=gb_rows[0:O_TILES, :], in_=gamma.rearrange("(t o) -> t o", o=P)
                )
                nc.sync.dma_start(
                    out=gb_rows[O_TILES : 2 * O_TILES, :], in_=beta.rearrange("(t o) -> t o", o=P)
                )
                for b in range(B):
                    nc.sync.dma_start(
                        out=a5_sb[:, :, b, :], in_=a5_rows[b].rearrange("(t o) x -> o t x", o=P)
                    )
                nc.gpsimd.tensor_scalar(
                    out=a5_scaled[:].rearrange("o t b x -> o (t b x)"),
                    in0=a5_sb[:].rearrange("o t b x -> o (t b x)"),
                    scalar1=2.0 * FIVE, scalar2=0.0, op0=ALU.mult, op1=ALU.add,
                )

            def turn_gamma_beta():
                gb_ps = psum.tile([P, P], BF16, tag="turned", bufs=3)
                nc.tensor.transpose(out=gb_ps[:], in_=gb_rows[:], identity=ident_bf[:])
                nc.vector.tensor_copy(out=gamma_beta[:], in_=gb_ps[:, 0 : 2 * O_TILES])
                nc.vector.tensor_scalar_mul(
                    out=gamma_pair[:, :, 0], in0=gamma_beta[:, 0:O_TILES], scalar1=1.0 * COUNT
                )
                nc.vector.tensor_scalar_mul(
                    out=gamma_pair[:, :, 1], in0=gamma_beta[:, 0:O_TILES], scalar1=-1.0
                )

            def has_4p1(ot):
                return not a2_apart(O_TILES + ot)

            def load_weights(ot):
                w_raw = stage.tile([P, N_W * C], BF16, bufs=2)
                for which in range(N_W):
                    nc.sync.dma_start(
                        out=w_raw[:, which * C : (which + 1) * C],
                        in_=weights[which][ot * P : (ot + 1) * P, :],
                    )
                w_raw_of[ot] = w_raw

            def turn_weights(ot, pair):
                if pair == 0:
                    w_grp = stage.tile([P, N_SLOTS * P * PACK], BF16, bufs=1, align_bytes=64)
                    w_grp_of[ot] = w_grp
                w_words = w_raw_of[ot][:].bitcast(F32).rearrange(
                    "o (w g p u) -> o w g p u", w=N_W, g=PASSES, u=2
                )
                target_words = w_grp_of[ot][:].bitcast(F32).rearrange("p (s o u) -> p s o u", o=P, u=2)
                for half in range(2):
                    which = 2 * pair + half
                    first_slot = which * PASSES
                    wt_ps = psum.tile([P, PASSES, 2, P], F32, tag="turned", bufs=3)
                    for g in range(PASSES):
                        for u in range(2):
                            nc.tensor.transpose(
                                out=wt_ps[:, g, u, :],
                                in_=w_words[:, which, g, :, u],
                                identity=ident_f32[:],
                            )
                    nc.scalar.copy(
                        out=target_words[:, first_slot : first_slot + PASSES, :, :],
                        in_=wt_ps[:].rearrange("p g u o -> p g o u"),
                    )
                if pair == 0 and has_4p1(ot):
                    cols = PASSES * P * PACK
                    nc.vector.tensor_scalar_mul(
                        out=w_grp_of[ot][:, SLOT_4P1 * P * PACK : SLOT_4P1 * P * PACK + cols],
                        in0=w_grp_of[ot][:, SLOT_P1 * P * PACK : SLOT_P1 * P * PACK + cols],
                        scalar1=4.0,
                    )

            def quantise_weights(ot):
                for first, last in [(0, SLOT_4P1)] + [(SLOT_4P1, N_SLOTS)] * has_4p1(ot):
                    nc.vector.quantize_mx(
                        out=w_codes[:, ot, first:last, :].rearrange("p s o -> p (s o)").bitcast(FP8X4),
                        scales=w_scales[:, ot, first:last, :].rearrange("p s o -> p (s o)"),
                        in_=w_grp_of[ot][:, first * P * PACK : last * P * PACK],
                    )

            for ot in range(O_TILES):
                y_of[ot] = y_first[:, ot, :]
            for sg in range(4):
                load(sg)
            regroup(0)
            regroup(1)
            load_weights(0)
            for sg in range(STEPS):
                c, mm = divmod(sg, 2)
                if sg + 4 < STEPS:
                    load(sg + 4)
                turn(sg)
                if sg + 2 < STEPS:
                    regroup(sg + 2)
                if mm == 0:
                    quantise(c)
                if sg % 4 == 3 and sg < STEPS // 2:
                    sum_over_m(sg // 4)
                if sg >= 1:
                    means(sg - 1)
                if sg >= 4 and sg % 4 == 0:
                    finish((sg - 4) // 8, ((sg - 4) // 4) % 2)
                if sg == 1:
                    small_inputs()
                if sg == 4:
                    turn_gamma_beta()
                if sg >= STEPS // 2:
                    unit_step(sg - STEPS // 2, psum, 2, "means", 2)
                    relus_up_to(begun(sg - STEPS // 2 - 2), nothing)
                if sg >= 2:
                    ot, part = divmod(sg - 2, 3)
                    if ot < O_TILES and part < 2:
                        turn_weights(ot, part)
                    if part == 0 and ot + 1 < O_TILES:
                        load_weights(ot + 1)
                    if ot < O_TILES and part == 1:
                        quantise_weights(ot)
            means(STEPS - 1)
            finish(1, 1)
            unit_step(N_UNITS // 2, psum, 2, "means", 2)
            relus_up_to(begun(N_UNITS // 2 - 2), nothing)

        with ExitStack() as second:
            late = second.enter_context(tc.tile_pool(name="late", bufs=4))
            psum = second.enter_context(tc.psum_pool(name="psum_late", bufs=6))
            affine_of = {}

            def statistics(ot):
                total = work.tile([P, 2], F32)
                nc.vector.tensor_reduce(
                    out=total[:], in_=sums[:, ot, :, :], axis=AXIS_X, op=ALU.add
                )
                minus_spread = work.tile([P, 1], F32)
                nc.vector.scalar_tensor_tensor(
                    out=minus_spread[:], in0=total[:, 0:1], scalar=total[:, 0:1],
                    in1=total[:, 1:2], op0=ALU.mult, op1=ALU.subtract,
                )
                spread = work.tile([P, 1], F32)
                nc.vector.tensor_scalar(
                    out=spread[:], in0=minus_spread[:], scalar1=-1.0,
                    scalar2=BN_EPS * FIVE * FIVE * COUNT * COUNT, op0=ALU.mult, op1=ALU.max,
                )
                w = work.tile([P, 1], F32)
                nc.scalar.activation(out=w[:], in_=spread[:], func=ACT.Abs_reciprocal_sqrt)
                minus_mean = work.tile([P, 1], F32)
                nc.vector.tensor_scalar_mul(
                    out=minus_mean[:], in0=total[:, 0:1], scalar1=gamma_pair[:, ot, 1:2]
                )
                gain = work.tile([P, 1], F32)
                nc.vector.tensor_scalar_mul(out=gain[:], in0=w[:], scalar1=gamma_pair[:, ot, 0:1])
                shift = work.tile([P, 1], F32)
                nc.vector.tensor_scalar(
                    out=shift[:], in0=w[:], scalar1=minus_mean[:],
                    scalar2=gamma_beta[:, O_TILES + ot : O_TILES + ot + 1],
                    op0=ALU.mult, op1=ALU.add,
                )
                affine_of[ot] = (gain[:], shift[:])

            def normalise_and_store(ot, b):
                gain, shift = affine_of[ot]
                y = y_of[b * O_TILES + ot]
                on_scalar = b == 1 and ot == O_TILES - 1
                for hm in range(2):
                    half = slice(hm * HALF, (hm + 1) * HALF)
                    if on_scalar:
                        nc.scalar.activation(
                            out=y[:, half], in_=y[:, half], func=ACT.Identity,
                            scale=gain, bias=shift,
                        )
                    else:
                        nc.vector.tensor_scalar(
                            out=y[:, half], in0=y[:, half],
                            scalar1=gain, scalar2=shift, op0=ALU.mult, op1=ALU.add,
                        )
                    nc.sync.dma_start(out=out_rows[b, ot * P : (ot + 1) * P, half], in_=y[:, half])

            def after_square(unit):
                stage, b, ot, hm = where(unit)
                if b == 1 and hm == 0 and ot >= 1:
                    normalise_and_store(ot - 1, 1)
                if b == 1 and hm == 1:
                    statistics(ot)
                    normalise_and_store(ot, 0)

            for step in range(N_UNITS // 2 + 1, N_UNITS + LAG + 2):
                n = begun(step)
                if n is not None and n % 2 == 0:
                    y_second = late.tile([P, POS], F32)
                    y_of[n // 2] = y_second[:]
                unit_step(step, psum, 7, "a1_ps", 7)
                relus_up_to(step - LAG - 1, after_square)
            normalise_and_store(O_TILES - 1, 1)
